import numpy as np
import ml_dtypes


def mxq(x, axis, fmt="e4m3"):
    dtype, down = {"e4m3": (ml_dtypes.float8_e4m3fn, 7), "e5m2": (ml_dtypes.float8_e5m2, 14)}[fmt]
    v = np.moveaxis(np.asarray(x, np.float32).astype(ml_dtypes.bfloat16).astype(np.float64), axis, -1)
    blocks = v.reshape(v.shape[:-1] + (-1, 32))
    amax = np.abs(blocks).max(-1, keepdims=True)
    byte = np.maximum(np.where(amax > 0, np.frexp(amax)[1] - 1 + 127, 0) - down, 1)
    scale = np.exp2(byte - 127.0)
    codes = (blocks / scale).astype(np.float32).astype(dtype).astype(np.float64)
    return np.moveaxis((codes * scale).reshape(v.shape), -1, axis)


WIDE = False


def mx_kscale(k):
    if not WIDE:
        return np.ones(k)
    levels = np.array([10, -10, 5, -5, 0])
    a = np.random.permutation(np.resize(levels, k // 512 * 4)).reshape(k // 512, 4)
    idx = np.arange(k)
    return np.exp2(a[idx // 512, idx % 128 // 32])


BF16 = ml_dtypes.bfloat16


def bf(x):
    return np.asarray(x, np.float32).astype(BF16)


def f64(x):
    return np.asarray(x).astype(np.float64)


E2M1 = np.array([0.0, 0.5, 1.0, 1.5, 2.0, 3.0, 4.0, 6.0, -0.0, -0.5, -1.0, -1.5, -2.0, -3.0, -4.0, -6.0])


def pack_weight(w, fmt):
    k, n = w.shape
    w = f64(bf(w)).reshape(k // 32, 32, n)
    amax = np.abs(w).max(1)
    if fmt == "e4m3":
        byte = np.frexp(amax)[1] - 1 + 127 - 7
    else:
        mant, ex = np.frexp(amax / 6.0)
        byte = np.where(mant > 0.5, ex, ex - 1) + 127
    byte = np.clip(np.where(amax > 0, byte, 1), 1, 254)
    scaled = (w * np.exp2(127.0 - byte)[:, None, :]).reshape(k, n).astype(np.float32)
    by_word = np.ascontiguousarray(scaled.reshape(k // 512, 128, 4, n).transpose(0, 1, 3, 2))
    if fmt == "e4m3":
        words = by_word.astype(ml_dtypes.float8_e4m3fn).view(np.uint8)
    else:
        c = by_word.astype(ml_dtypes.float4_e2m1fn).view(np.uint8) & 0xF
        words = c[..., 0::2] | (c[..., 1::2] << 4)
    return np.ascontiguousarray(words), np.ascontiguousarray(byte.astype(np.uint8).reshape(k // 512, 16, n))


def unpack_weight(words, scales, fmt):
    g, p, n, _ = words.shape
    if fmt == "e4m3":
        vals = np.ascontiguousarray(words).view(ml_dtypes.float8_e4m3fn).astype(np.float64)
    else:
        nib = np.empty((g, p, n, 4), np.uint8)
        nib[..., 0::2] = words & 0xF
        nib[..., 1::2] = words >> 4
        vals = E2M1[nib]
    vals = vals * np.repeat(np.exp2(scales.astype(np.float64) - 127.0), 8, axis=1)[..., None]
    return vals.transpose(0, 1, 3, 2).reshape(g * 512, n)

def pack4(w):
    words, scales = pack_weight(w, "e2m1")
    return words.reshape(words.shape[0], 128, -1), scales


def unpack4(words, scales):
    return unpack_weight(words.reshape(words.shape[0], 128, -1, 2), scales, "e2m1")


B, CL, CH, CK, CV, CO, H, W = 2, 1024, 2048, 256, 512, 1024, 24, 24
N = H * W
PSP = (1, 3, 6, 8)
EPS = 1e-5


def psp(x):
    b, c, h, w = x.shape
    return np.concatenate(
        [x.reshape(b, c, s, h // s, s, w // s).mean(axis=(3, 5)).reshape(b, c, s * s) for s in PSP], axis=2)


def setup_inputs():
    s = mx_kscale(CL)
    low_feats = bf(np.random.standard_normal((B, CL, H, W)) * s[None, :, None, None])
    wk = np.random.standard_normal((CK, CL)) * 2.5 / np.sqrt(CL) / s[None, :]
    wk_words, wk_scales = pack4(np.ascontiguousarray(wk.T))
    bk = bf(np.random.standard_normal(CK) * 0.3)
    gk = bf(np.random.uniform(0.5, 1.5, CK))
    bek = bf(np.random.standard_normal(CK) * 0.3)
    mk = bf(np.random.standard_normal(CK) * 0.3)
    vk = bf(np.random.uniform(0.5, 1.5, CK))
    wv = np.random.standard_normal((CV, CL)) * 3.0 / np.sqrt(CL) / s[None, :]
    wv_words, wv_scales = pack4(np.ascontiguousarray(wv.T))
    bv = bf(np.random.standard_normal(CV) * 0.3)
    return {"low_feats": low_feats,
            "wk_words": wk_words,
            "wk_scales": wk_scales,
            "bk": bk,
            "gk": gk,
            "bek": bek,
            "mk": mk,
            "vk": vk,
            "wv_words": wv_words,
            "wv_scales": wv_scales,
            "bv": bv}


def reference(low_feats, wk_words, wk_scales, bk, gk, bek, mk, vk, wv_words, wv_scales, bv):
    xq = mxq(f64(low_feats).reshape(B, CL, N), 1, "e4m3")
    v = (unpack4(wv_words, wv_scales).T @ xq) + f64(bv)[None, :, None]
    value = psp(v.reshape(B, CV, H, W)).transpose(0, 2, 1)
    u = (unpack4(wk_words, wk_scales).T @ xq) + f64(bk)[None, :, None]
    sc = f64(gk) / np.sqrt(f64(vk) + EPS)
    r = np.maximum((u - f64(mk)[None, :, None]) * sc[None, :, None] + f64(bek)[None, :, None], 0.0)
    key = psp(r.reshape(B, CK, H, W))
    return value, key

@@ -1,0 +1,318 @@
+from contextlib import ExitStack
+
+import concourse.mybir as mybir
+from concourse.masks import make_identity
+
+F32 = mybir.dt.float32
+BF16 = mybir.dt.bfloat16
+I32 = mybir.dt.int32
+U32 = mybir.dt.uint32
+U8 = mybir.dt.uint8
+FP8X4 = mybir.dt.float8_e4m3fn_x4
+FP4X4 = mybir.dt.float4_e2m1fn_x4
+ADD = mybir.AluOpType.add
+MULT = mybir.AluOpType.mult
+ACT = mybir.ActivationFunctionType
+AXIS = mybir.AxisListType
+
+P = 128
+PACK = 4
+K_PASS = P * PACK
+B, CL, CK, CV, SIDE = 2, 1024, 256, 512, 24
+PIX = SIDE * SIDE
+PASSES = CL // K_PASS
+KEY_TILES = CK // P
+EPS = 1e-5
+FLOPS = 2 * B * PIX * CL * (CK + CV)
+
+LAYER_BASE = (0, 1, 2)
+LAYER_STEP = (4, 4, 1)
+LAYERS = 9
+SLOTS = 128
+COARSE = 46
+FINE = 64
+ROWS = 64
+
+
+def layer_class(layer):
+    return 2 * (layer // 3 == 2) + (layer % 3 == 2)
+
+
+def three_to_four(nc, out_views, outer, inner, total):
+    nc.vector.tensor_tensor(out=out_views[0], in0=total(0, 0), in1=inner(1, 0), op=ADD)
+    nc.vector.tensor_tensor(out=out_views[2], in0=total(1, 1), in1=inner(0, 1), op=ADD)
+    nc.vector.tensor_tensor(out=out_views[1], in0=outer(1, 0), in1=outer(0, 1), op=ADD)
+
+
+def along_w(ap):
+    view = ap.rearrange("c t (ph pw m e x) -> c t ph pw m e x", ph=2, pw=2, m=8, e=2, x=2)
+    return lambda p, x: view[:, :, :, p, :, :, x]
+
+
+def along_h(ap):
+    view = ap.rearrange("c t ph (b e x) k -> c t ph b e x k", b=B, e=2, x=2)
+    return lambda p, x: view[:, :, p, :, :, x, :]
+
+
+def pool_refined(nc, work, label, tiles, oo, oi, io, ii, coarse):
+    tw = work.tile([P, 2, tiles, SLOTS], F32, name="%s_tw" % label)
+    cw = work.tile([P, 2, tiles, 2, 8, 6], F32, name="%s_cw" % label)
+    th = work.tile([P, tiles, 2, 8, 6], F32, name="%s_th" % label)
+    s6 = work.tile([P, tiles, B, 36], F32, name="%s_s6" % label)
+    s3 = work.tile([P, tiles, B, 9], F32, name="%s_s3" % label)
+    s1 = work.tile([P, tiles, B, 1], F32, name="%s_s1" % label)
+    for kh, (outer, inner) in enumerate(((oo, oi), (io, ii))):
+        nc.vector.tensor_tensor(out=tw[:, kh], in0=outer, in1=inner, op=ADD)
+        cells = cw[:, kh].rearrange("c t ph m (e k) -> c t ph m e k", k=3)
+        three_to_four(
+            nc,
+            [cells[:, :, :, :, :, k] for k in range(3)],
+            along_w(outer),
+            along_w(inner),
+            along_w(tw[:, kh]),
+        )
+    nc.vector.tensor_tensor(out=th[:], in0=cw[:, 0], in1=cw[:, 1], op=ADD)
+    cells = s6[:].rearrange("c t b (e k w) -> c t b e k w", e=2, k=3)
+    three_to_four(
+        nc,
+        [cells[:, :, :, :, k, :] for k in range(3)],
+        along_h(cw[:, 0]),
+        along_h(cw[:, 1]),
+        along_h(th[:]),
+    )
+    nc.vector.tensor_reduce(
+        out=s3[:].rearrange("c t b (h w) -> c (t b h) w", h=3),
+        in_=s6[:].rearrange("c t b (h i w j) -> c (t b h) w i j", h=3, i=2, w=3, j=2),
+        axis=AXIS.XY,
+        op=ADD,
+    )
+    nc.vector.tensor_reduce(
+        out=s1[:].rearrange("c t b o -> c (t b o)"),
+        in_=s3[:].rearrange("c t b n -> c (t b) n"),
+        axis=AXIS.X,
+        op=ADD,
+    )
+    nc.vector.tensor_scalar_mul(out=coarse[:, :, :, 0:1], in0=s1[:], scalar1=1.0 / 576.0)
+    nc.vector.tensor_scalar_mul(out=coarse[:, :, :, 1:10], in0=s3[:], scalar1=1.0 / 64.0)
+    nc.vector.tensor_scalar_mul(out=coarse[:, :, :, 10:46], in0=s6[:], scalar1=1.0 / 16.0)
+    return tw
+
+
+def tile_afnb_pa_kernel(
+    tc, low_feats, wk_words, wk_scales, bk, gk, bek, mk, vk, wv_words, wv_scales, bv, out_0, out_1
+):
+    nc = tc.nc
+    with ExitStack() as ctx:
+        keep = ctx.enter_context(tc.tile_pool(name="keep", bufs=1))
+        work = ctx.enter_context(tc.tile_pool(name="work", bufs=1))
+        stage = ctx.enter_context(tc.tile_pool(name="stage", bufs=4))
+        psum = ctx.enter_context(tc.psum_pool(name="psum", bufs=1))
+        ctx.enter_context(tc.manual_schedule())
+
+        wk_planes = keep.tile([P, PASSES, CK], U8, align_bytes=64)
+        wv_planes = keep.tile([P, PASSES, CV], U8, align_bytes=64)
+        wk_codes = keep.tile([P, PASSES, 2 * CK], U8, align_bytes=64)
+        wv_codes = keep.tile([P, PASSES, 2 * CV], U8, align_bytes=64)
+        raw = [keep.tile([P, PACK, B, PIX], BF16, name="raw%d" % g) for g in range(PASSES)]
+        nc.vector.memset(wv_planes[:].bitcast(I32), 0)
+        nc.vector.memset(wk_planes[:].bitcast(I32), 0)
+
+        def load_planes(planes, scales):
+            for quad in range(4):
+                nc.sync.dma_start(
+                    out=planes[32 * quad : 32 * quad + 4].bitcast(I32),
+                    in_=scales.bitcast(I32)[:, 4 * quad : 4 * quad + 4, :].rearrange("g r n -> r g n"),
+                )
+
+        def load_x(g):
+            for b in range(B):
+                nc.scalar.dma_start(
+                    out=raw[g][:, :, b, :],
+                    in_=low_feats[b, g * K_PASS : (g + 1) * K_PASS].rearrange("(p j) h w -> p j (h w)", j=PACK),
+                )
+
+        load_planes(wv_planes, wv_scales)
+        nc.sync.dma_start(out=wv_codes[:].bitcast(I32), in_=wv_words.bitcast(I32).rearrange("g p n -> p g n"))
+        load_x(0)
+        nc.sync.dma_start(out=wk_codes[:].bitcast(I32), in_=wk_words.bitcast(I32).rearrange("g p n -> p g n"))
+        load_planes(wk_planes, wk_scales)
+        load_x(1)
+
+        ident = keep.tile([P, P], BF16)
+        make_identity(nc, ident[:])
+        vecs = [keep.tile([P, KEY_TILES], BF16, name="vec%d" % i) for i in range(5)]
+        with nc.allow_non_contiguous_dma(reason="five vectors of 256 values, one value a partition"):
+            for tile_, vec in zip(vecs, (bk, gk, bek, mk, vk)):
+                nc.gpsimd.dma_start(out=tile_[:], in_=vec.rearrange("(t c) -> c t", c=P))
+        bv_all = keep.tile([P, CV], BF16)
+        nc.gpsimd.dma_start(out=bv_all[:], in_=bv.partition_broadcast(P))
+        bk_c, gk_c, bek_c, mk_c, vk_c = [tile_[:] for tile_ in vecs]
+        minus_half = keep.tile([P, KEY_TILES], F32)
+        var_eps = keep.tile([P, KEY_TILES], F32)
+        rstd = keep.tile([P, KEY_TILES], F32)
+        bn_scale = keep.tile([P, KEY_TILES], F32)
+        centred = keep.tile([P, KEY_TILES], F32)
+        scaled = keep.tile([P, KEY_TILES], F32)
+        bn_shift = keep.tile([P, KEY_TILES], F32)
+        nc.gpsimd.memset(minus_half[:], -0.5)
+        nc.gpsimd.tensor_scalar(out=var_eps[:], in0=vk_c, scalar1=1.0, scalar2=EPS, op0=MULT, op1=ADD)
+        nc.gpsimd.tensor_tensor(out=rstd[:], in0=var_eps[:], in1=minus_half[:], op=mybir.AluOpType.pow)
+        nc.gpsimd.tensor_tensor(out=bn_scale[:], in0=gk_c, in1=rstd[:], op=MULT)
+        nc.gpsimd.tensor_tensor(out=centred[:], in0=bk_c, in1=mk_c, op=mybir.AluOpType.subtract)
+        nc.gpsimd.tensor_tensor(out=scaled[:], in0=centred[:], in1=bn_scale[:], op=MULT)
+        nc.gpsimd.tensor_tensor(out=bn_shift[:], in0=scaled[:], in1=bek_c, op=ADD)
+
+        units = keep.tile([P, 7, SLOTS], F32)
+        pool_mat = keep.tile([P, 4, B, ROWS], F32)
+        nc.vector.memset(units[:], 0.0)
+        nc.vector.memset(pool_mat[:], 0.0)
+        nc.vector.tensor_copy(out=units[:, 3, :], in_=ident[:])
+        pool_refined(
+            nc, work, "mat", 4, units[:, 3:7], units[:, 2:6], units[:, 1:5], units[:, 0:4], pool_mat[:, :, :, 0:COARSE]
+        )
+
+        x_codes = keep.tile([P, PASSES, LAYERS, SLOTS], U32, align_bytes=64)
+        x_planes = keep.tile([P, PASSES, LAYERS, SLOTS], U8, align_bytes=64)
+        v_class = [psum.tile([P, CV], F32, name="v_class%d" % c) for c in range(4)]
+        key_tags = (("key_a", "key_c"), ("key_b", "key_d"))
+        u_wide = {}
+        relu = keep.tile([P, LAYERS, KEY_TILES, SLOTS], F32)
+        g_sb = [keep.tile([P, CV], F32, name="g_sb%d" % c) for c in range(4)]
+        members = [[layer for layer in range(LAYERS) if layer_class(layer) == c] for c in range(4)]
+        steps = [(g, layer) for g in range(PASSES) for layer in range(LAYERS)]
+        grouped = {}
+
+        def regroup(g, layer):
+            lh, lw = divmod(layer, 3)
+            pixels = raw[g][:].rearrange("p j b (eh sh ew sw) -> p j b eh sh ew sw", eh=4, sh=6, ew=4, sw=6)
+            tile_ = stage.tile([P, SLOTS, PACK], BF16, align_bytes=64, name="grouped")
+            grouped[(g, layer)] = tile_
+            quarters = tile_[:].rearrange("p (ph pw m ew) j -> p ph pw m ew j", ph=2, pw=2, m=8)
+            cols = slice(LAYER_BASE[lw], LAYER_BASE[lw] + LAYER_STEP[lw] + 1, LAYER_STEP[lw])
+            rows = [
+                pixels[:, :, :, :, LAYER_BASE[lh] + LAYER_STEP[lh] * ph, :, cols].rearrange(
+                    "p j b eh ew pw -> p pw (b eh) ew j"
+                )
+                for ph in range(2)
+            ]
+            nc.vector.tensor_copy(out=quarters[:, 0], in_=rows[0])
+            for pw in range(2):
+                nc.scalar.copy(out=quarters[:, 1, pw], in_=rows[1][:, pw])
+
+        def key_pass(out, t, g, codes, planes):
+            nc.tensor.matmul_mx(
+                out=out,
+                lhsT=wk_codes[:, g, 2 * P * t : 2 * P * (t + 1)].bitcast(FP4X4),
+                lhsT_scale=wk_planes[:, g, P * t : P * (t + 1)],
+                rhs=codes.bitcast(FP8X4),
+                rhs_scale=planes,
+                start=(g == 0),
+                stop=(g == PASSES - 1),
+            )
+
+        def norm_relu(out, in_, t):
+            nc.scalar.activation(
+                out=out, in_=in_, func=ACT.Relu, bias=bn_shift[:, t : t + 1], scale=bn_scale[:, t : t + 1]
+            )
+
+        def relu_wide(q):
+            for t in range(KEY_TILES):
+                norm_relu(
+                    relu[:, 4 * q : 4 * q + 4, t, :], u_wide[(t, q)][:].rearrange("c (l s) -> c l s", s=SLOTS), t
+                )
+
+        regroup(*steps[0])
+        for i, (g, layer) in enumerate(steps):
+            if i + 1 < len(steps):
+                regroup(*steps[i + 1])
+            nc.vector.quantize_mx(
+                out=x_codes[:, g, layer, :].bitcast(FP8X4),
+                scales=x_planes[:, g, layer, :],
+                in_=grouped[(g, layer)][:].rearrange("p s j -> p (s j)"),
+            )
+            c = layer_class(layer)
+            nc.tensor.matmul_mx(
+                out=v_class[c][:],
+                lhsT=x_codes[:, g, layer, :].bitcast(FP8X4),
+                lhsT_scale=x_planes[:, g, layer, :],
+                rhs=wv_codes[:, g, :].bitcast(FP4X4),
+                rhs_scale=wv_planes[:, g, :],
+                start=(g == 0 and layer == members[c][0]),
+                stop=(g == PASSES - 1 and layer == members[c][-1]),
+            )
+            if layer % 4 == 3:
+                q = layer // 4
+                for t in range(KEY_TILES):
+                    if g == 0:
+                        u_wide[(t, q)] = psum.tile([P, 4 * SLOTS], F32, name="u_wide%d%d" % (t, q), tag=key_tags[t][q])
+                    key_pass(
+                        u_wide[(t, q)][:],
+                        t,
+                        g,
+                        x_codes[:, g, 4 * q : 4 * q + 4, :].rearrange("p l s -> p (l s)"),
+                        x_planes[:, g, 4 * q : 4 * q + 4, :].rearrange("p l s -> p (l s)"),
+                    )
+            if g == PASSES - 1 and layer == 6:
+                relu_wide(0)
+
+        relu_wide(1)
+        u_last = psum.tile([P, KEY_TILES, SLOTS], F32, tag="key_a")
+        for t in range(KEY_TILES):
+            for g in range(PASSES):
+                key_pass(u_last[:, t, :], t, g, x_codes[:, g, LAYERS - 1, :], x_planes[:, g, LAYERS - 1, :])
+            norm_relu(relu[:, LAYERS - 1, t, :], u_last[:, t, :], t)
+
+        coarse_ps = psum.tile([P, CV], F32, tag="key_b")
+        for c in range(4):
+            nc.scalar.copy(out=g_sb[c][:], in_=v_class[c][:])
+            nc.tensor.matmul(
+                out=coarse_ps[:],
+                lhsT=pool_mat[:, c].rearrange("p b l -> p (b l)"),
+                rhs=g_sb[c][:],
+                start=(c == 0),
+                stop=(c == 3),
+            )
+
+        h01 = keep.tile([P, 3, KEY_TILES, SLOTS], F32)
+        k_oo = keep.tile([P, KEY_TILES, SLOTS], F32)
+        k_io = keep.tile([P, KEY_TILES, SLOTS], F32)
+        nc.vector.tensor_tensor(out=h01[:], in0=relu[:, 0:3], in1=relu[:, 3:6], op=ADD)
+        nc.vector.tensor_tensor(out=k_oo[:], in0=h01[:, 0], in1=h01[:, 1], op=ADD)
+        nc.vector.tensor_tensor(out=k_io[:], in0=relu[:, 6], in1=relu[:, 7], op=ADD)
+        key_sb = keep.tile([P, KEY_TILES, B, COARSE + FINE], F32)
+        tw = pool_refined(
+            nc, work, "key", KEY_TILES, k_oo[:], h01[:, 2], k_io[:], relu[:, 8], key_sb[:, :, :, 0:COARSE]
+        )
+        k_fine = keep.tile([P, KEY_TILES, SLOTS], F32)
+        nc.vector.tensor_tensor(out=k_fine[:], in0=tw[:, 0], in1=tw[:, 1], op=ADD)
+        by_slot = k_fine[:].rearrange("c t (ph pw b eh ew) -> c t ph b eh ew pw", ph=2, pw=2, b=B, eh=4)
+        by_cell = key_sb[:, :, :, COARSE : COARSE + FINE].rearrange(
+            "c t b (eh ph ew pw) -> c t ph b eh ew pw", eh=4, ph=2, ew=4
+        )
+        for ph in range(2):
+            nc.vector.tensor_scalar_mul(out=by_cell[:, :, ph], in0=by_slot[:, :, ph], scalar1=1.0 / 9.0)
+        for t in range(KEY_TILES):
+            nc.scalar.dma_start(out=out_1[:, P * t : P * (t + 1), :].rearrange("b c l -> c b l"), in_=key_sb[:, t])
+
+        sum01 = keep.tile([P, CV], F32)
+        sum23 = keep.tile([P, CV], F32)
+        sum_all = keep.tile([P, CV], F32)
+        v_fine = keep.tile([P, CV], F32)
+        nc.gpsimd.tensor_tensor(out=sum01[:], in0=g_sb[0][:], in1=g_sb[1][:], op=ADD)
+        nc.gpsimd.tensor_tensor(out=sum23[:], in0=g_sb[2][:], in1=g_sb[3][:], op=ADD)
+        nc.gpsimd.tensor_tensor(out=sum_all[:], in0=sum01[:], in1=sum23[:], op=ADD)
+        nc.vector.scalar_tensor_tensor(
+            out=v_fine[:], in0=sum_all[:], scalar=1.0 / 9.0, in1=bv_all[:], op0=MULT, op1=ADD
+        )
+        for b in range(B):
+            cells = out_0[b, COARSE : COARSE + FINE, :].rearrange(
+                "(eh ph ew pw) c -> ph pw eh ew c", eh=4, ph=2, ew=4, pw=2
+            )
+            for ph in range(2):
+                for pw in range(2):
+                    first = 64 * ph + 32 * pw + 16 * b
+                    nc.sync.dma_start(out=cells[ph, pw], in_=v_fine[first : first + 16, :])
+        v_coarse = keep.tile([P, CV], F32)
+        nc.vector.tensor_tensor(out=v_coarse[:], in0=coarse_ps[:], in1=bv_all[:], op=ADD)
+        for b in range(B):
+            nc.sync.dma_start(out=out_0[b, 0:COARSE, :], in_=v_coarse[ROWS * b : ROWS * b + COARSE, :])

@@ -143,9 +143,9 @@ def tile_afnb_pa_kernel(
         vecs = [keep.tile([P, KEY_TILES], BF16, name="vec%d" % i) for i in range(5)]
         with nc.allow_non_contiguous_dma(reason="five vectors of 256 values, one value a partition"):
             for tile_, vec in zip(vecs, (bk, gk, bek, mk, vk)):
-                nc.gpsimd.dma_start(out=tile_[:], in_=vec.rearrange("(t c) -> c t", c=P))
+                nc.sync.dma_start(out=tile_[:], in_=vec.rearrange("(t c) -> c t", c=P))
         bv_all = keep.tile([P, CV], BF16)
-        nc.gpsimd.dma_start(out=bv_all[:], in_=bv.partition_broadcast(P))
+        nc.sync.dma_start(out=bv_all[:], in_=bv.partition_broadcast(P))
         bk_c, gk_c, bek_c, mk_c, vk_c = [tile_[:] for tile_ in vecs]
         minus_half = keep.tile([P, KEY_TILES], F32)
         var_eps = keep.tile([P, KEY_TILES], F32)

@@ -38,12 +38,6 @@ def layer_class(layer):
     return 2 * (layer // 3 == 2) + (layer % 3 == 2)
 
 
-def three_to_four(nc, out_views, outer, inner, total):
-    nc.vector.tensor_tensor(out=out_views[0], in0=total(0, 0), in1=inner(1, 0), op=ADD)
-    nc.vector.tensor_tensor(out=out_views[2], in0=total(1, 1), in1=inner(0, 1), op=ADD)
-    nc.vector.tensor_tensor(out=out_views[1], in0=outer(1, 0), in1=outer(0, 1), op=ADD)
-
-
 def along_w(ap):
     view = ap.rearrange("c t (ph pw m e x) -> c t ph pw m e x", ph=2, pw=2, m=8, e=2, x=2)
     return lambda p, x: view[:, :, :, p, :, :, x]
@@ -54,32 +48,42 @@ def along_h(ap):
     return lambda p, x: view[:, :, p, :, :, x, :]
 
 
-def pool_refined(nc, work, label, tiles, oo, oi, io, ii, coarse):
+def add(nc, out, in0, in1):
+    nc.vector.tensor_tensor(out=out, in0=in0, in1=in1, op=ADD)
+
+
+def pool_refined(nc, work, label, tiles, oo, oi, io, ii, coarse, fine):
     tw = work.tile([P, 2, tiles, SLOTS], F32, name="%s_tw" % label)
     cw = work.tile([P, 2, tiles, 2, 8, 6], F32, name="%s_cw" % label)
     th = work.tile([P, tiles, 2, 8, 6], F32, name="%s_th" % label)
     s6 = work.tile([P, tiles, B, 36], F32, name="%s_s6" % label)
     s3 = work.tile([P, tiles, B, 9], F32, name="%s_s3" % label)
     s1 = work.tile([P, tiles, B, 1], F32, name="%s_s1" % label)
-    for kh, (outer, inner) in enumerate(((oo, oi), (io, ii))):
-        nc.vector.tensor_tensor(out=tw[:, kh], in0=outer, in1=inner, op=ADD)
-        cells = cw[:, kh].rearrange("c t ph m (e k) -> c t ph m e k", k=3)
-        three_to_four(
-            nc,
-            [cells[:, :, :, :, :, k] for k in range(3)],
-            along_w(outer),
-            along_w(inner),
-            along_w(tw[:, kh]),
-        )
-    nc.vector.tensor_tensor(out=th[:], in0=cw[:, 0], in1=cw[:, 1], op=ADD)
-    cells = s6[:].rearrange("c t b (e k w) -> c t b e k w", e=2, k=3)
-    three_to_four(
-        nc,
-        [cells[:, :, :, :, k, :] for k in range(3)],
-        along_h(cw[:, 0]),
-        along_h(cw[:, 1]),
-        along_h(th[:]),
-    )
+    outer_w = (along_w(oo), along_w(io))
+    inner_w = (along_w(oi), along_w(ii))
+    total_w = (along_w(tw[:, 0]), along_w(tw[:, 1]))
+    cells_w = [cw[:, kh].rearrange("c t ph m (e k) -> c t ph m e k", k=3) for kh in range(2)]
+    outer_h, inner_h, total_h = along_h(cw[:, 0]), along_h(cw[:, 1]), along_h(th[:])
+    cells_h = s6[:].rearrange("c t b (e k w) -> c t b e k w", e=2, k=3)
+    add(nc, tw[:, 0], oo, oi)
+    add(nc, tw[:, 1], io, ii)
+    for kh in range(2):
+        add(nc, cells_w[kh][:, :, :, :, :, 1], outer_w[kh](1, 0), outer_w[kh](0, 1))
+    for kh in range(2):
+        add(nc, cells_w[kh][:, :, :, :, :, 0], total_w[kh](0, 0), inner_w[kh](1, 0))
+        add(nc, cells_w[kh][:, :, :, :, :, 2], total_w[kh](1, 1), inner_w[kh](0, 1))
+    if fine is not None:
+        s8 = work.tile([P, tiles, SLOTS], F32, name="%s_s8" % label)
+        add(nc, s8[:], tw[:, 0], tw[:, 1])
+    add(nc, cells_h[:, :, :, :, 1, :], outer_h(1, 0), outer_h(0, 1))
+    add(nc, th[:], cw[:, 0], cw[:, 1])
+    if fine is not None:
+        by_slot = s8[:].rearrange("c t (ph pw b eh ew) -> c t ph b eh ew pw", ph=2, pw=2, b=B, eh=4)
+        by_cell = fine.rearrange("c t b (eh ph ew pw) -> c t ph b eh ew pw", eh=4, ph=2, ew=4)
+        for ph in range(2):
+            nc.vector.tensor_scalar_mul(out=by_cell[:, :, ph], in0=by_slot[:, :, ph], scalar1=1.0 / 9.0)
+    add(nc, cells_h[:, :, :, :, 0, :], total_h(0, 0), inner_h(1, 0))
+    add(nc, cells_h[:, :, :, :, 2, :], total_h(1, 1), inner_h(0, 1))
     nc.vector.tensor_reduce(
         out=s3[:].rearrange("c t b (h w) -> c (t b h) w", h=3),
         in_=s6[:].rearrange("c t b (h i w j) -> c (t b h) w i j", h=3, i=2, w=3, j=2),
@@ -88,14 +92,13 @@ def pool_refined(nc, work, label, tiles, oo, oi, io, ii, coarse):
     )
     nc.vector.tensor_reduce(
         out=s1[:].rearrange("c t b o -> c (t b o)"),
-        in_=s3[:].rearrange("c t b n -> c (t b) n"),
+        in_=s6[:].rearrange("c t b n -> c (t b) n"),
         axis=AXIS.X,
         op=ADD,
     )
-    nc.vector.tensor_scalar_mul(out=coarse[:, :, :, 0:1], in0=s1[:], scalar1=1.0 / 576.0)
-    nc.vector.tensor_scalar_mul(out=coarse[:, :, :, 1:10], in0=s3[:], scalar1=1.0 / 64.0)
     nc.vector.tensor_scalar_mul(out=coarse[:, :, :, 10:46], in0=s6[:], scalar1=1.0 / 16.0)
-    return tw
+    nc.vector.tensor_scalar_mul(out=coarse[:, :, :, 1:10], in0=s3[:], scalar1=1.0 / 64.0)
+    nc.vector.tensor_scalar_mul(out=coarse[:, :, :, 0:1], in0=s1[:], scalar1=1.0 / 576.0)
 
 
 def tile_afnb_pa_kernel(
@@ -168,7 +171,7 @@ def tile_afnb_pa_kernel(
         nc.vector.memset(pool_mat[:], 0.0)
         nc.vector.tensor_copy(out=units[:, 3, :], in_=ident[:])
         pool_refined(
-            nc, work, "mat", 4, units[:, 3:7], units[:, 2:6], units[:, 1:5], units[:, 0:4], pool_mat[:, :, :, 0:COARSE]
+            nc, work, "mat", 4, units[:, 3:7], units[:, 2:6], units[:, 1:5], units[:, 0:4], pool_mat[:, :, :, 0:COARSE], None
         )
 
         x_codes = keep.tile([P, PASSES, LAYERS, SLOTS], U32, align_bytes=64)
@@ -276,21 +279,22 @@ def tile_afnb_pa_kernel(
         h01 = keep.tile([P, 3, KEY_TILES, SLOTS], F32)
         k_oo = keep.tile([P, KEY_TILES, SLOTS], F32)
         k_io = keep.tile([P, KEY_TILES, SLOTS], F32)
-        nc.vector.tensor_tensor(out=h01[:], in0=relu[:, 0:3], in1=relu[:, 3:6], op=ADD)
-        nc.vector.tensor_tensor(out=k_oo[:], in0=h01[:, 0], in1=h01[:, 1], op=ADD)
-        nc.vector.tensor_tensor(out=k_io[:], in0=relu[:, 6], in1=relu[:, 7], op=ADD)
+        add(nc, h01[:], relu[:, 0:3], relu[:, 3:6])
+        add(nc, k_io[:], relu[:, 6], relu[:, 7])
+        add(nc, k_oo[:], h01[:, 0], h01[:, 1])
         key_sb = keep.tile([P, KEY_TILES, B, COARSE + FINE], F32)
-        tw = pool_refined(
-            nc, work, "key", KEY_TILES, k_oo[:], h01[:, 2], k_io[:], relu[:, 8], key_sb[:, :, :, 0:COARSE]
+        pool_refined(
+            nc,
+            work,
+            "key",
+            KEY_TILES,
+            k_oo[:],
+            h01[:, 2],
+            k_io[:],
+            relu[:, 8],
+            key_sb[:, :, :, 0:COARSE],
+            key_sb[:, :, :, COARSE : COARSE + FINE],
         )
-        k_fine = keep.tile([P, KEY_TILES, SLOTS], F32)
-        nc.vector.tensor_tensor(out=k_fine[:], in0=tw[:, 0], in1=tw[:, 1], op=ADD)
-        by_slot = k_fine[:].rearrange("c t (ph pw b eh ew) -> c t ph b eh ew pw", ph=2, pw=2, b=B, eh=4)
-        by_cell = key_sb[:, :, :, COARSE : COARSE + FINE].rearrange(
-            "c t b (eh ph ew pw) -> c t ph b eh ew pw", eh=4, ph=2, ew=4
-        )
-        for ph in range(2):
-            nc.vector.tensor_scalar_mul(out=by_cell[:, :, ph], in0=by_slot[:, :, ph], scalar1=1.0 / 9.0)
         for t in range(KEY_TILES):
             nc.scalar.dma_start(out=out_1[:, P * t : P * (t + 1), :].rearrange("b c l -> c b l"), in_=key_sb[:, t])
 

@@ -10,8 +10,7 @@ U32 = mybir.dt.uint32
 U8 = mybir.dt.uint8
 FP8X4 = mybir.dt.float8_e4m3fn_x4
 FP4X4 = mybir.dt.float4_e2m1fn_x4
-ADD = mybir.AluOpType.add
-MULT = mybir.AluOpType.mult
+ALU = mybir.AluOpType
 ACT = mybir.ActivationFunctionType
 AXIS = mybir.AxisListType
 
@@ -27,20 +26,23 @@ FLOPS = 2 * B * PIX * CL * (CK + CV)
 
 LAYER_BASE = (0, 1, 2)
 LAYER_STEP = (4, 4, 1)
-LAYERS = 9
+INNER = 2
+LAYERS = sorted([(lh, lw) for lh in range(3) for lw in range(3)], key=lambda hw: (hw[1] == INNER, hw[0] == INNER))
+KINDS = 4
 SLOTS = 128
+WIDE = 4
 COARSE = 46
 FINE = 64
 ROWS = 64
 
 
-def layer_class(layer):
-    return 2 * (layer // 3 == 2) + (layer % 3 == 2)
+def kind_of(lh, lw):
+    return 2 * (lw == INNER) + (lh == INNER)
 
 
 def along_w(ap):
-    view = ap.rearrange("c t (ph pw m e x) -> c t ph pw m e x", ph=2, pw=2, m=8, e=2, x=2)
-    return lambda p, x: view[:, :, :, p, :, :, x]
+    view = ap.rearrange("c kh t (ph pw m e x) -> c kh t ph pw m e x", ph=2, pw=2, m=8, e=2, x=2)
+    return lambda p, x: view[:, :, :, :, p, :, :, x]
 
 
 def along_h(ap):
@@ -49,56 +51,51 @@ def along_h(ap):
 
 
 def add(nc, out, in0, in1):
-    nc.vector.tensor_tensor(out=out, in0=in0, in1=in1, op=ADD)
+    nc.vector.tensor_tensor(out=out, in0=in0, in1=in1, op=ALU.add)
 
 
-def pool_refined(nc, work, label, tiles, oo, oi, io, ii, coarse, fine):
-    tw = work.tile([P, 2, tiles, SLOTS], F32, name="%s_tw" % label)
-    cw = work.tile([P, 2, tiles, 2, 8, 6], F32, name="%s_cw" % label)
-    th = work.tile([P, tiles, 2, 8, 6], F32, name="%s_th" % label)
-    s6 = work.tile([P, tiles, B, 36], F32, name="%s_s6" % label)
+def pool_along_w(nc, work, label, tiles, dtype, outer, inner):
+    three = work.tile([P, 2, tiles, SLOTS], dtype, name="%s_three_w" % label)
+    four = work.tile([P, 2, tiles, 2, 8, 6], dtype, name="%s_four_w" % label)
+    cells = four[:].rearrange("c kh t ph m (e k) -> c kh t ph m e k", k=3)
+    outer_at, inner_at, three_at = along_w(outer), along_w(inner), along_w(three[:])
+    add(nc, three[:], outer, inner)
+    add(nc, cells[:, :, :, :, :, :, 1], outer_at(1, 0), outer_at(0, 1))
+    add(nc, cells[:, :, :, :, :, :, 0], three_at(0, 0), inner_at(1, 0))
+    add(nc, cells[:, :, :, :, :, :, 2], three_at(1, 1), inner_at(0, 1))
+    return three, four
+
+
+def pool_along_h(nc, work, label, tiles, dtype, four):
+    three = work.tile([P, tiles, 2, 8, 6], dtype, name="%s_three_h" % label)
+    s6 = work.tile([P, tiles, B, 36], dtype, name="%s_s6" % label)
+    cells = s6[:].rearrange("c t b (e k w) -> c t b e k w", e=2, k=3)
+    outer_at, inner_at, three_at = along_h(four[:, 0]), along_h(four[:, 1]), along_h(three[:])
+    add(nc, three[:], four[:, 0], four[:, 1])
+    add(nc, cells[:, :, :, :, 1, :], outer_at(1, 0), outer_at(0, 1))
+    add(nc, cells[:, :, :, :, 0, :], three_at(0, 0), inner_at(1, 0))
+    add(nc, cells[:, :, :, :, 2, :], three_at(1, 1), inner_at(0, 1))
+    return s6
+
+
+def pool_coarser(nc, work, label, tiles, s6, coarse):
     s3 = work.tile([P, tiles, B, 9], F32, name="%s_s3" % label)
     s1 = work.tile([P, tiles, B, 1], F32, name="%s_s1" % label)
-    outer_w = (along_w(oo), along_w(io))
-    inner_w = (along_w(oi), along_w(ii))
-    total_w = (along_w(tw[:, 0]), along_w(tw[:, 1]))
-    cells_w = [cw[:, kh].rearrange("c t ph m (e k) -> c t ph m e k", k=3) for kh in range(2)]
-    outer_h, inner_h, total_h = along_h(cw[:, 0]), along_h(cw[:, 1]), along_h(th[:])
-    cells_h = s6[:].rearrange("c t b (e k w) -> c t b e k w", e=2, k=3)
-    add(nc, tw[:, 0], oo, oi)
-    add(nc, tw[:, 1], io, ii)
-    for kh in range(2):
-        add(nc, cells_w[kh][:, :, :, :, :, 1], outer_w[kh](1, 0), outer_w[kh](0, 1))
-    for kh in range(2):
-        add(nc, cells_w[kh][:, :, :, :, :, 0], total_w[kh](0, 0), inner_w[kh](1, 0))
-        add(nc, cells_w[kh][:, :, :, :, :, 2], total_w[kh](1, 1), inner_w[kh](0, 1))
-    if fine is not None:
-        s8 = work.tile([P, tiles, SLOTS], F32, name="%s_s8" % label)
-        add(nc, s8[:], tw[:, 0], tw[:, 1])
-    add(nc, cells_h[:, :, :, :, 1, :], outer_h(1, 0), outer_h(0, 1))
-    add(nc, th[:], cw[:, 0], cw[:, 1])
-    if fine is not None:
-        by_slot = s8[:].rearrange("c t (ph pw b eh ew) -> c t ph b eh ew pw", ph=2, pw=2, b=B, eh=4)
-        by_cell = fine.rearrange("c t b (eh ph ew pw) -> c t ph b eh ew pw", eh=4, ph=2, ew=4)
-        for ph in range(2):
-            nc.vector.tensor_scalar_mul(out=by_cell[:, :, ph], in0=by_slot[:, :, ph], scalar1=1.0 / 9.0)
-    add(nc, cells_h[:, :, :, :, 0, :], total_h(0, 0), inner_h(1, 0))
-    add(nc, cells_h[:, :, :, :, 2, :], total_h(1, 1), inner_h(0, 1))
     nc.vector.tensor_reduce(
         out=s3[:].rearrange("c t b (h w) -> c (t b h) w", h=3),
         in_=s6[:].rearrange("c t b (h i w j) -> c (t b h) w i j", h=3, i=2, w=3, j=2),
         axis=AXIS.XY,
-        op=ADD,
+        op=ALU.add,
     )
     nc.vector.tensor_reduce(
         out=s1[:].rearrange("c t b o -> c (t b o)"),
         in_=s6[:].rearrange("c t b n -> c (t b) n"),
         axis=AXIS.X,
-        op=ADD,
+        op=ALU.add,
     )
-    nc.vector.tensor_scalar_mul(out=coarse[:, :, :, 10:46], in0=s6[:], scalar1=1.0 / 16.0)
-    nc.vector.tensor_scalar_mul(out=coarse[:, :, :, 1:10], in0=s3[:], scalar1=1.0 / 64.0)
-    nc.vector.tensor_scalar_mul(out=coarse[:, :, :, 0:1], in0=s1[:], scalar1=1.0 / 576.0)
+    nc.scalar.mul(out=coarse[:, :, :, 10:46], in_=s6[:], mul=1.0 / 16.0)
+    nc.scalar.mul(out=coarse[:, :, :, 1:10], in_=s3[:], mul=1.0 / 64.0)
+    nc.scalar.mul(out=coarse[:, :, :, 0:1], in_=s1[:], mul=1.0 / 576.0)
 
 
 def tile_afnb_pa_kernel(
@@ -140,15 +137,15 @@ def tile_afnb_pa_kernel(
         nc.sync.dma_start(out=wk_codes[:].bitcast(I32), in_=wk_words.bitcast(I32).rearrange("g p n -> p g n"))
         load_planes(wk_planes, wk_scales)
         load_x(1)
-
-        ident = keep.tile([P, P], BF16)
-        make_identity(nc, ident[:])
         vecs = [keep.tile([P, KEY_TILES], BF16, name="vec%d" % i) for i in range(5)]
         with nc.allow_non_contiguous_dma(reason="five vectors of 256 values, one value a partition"):
             for tile_, vec in zip(vecs, (bk, gk, bek, mk, vk)):
                 nc.sync.dma_start(out=tile_[:], in_=vec.rearrange("(t c) -> c t", c=P))
         bv_all = keep.tile([P, CV], BF16)
         nc.sync.dma_start(out=bv_all[:], in_=bv.partition_broadcast(P))
+
+        ident = keep.tile([P, P], BF16)
+        make_identity(nc, ident[:])
         bk_c, gk_c, bek_c, mk_c, vk_c = [tile_[:] for tile_ in vecs]
         minus_half = keep.tile([P, KEY_TILES], F32)
         var_eps = keep.tile([P, KEY_TILES], F32)
@@ -158,38 +155,43 @@ def tile_afnb_pa_kernel(
         scaled = keep.tile([P, KEY_TILES], F32)
         bn_shift = keep.tile([P, KEY_TILES], F32)
         nc.gpsimd.memset(minus_half[:], -0.5)
-        nc.gpsimd.tensor_scalar(out=var_eps[:], in0=vk_c, scalar1=1.0, scalar2=EPS, op0=MULT, op1=ADD)
-        nc.gpsimd.tensor_tensor(out=rstd[:], in0=var_eps[:], in1=minus_half[:], op=mybir.AluOpType.pow)
-        nc.gpsimd.tensor_tensor(out=bn_scale[:], in0=gk_c, in1=rstd[:], op=MULT)
-        nc.gpsimd.tensor_tensor(out=centred[:], in0=bk_c, in1=mk_c, op=mybir.AluOpType.subtract)
-        nc.gpsimd.tensor_tensor(out=scaled[:], in0=centred[:], in1=bn_scale[:], op=MULT)
-        nc.gpsimd.tensor_tensor(out=bn_shift[:], in0=scaled[:], in1=bek_c, op=ADD)
+        nc.gpsimd.tensor_scalar(out=var_eps[:], in0=vk_c, scalar1=1.0, scalar2=EPS, op0=ALU.mult, op1=ALU.add)
+        nc.gpsimd.tensor_tensor(out=rstd[:], in0=var_eps[:], in1=minus_half[:], op=ALU.pow)
+        nc.gpsimd.tensor_tensor(out=bn_scale[:], in0=gk_c, in1=rstd[:], op=ALU.mult)
+        nc.gpsimd.tensor_tensor(out=centred[:], in0=bk_c, in1=mk_c, op=ALU.subtract)
+        nc.gpsimd.tensor_tensor(out=scaled[:], in0=centred[:], in1=bn_scale[:], op=ALU.mult)
+        nc.gpsimd.tensor_tensor(out=bn_shift[:], in0=scaled[:], in1=bek_c, op=ALU.add)
 
-        units = keep.tile([P, 7, SLOTS], F32)
-        pool_mat = keep.tile([P, 4, B, ROWS], F32)
-        nc.vector.memset(units[:], 0.0)
+        units = keep.tile([P, 2, 2, KINDS, SLOTS], BF16)
+        pool_mat = keep.tile([P, KINDS, B, ROWS], F32)
+        nc.vector.memset(units[:].bitcast(I32), 0)
         nc.vector.memset(pool_mat[:], 0.0)
-        nc.vector.tensor_copy(out=units[:, 3, :], in_=ident[:])
-        pool_refined(
-            nc, work, "mat", 4, units[:, 3:7], units[:, 2:6], units[:, 1:5], units[:, 0:4], pool_mat[:, :, :, 0:COARSE], None
+        nc.vector.tensor_copy(
+            out=units[:].rearrange("c kw kh t s -> c (kw kh t) s")[:, 0 : 4 * KINDS : KINDS + 1, :],
+            in_=ident[:].unsqueeze(1).to_broadcast([P, KINDS, SLOTS]),
         )
+        mat_three, mat_four = pool_along_w(nc, work, "mat", KINDS, BF16, units[:, 0], units[:, 1])
+        mat_s6 = pool_along_h(nc, work, "mat", KINDS, BF16, mat_four)
+        pool_coarser(nc, work, "mat", KINDS, mat_s6, pool_mat[:, :, :, 0:COARSE])
 
-        x_codes = keep.tile([P, PASSES, LAYERS, SLOTS], U32, align_bytes=64)
-        x_planes = keep.tile([P, PASSES, LAYERS, SLOTS], U8, align_bytes=64)
-        v_class = [psum.tile([P, CV], F32, name="v_class%d" % c) for c in range(4)]
+        n_layers = len(LAYERS)
+        x_codes = keep.tile([P, PASSES, n_layers, SLOTS], U32, align_bytes=64)
+        x_planes = keep.tile([P, PASSES, n_layers, SLOTS], U8, align_bytes=64)
+        v_kind = [psum.tile([P, CV], F32, name="v_kind%d" % kind) for kind in range(KINDS)]
         key_tags = (("key_a", "key_c"), ("key_b", "key_d"))
         u_wide = {}
-        relu = keep.tile([P, LAYERS, KEY_TILES, SLOTS], F32)
-        g_sb = [keep.tile([P, CV], F32, name="g_sb%d" % c) for c in range(4)]
-        members = [[layer for layer in range(LAYERS) if layer_class(layer) == c] for c in range(4)]
-        steps = [(g, layer) for g in range(PASSES) for layer in range(LAYERS)]
+        relu = keep.tile([P, 2 * WIDE, KEY_TILES, SLOTS], F32)
+        k_sums = keep.tile([P, 5, KEY_TILES, SLOTS], F32)
+        g_sb = [keep.tile([P, CV], F32, name="g_sb%d" % kind) for kind in range(KINDS)]
+        kinds = [kind_of(lh, lw) for lh, lw in LAYERS]
+        steps = [(g, pos) for g in range(PASSES) for pos in range(n_layers)]
         grouped = {}
 
-        def regroup(g, layer):
-            lh, lw = divmod(layer, 3)
+        def regroup(g, pos):
+            lh, lw = LAYERS[pos]
             pixels = raw[g][:].rearrange("p j b (eh sh ew sw) -> p j b eh sh ew sw", eh=4, sh=6, ew=4, sw=6)
             tile_ = stage.tile([P, SLOTS, PACK], BF16, align_bytes=64, name="grouped")
-            grouped[(g, layer)] = tile_
+            grouped[(g, pos)] = tile_
             quarters = tile_[:].rearrange("p (ph pw m ew) j -> p ph pw m ew j", ph=2, pw=2, m=8)
             cols = slice(LAYER_BASE[lw], LAYER_BASE[lw] + LAYER_STEP[lw] + 1, LAYER_STEP[lw])
             rows = [
@@ -221,92 +223,91 @@ def tile_afnb_pa_kernel(
         def relu_wide(q):
             for t in range(KEY_TILES):
                 norm_relu(
-                    relu[:, 4 * q : 4 * q + 4, t, :], u_wide[(t, q)][:].rearrange("c (l s) -> c l s", s=SLOTS), t
+                    relu[:, WIDE * q : WIDE * (q + 1), t, :],
+                    u_wide[(t, q)][:].rearrange("c (l s) -> c l s", s=SLOTS),
+                    t,
                 )
 
         regroup(*steps[0])
-        for i, (g, layer) in enumerate(steps):
+        for i, (g, pos) in enumerate(steps):
             if i + 1 < len(steps):
                 regroup(*steps[i + 1])
             nc.vector.quantize_mx(
-                out=x_codes[:, g, layer, :].bitcast(FP8X4),
-                scales=x_planes[:, g, layer, :],
-                in_=grouped[(g, layer)][:].rearrange("p s j -> p (s j)"),
+                out=x_codes[:, g, pos, :].bitcast(FP8X4),
+                scales=x_planes[:, g, pos, :],
+                in_=grouped[(g, pos)][:].rearrange("p s j -> p (s j)"),
             )
-            c = layer_class(layer)
+            kind = kinds[pos]
             nc.tensor.matmul_mx(
-                out=v_class[c][:],
-                lhsT=x_codes[:, g, layer, :].bitcast(FP8X4),
-                lhsT_scale=x_planes[:, g, layer, :],
+                out=v_kind[kind][:],
+                lhsT=x_codes[:, g, pos, :].bitcast(FP8X4),
+                lhsT_scale=x_planes[:, g, pos, :],
                 rhs=wv_codes[:, g, :].bitcast(FP4X4),
                 rhs_scale=wv_planes[:, g, :],
-                start=(g == 0 and layer == members[c][0]),
-                stop=(g == PASSES - 1 and layer == members[c][-1]),
+                start=(g == 0 and pos == kinds.index(kind)),
+                stop=(g == PASSES - 1 and (pos + 1 == n_layers or kinds[pos + 1] != kind)),
             )
-            if layer % 4 == 3:
-                q = layer // 4
+            if pos % WIDE == WIDE - 1:
+                q = pos // WIDE
                 for t in range(KEY_TILES):
                     if g == 0:
-                        u_wide[(t, q)] = psum.tile([P, 4 * SLOTS], F32, name="u_wide%d%d" % (t, q), tag=key_tags[t][q])
+                        u_wide[(t, q)] = psum.tile([P, WIDE * SLOTS], F32, name="u_wide%d%d" % (t, q), tag=key_tags[t][q])
                     key_pass(
                         u_wide[(t, q)][:],
                         t,
                         g,
-                        x_codes[:, g, 4 * q : 4 * q + 4, :].rearrange("p l s -> p (l s)"),
-                        x_planes[:, g, 4 * q : 4 * q + 4, :].rearrange("p l s -> p (l s)"),
+                        x_codes[:, g, WIDE * q : WIDE * (q + 1), :].rearrange("p l s -> p (l s)"),
+                        x_planes[:, g, WIDE * q : WIDE * (q + 1), :].rearrange("p l s -> p (l s)"),
                     )
-            if g == PASSES - 1 and layer == 6:
+            if g == PASSES - 1 and pos == 6:
                 relu_wide(0)
 
         relu_wide(1)
         u_last = psum.tile([P, KEY_TILES, SLOTS], F32, tag="key_a")
         for t in range(KEY_TILES):
             for g in range(PASSES):
-                key_pass(u_last[:, t, :], t, g, x_codes[:, g, LAYERS - 1, :], x_planes[:, g, LAYERS - 1, :])
-            norm_relu(relu[:, LAYERS - 1, t, :], u_last[:, t, :], t)
+                key_pass(u_last[:, t, :], t, g, x_codes[:, g, n_layers - 1, :], x_planes[:, g, n_layers - 1, :])
+            norm_relu(k_sums[:, 4, t, :], u_last[:, t, :], t)
 
         coarse_ps = psum.tile([P, CV], F32, tag="key_b")
-        for c in range(4):
-            nc.scalar.copy(out=g_sb[c][:], in_=v_class[c][:])
+        for kind in range(KINDS):
+            nc.scalar.copy(out=g_sb[kind][:], in_=v_kind[kind][:])
             nc.tensor.matmul(
                 out=coarse_ps[:],
-                lhsT=pool_mat[:, c].rearrange("p b l -> p (b l)"),
-                rhs=g_sb[c][:],
-                start=(c == 0),
-                stop=(c == 3),
+                lhsT=pool_mat[:, kind].rearrange("p b l -> p (b l)"),
+                rhs=g_sb[kind][:],
+                start=(kind == 0),
+                stop=(kind == KINDS - 1),
             )
 
-        h01 = keep.tile([P, 3, KEY_TILES, SLOTS], F32)
-        k_oo = keep.tile([P, KEY_TILES, SLOTS], F32)
-        k_io = keep.tile([P, KEY_TILES, SLOTS], F32)
-        add(nc, h01[:], relu[:, 0:3], relu[:, 3:6])
-        add(nc, k_io[:], relu[:, 6], relu[:, 7])
-        add(nc, k_oo[:], h01[:, 0], h01[:, 1])
+        sum01 = keep.tile([P, CV], F32)
+        sum012 = keep.tile([P, CV], F32)
+        sum_all = keep.tile([P, CV], F32)
+        v_fine = keep.tile([P, CV], F32)
+        v_coarse = keep.tile([P, CV], F32)
         key_sb = keep.tile([P, KEY_TILES, B, COARSE + FINE], F32)
-        pool_refined(
-            nc,
-            work,
-            "key",
-            KEY_TILES,
-            k_oo[:],
-            h01[:, 2],
-            k_io[:],
-            relu[:, 8],
-            key_sb[:, :, :, 0:COARSE],
-            key_sb[:, :, :, COARSE : COARSE + FINE],
+        k_fine = keep.tile([P, KEY_TILES, SLOTS], F32)
+        pairs = relu[:].rearrange("c (i two) t s -> c i two t s", two=2)
+        add(nc, k_sums[:, 0:4], pairs[:, :, 0], pairs[:, :, 1])
+        add(nc, sum01[:], g_sb[0][:], g_sb[1][:])
+        add(nc, k_sums[:, 1], k_sums[:, 0], k_sums[:, 1])
+        add(nc, sum012[:], sum01[:], g_sb[2][:])
+        k_three, k_four = pool_along_w(nc, work, "key", KEY_TILES, F32, k_sums[:, 1:3], k_sums[:, 3:5])
+        add(nc, k_fine[:], k_three[:, 0], k_three[:, 1])
+        by_slot = k_fine[:].rearrange("c t (ph pw b eh ew) -> c t ph b eh ew pw", ph=2, pw=2, b=B, eh=4)
+        by_cell = key_sb[:, :, :, COARSE : COARSE + FINE].rearrange(
+            "c t b (eh ph ew pw) -> c t ph b eh ew pw", eh=4, ph=2, ew=4
         )
+        for ph in range(2):
+            nc.scalar.mul(out=by_cell[:, :, ph], in_=by_slot[:, :, ph], mul=1.0 / 9.0)
+        k_s6 = pool_along_h(nc, work, "key", KEY_TILES, F32, k_four)
+        add(nc, sum_all[:], sum012[:], g_sb[3][:])
+        pool_coarser(nc, work, "key", KEY_TILES, k_s6, key_sb[:, :, :, 0:COARSE])
         for t in range(KEY_TILES):
             nc.scalar.dma_start(out=out_1[:, P * t : P * (t + 1), :].rearrange("b c l -> c b l"), in_=key_sb[:, t])
 
-        sum01 = keep.tile([P, CV], F32)
-        sum23 = keep.tile([P, CV], F32)
-        sum_all = keep.tile([P, CV], F32)
-        v_fine = keep.tile([P, CV], F32)
-        nc.gpsimd.tensor_tensor(out=sum01[:], in0=g_sb[0][:], in1=g_sb[1][:], op=ADD)
-        nc.gpsimd.tensor_tensor(out=sum23[:], in0=g_sb[2][:], in1=g_sb[3][:], op=ADD)
-        nc.gpsimd.tensor_tensor(out=sum_all[:], in0=sum01[:], in1=sum23[:], op=ADD)
         nc.vector.scalar_tensor_tensor(
-            out=v_fine[:], in0=sum_all[:], scalar=1.0 / 9.0, in1=bv_all[:], op0=MULT, op1=ADD
+            out=v_fine[:], in0=sum_all[:], scalar=1.0 / 9.0, in1=bv_all[:], op0=ALU.mult, op1=ALU.add
         )
         for b in range(B):
             cells = out_0[b, COARSE : COARSE + FINE, :].rearrange(
@@ -316,7 +317,6 @@ def tile_afnb_pa_kernel(
                 for pw in range(2):
                     first = 64 * ph + 32 * pw + 16 * b
                     nc.sync.dma_start(out=cells[ph, pw], in_=v_fine[first : first + 16, :])
-        v_coarse = keep.tile([P, CV], F32)
-        nc.vector.tensor_tensor(out=v_coarse[:], in0=coarse_ps[:], in1=bv_all[:], op=ADD)
+        add(nc, v_coarse[:], coarse_ps[:], bv_all[:])
         for b in range(B):
             nc.sync.dma_start(out=out_0[b, 0:COARSE, :], in_=v_coarse[ROWS * b : ROWS * b + COARSE, :])

@@ -40,41 +40,40 @@ def kind_of(lh, lw):
     return 2 * (lw == INNER) + (lh == INNER)
 
 
-def along_w(ap):
-    view = ap.rearrange("c kh t (ph pw m e x) -> c kh t ph pw m e x", ph=2, pw=2, m=8, e=2, x=2)
-    return lambda p, x: view[:, :, :, :, p, :, :, x]
-
-
-def along_h(ap):
-    view = ap.rearrange("c t ph (b e x) k -> c t ph b e x k", b=B, e=2, x=2)
-    return lambda p, x: view[:, :, p, :, :, x, :]
-
-
 def add(nc, out, in0, in1):
     nc.vector.tensor_tensor(out=out, in0=in0, in1=in1, op=ALU.add)
 
 
+def three_to_four(nc, cells, outer, inner, three):
+    add(nc, cells[:, :, :, :, 1], outer[:, :, :, :, 1], outer[:, :, :, :, 2])
+    add(nc, cells[:, :, :, :, 0:3:2], three[:, :, :, :, 0:4:3], inner[:, :, :, :, 1:3])
+
+
 def pool_along_w(nc, work, label, tiles, dtype, outer, inner):
     three = work.tile([P, 2, tiles, SLOTS], dtype, name="%s_three_w" % label)
-    four = work.tile([P, 2, tiles, 2, 8, 6], dtype, name="%s_four_w" % label)
-    cells = four[:].rearrange("c kh t ph m (e k) -> c kh t ph m e k", k=3)
-    outer_at, inner_at, three_at = along_w(outer), along_w(inner), along_w(three[:])
+    four = work.tile([P, 2, tiles, 16, 6], dtype, name="%s_four_w" % label)
     add(nc, three[:], outer, inner)
-    add(nc, cells[:, :, :, :, :, :, 1], outer_at(1, 0), outer_at(0, 1))
-    add(nc, cells[:, :, :, :, :, :, 0], three_at(0, 0), inner_at(1, 0))
-    add(nc, cells[:, :, :, :, :, :, 2], three_at(1, 1), inner_at(0, 1))
+    three_to_four(
+        nc,
+        four[:].rearrange("c kh t m (e k) -> c kh (t m) e k", k=3),
+        outer.rearrange("c kh t (m e a) -> c kh (t m) e a", e=2, a=4),
+        inner.rearrange("c kh t (m e a) -> c kh (t m) e a", e=2, a=4),
+        three[:].rearrange("c kh t (m e a) -> c kh (t m) e a", e=2, a=4),
+    )
     return three, four
 
 
 def pool_along_h(nc, work, label, tiles, dtype, four):
-    three = work.tile([P, tiles, 2, 8, 6], dtype, name="%s_three_h" % label)
+    three = work.tile([P, tiles, 16, 6], dtype, name="%s_three_h" % label)
     s6 = work.tile([P, tiles, B, 36], dtype, name="%s_s6" % label)
-    cells = s6[:].rearrange("c t b (e k w) -> c t b e k w", e=2, k=3)
-    outer_at, inner_at, three_at = along_h(four[:, 0]), along_h(four[:, 1]), along_h(three[:])
     add(nc, three[:], four[:, 0], four[:, 1])
-    add(nc, cells[:, :, :, :, 1, :], outer_at(1, 0), outer_at(0, 1))
-    add(nc, cells[:, :, :, :, 0, :], three_at(0, 0), inner_at(1, 0))
-    add(nc, cells[:, :, :, :, 2, :], three_at(1, 1), inner_at(0, 1))
+    three_to_four(
+        nc,
+        s6[:].rearrange("c t b (e k w) -> c t b e k w", e=2, k=3),
+        four[:, 0].rearrange("c t (b e a) w -> c t b e a w", b=B, e=2),
+        four[:, 1].rearrange("c t (b e a) w -> c t b e a w", b=B, e=2),
+        three[:].rearrange("c t (b e a) w -> c t b e a w", b=B, e=2),
+    )
     return s6
 
 
@@ -114,6 +113,11 @@ def tile_afnb_pa_kernel(
         wk_codes = keep.tile([P, PASSES, 2 * CK], U8, align_bytes=64)
         wv_codes = keep.tile([P, PASSES, 2 * CV], U8, align_bytes=64)
         raw = [keep.tile([P, PACK, B, PIX], BF16, name="raw%d" % g) for g in range(PASSES)]
+        bias_rows = keep.tile([P, CV], BF16)
+        ones = keep.tile([P, P], BF16)
+        nc.gpsimd.memset(bias_rows[:], 0.0)
+        nc.gpsimd.memset(ones[:], 1.0)
+
         nc.vector.memset(wv_planes[:].bitcast(I32), 0)
         nc.vector.memset(wk_planes[:].bitcast(I32), 0)
 
@@ -134,15 +138,14 @@ def tile_afnb_pa_kernel(
         load_planes(wv_planes, wv_scales)
         nc.sync.dma_start(out=wv_codes[:].bitcast(I32), in_=wv_words.bitcast(I32).rearrange("g p n -> p g n"))
         load_x(0)
-        nc.sync.dma_start(out=wk_codes[:].bitcast(I32), in_=wk_words.bitcast(I32).rearrange("g p n -> p g n"))
         load_planes(wk_planes, wk_scales)
+        nc.sync.dma_start(out=wk_codes[:].bitcast(I32), in_=wk_words.bitcast(I32).rearrange("g p n -> p g n"))
         load_x(1)
         vecs = [keep.tile([P, KEY_TILES], BF16, name="vec%d" % i) for i in range(5)]
         with nc.allow_non_contiguous_dma(reason="five vectors of 256 values, one value a partition"):
             for tile_, vec in zip(vecs, (bk, gk, bek, mk, vk)):
                 nc.sync.dma_start(out=tile_[:], in_=vec.rearrange("(t c) -> c t", c=P))
-        bv_all = keep.tile([P, CV], BF16)
-        nc.sync.dma_start(out=bv_all[:], in_=bv.partition_broadcast(P))
+        nc.sync.dma_start(out=bias_rows[0:1, :], in_=bv.unsqueeze(0))
 
         ident = keep.tile([P, P], BF16)
         make_identity(nc, ident[:])
@@ -192,17 +195,17 @@ def tile_afnb_pa_kernel(
             pixels = raw[g][:].rearrange("p j b (eh sh ew sw) -> p j b eh sh ew sw", eh=4, sh=6, ew=4, sw=6)
             tile_ = stage.tile([P, SLOTS, PACK], BF16, align_bytes=64, name="grouped")
             grouped[(g, pos)] = tile_
-            quarters = tile_[:].rearrange("p (ph pw m ew) j -> p ph pw m ew j", ph=2, pw=2, m=8)
+            halves = tile_[:].rearrange("p (m ph ew pw) j -> p ph m ew pw j", m=8, ph=2, ew=4)
             cols = slice(LAYER_BASE[lw], LAYER_BASE[lw] + LAYER_STEP[lw] + 1, LAYER_STEP[lw])
             rows = [
                 pixels[:, :, :, :, LAYER_BASE[lh] + LAYER_STEP[lh] * ph, :, cols].rearrange(
-                    "p j b eh ew pw -> p pw (b eh) ew j"
+                    "p j b eh ew pw -> p (b eh) ew pw j"
                 )
                 for ph in range(2)
             ]
-            nc.vector.tensor_copy(out=quarters[:, 0], in_=rows[0])
+            nc.vector.tensor_copy(out=halves[:, 0], in_=rows[0])
             for pw in range(2):
-                nc.scalar.copy(out=quarters[:, 1, pw], in_=rows[1][:, pw])
+                nc.scalar.copy(out=halves[:, 1, :, :, pw, :], in_=rows[1][:, :, :, pw, :])
 
         def key_pass(out, t, g, codes, planes):
             nc.tensor.matmul_mx(
@@ -269,14 +272,17 @@ def tile_afnb_pa_kernel(
                 key_pass(u_last[:, t, :], t, g, x_codes[:, g, n_layers - 1, :], x_planes[:, g, n_layers - 1, :])
             norm_relu(k_sums[:, 4, t, :], u_last[:, t, :], t)
 
+        bv_ps = psum.tile([P, CV], F32, tag="key_c")
+        nc.tensor.matmul(out=bv_ps[:], lhsT=ones[:], rhs=bias_rows[:], start=True, stop=True)
         coarse_ps = psum.tile([P, CV], F32, tag="key_b")
+        nc.tensor.matmul(out=coarse_ps[:], lhsT=ones[:], rhs=bias_rows[:], start=True, stop=False)
         for kind in range(KINDS):
             nc.scalar.copy(out=g_sb[kind][:], in_=v_kind[kind][:])
             nc.tensor.matmul(
                 out=coarse_ps[:],
                 lhsT=pool_mat[:, kind].rearrange("p b l -> p (b l)"),
                 rhs=g_sb[kind][:],
-                start=(kind == 0),
+                start=False,
                 stop=(kind == KINDS - 1),
             )
 
@@ -294,29 +300,23 @@ def tile_afnb_pa_kernel(
         add(nc, sum012[:], sum01[:], g_sb[2][:])
         k_three, k_four = pool_along_w(nc, work, "key", KEY_TILES, F32, k_sums[:, 1:3], k_sums[:, 3:5])
         add(nc, k_fine[:], k_three[:, 0], k_three[:, 1])
-        by_slot = k_fine[:].rearrange("c t (ph pw b eh ew) -> c t ph b eh ew pw", ph=2, pw=2, b=B, eh=4)
-        by_cell = key_sb[:, :, :, COARSE : COARSE + FINE].rearrange(
-            "c t b (eh ph ew pw) -> c t ph b eh ew pw", eh=4, ph=2, ew=4
+        nc.scalar.mul(
+            out=key_sb[:, :, :, COARSE : COARSE + FINE],
+            in_=k_fine[:].rearrange("c t (b n) -> c t b n", b=B),
+            mul=1.0 / 9.0,
         )
-        for ph in range(2):
-            nc.scalar.mul(out=by_cell[:, :, ph], in_=by_slot[:, :, ph], mul=1.0 / 9.0)
         k_s6 = pool_along_h(nc, work, "key", KEY_TILES, F32, k_four)
         add(nc, sum_all[:], sum012[:], g_sb[3][:])
         pool_coarser(nc, work, "key", KEY_TILES, k_s6, key_sb[:, :, :, 0:COARSE])
         for t in range(KEY_TILES):
-            nc.scalar.dma_start(out=out_1[:, P * t : P * (t + 1), :].rearrange("b c l -> c b l"), in_=key_sb[:, t])
+            nc.sync.dma_start(out=out_1[:, P * t : P * (t + 1), :].rearrange("b c l -> c b l"), in_=key_sb[:, t])
 
         nc.vector.scalar_tensor_tensor(
-            out=v_fine[:], in0=sum_all[:], scalar=1.0 / 9.0, in1=bv_all[:], op0=ALU.mult, op1=ALU.add
+            out=v_fine[:], in0=sum_all[:], scalar=1.0 / 9.0, in1=bv_ps[:], op0=ALU.mult, op1=ALU.add
         )
         for b in range(B):
-            cells = out_0[b, COARSE : COARSE + FINE, :].rearrange(
-                "(eh ph ew pw) c -> ph pw eh ew c", eh=4, ph=2, ew=4, pw=2
-            )
-            for ph in range(2):
-                for pw in range(2):
-                    first = 64 * ph + 32 * pw + 16 * b
-                    nc.sync.dma_start(out=cells[ph, pw], in_=v_fine[first : first + 16, :])
-        add(nc, v_coarse[:], coarse_ps[:], bv_all[:])
+            nc.sync.dma_start(out=out_0[b, COARSE : COARSE + FINE, :], in_=v_fine[FINE * b : FINE * (b + 1), :])
+        nc.scalar.copy(out=v_coarse[:], in_=coarse_ps[:])
         for b in range(B):
-            nc.sync.dma_start(out=out_0[b, 0:COARSE, :], in_=v_coarse[ROWS * b : ROWS * b + COARSE, :])
+            for first, last in ((0, 32), (32, COARSE)):
+                nc.sync.dma_start(out=out_0[b, first:last, :], in_=v_coarse[ROWS * b + first : ROWS * b + last, :])

@@ -34,6 +34,7 @@ WIDE = 4
 COARSE = 46
 FINE = 64
 ROWS = 64
+AHEAD = 2
 
 
 def kind_of(lh, lw):
@@ -77,7 +78,7 @@ def pool_along_h(nc, work, label, tiles, dtype, four):
     return s6
 
 
-def pool_coarser(nc, work, label, tiles, s6, coarse):
+def pool_coarser(nc, work, label, tiles, s6, coarse, scale):
     s3 = work.tile([P, tiles, B, 9], F32, name="%s_s3" % label)
     s1 = work.tile([P, tiles, B, 1], F32, name="%s_s1" % label)
     nc.vector.tensor_reduce(
@@ -92,9 +93,9 @@ def pool_coarser(nc, work, label, tiles, s6, coarse):
         axis=AXIS.X,
         op=ALU.add,
     )
-    nc.scalar.mul(out=coarse[:, :, :, 10:46], in_=s6[:], mul=1.0 / 16.0)
-    nc.scalar.mul(out=coarse[:, :, :, 1:10], in_=s3[:], mul=1.0 / 64.0)
-    nc.scalar.mul(out=coarse[:, :, :, 0:1], in_=s1[:], mul=1.0 / 576.0)
+    scale(coarse[:, :, :, 10:46], s6[:], 1.0 / 16.0)
+    scale(coarse[:, :, :, 1:10], s3[:], 1.0 / 64.0)
+    scale(coarse[:, :, :, 0:1], s1[:], 1.0 / 576.0)
 
 
 def tile_afnb_pa_kernel(
@@ -104,7 +105,7 @@ def tile_afnb_pa_kernel(
     with ExitStack() as ctx:
         keep = ctx.enter_context(tc.tile_pool(name="keep", bufs=1))
         work = ctx.enter_context(tc.tile_pool(name="work", bufs=1))
-        stage = ctx.enter_context(tc.tile_pool(name="stage", bufs=4))
+        stage = ctx.enter_context(tc.tile_pool(name="stage", bufs=AHEAD + 2))
         psum = ctx.enter_context(tc.psum_pool(name="psum", bufs=1))
         ctx.enter_context(tc.manual_schedule())
 
@@ -113,8 +114,10 @@ def tile_afnb_pa_kernel(
         wk_codes = keep.tile([P, PASSES, 2 * CK], U8, align_bytes=64)
         wv_codes = keep.tile([P, PASSES, 2 * CV], U8, align_bytes=64)
         raw = [keep.tile([P, PACK, B, PIX], BF16, name="raw%d" % g) for g in range(PASSES)]
+        ident = keep.tile([P, P], BF16)
         bias_rows = keep.tile([P, CV], BF16)
         ones = keep.tile([P, P], BF16)
+        make_identity(nc, ident[:])
         nc.gpsimd.memset(bias_rows[:], 0.0)
         nc.gpsimd.memset(ones[:], 1.0)
 
@@ -147,8 +150,28 @@ def tile_afnb_pa_kernel(
                 nc.sync.dma_start(out=tile_[:], in_=vec.rearrange("(t c) -> c t", c=P))
         nc.sync.dma_start(out=bias_rows[0:1, :], in_=bv.unsqueeze(0))
 
-        ident = keep.tile([P, P], BF16)
-        make_identity(nc, ident[:])
+        units = keep.tile([P, 2, 2, KINDS, SLOTS], BF16)
+        pool_mat = keep.tile([P, KINDS, B, ROWS], F32)
+        nc.vector.memset(units[:].bitcast(I32), 0)
+        nc.vector.memset(pool_mat[:], 0.0)
+        nc.vector.tensor_copy(
+            out=units[:].rearrange("c kw kh t s -> c (kw kh t) s")[:, 0 : 4 * KINDS : KINDS + 1, :],
+            in_=ident[:].unsqueeze(1).to_broadcast([P, KINDS, SLOTS]),
+        )
+        mat_three, mat_four = pool_along_w(nc, work, "mat", KINDS, BF16, units[:, 0], units[:, 1])
+        mat_s6 = pool_along_h(nc, work, "mat", KINDS, BF16, mat_four)
+        pool_coarser(
+            nc,
+            work,
+            "mat",
+            KINDS,
+            mat_s6,
+            pool_mat[:, :, :, 0:COARSE],
+            lambda out, in_, factor: nc.gpsimd.tensor_scalar(
+                out=out, in0=in_, scalar1=factor, scalar2=0.0, op0=ALU.mult, op1=ALU.add
+            ),
+        )
+
         bk_c, gk_c, bek_c, mk_c, vk_c = [tile_[:] for tile_ in vecs]
         minus_half = keep.tile([P, KEY_TILES], F32)
         var_eps = keep.tile([P, KEY_TILES], F32)
@@ -164,18 +187,6 @@ def tile_afnb_pa_kernel(
         nc.gpsimd.tensor_tensor(out=centred[:], in0=bk_c, in1=mk_c, op=ALU.subtract)
         nc.gpsimd.tensor_tensor(out=scaled[:], in0=centred[:], in1=bn_scale[:], op=ALU.mult)
         nc.gpsimd.tensor_tensor(out=bn_shift[:], in0=scaled[:], in1=bek_c, op=ALU.add)
-
-        units = keep.tile([P, 2, 2, KINDS, SLOTS], BF16)
-        pool_mat = keep.tile([P, KINDS, B, ROWS], F32)
-        nc.vector.memset(units[:].bitcast(I32), 0)
-        nc.vector.memset(pool_mat[:], 0.0)
-        nc.vector.tensor_copy(
-            out=units[:].rearrange("c kw kh t s -> c (kw kh t) s")[:, 0 : 4 * KINDS : KINDS + 1, :],
-            in_=ident[:].unsqueeze(1).to_broadcast([P, KINDS, SLOTS]),
-        )
-        mat_three, mat_four = pool_along_w(nc, work, "mat", KINDS, BF16, units[:, 0], units[:, 1])
-        mat_s6 = pool_along_h(nc, work, "mat", KINDS, BF16, mat_four)
-        pool_coarser(nc, work, "mat", KINDS, mat_s6, pool_mat[:, :, :, 0:COARSE])
 
         n_layers = len(LAYERS)
         x_codes = keep.tile([P, PASSES, n_layers, SLOTS], U32, align_bytes=64)
@@ -231,10 +242,11 @@ def tile_afnb_pa_kernel(
                     t,
                 )
 
-        regroup(*steps[0])
+        for step in steps[:AHEAD]:
+            regroup(*step)
         for i, (g, pos) in enumerate(steps):
-            if i + 1 < len(steps):
-                regroup(*steps[i + 1])
+            if i + AHEAD < len(steps):
+                regroup(*steps[i + AHEAD])
             nc.vector.quantize_mx(
                 out=x_codes[:, g, pos, :].bitcast(FP8X4),
                 scales=x_planes[:, g, pos, :],
@@ -287,7 +299,7 @@ def tile_afnb_pa_kernel(
             )
 
         sum01 = keep.tile([P, CV], F32)
-        sum012 = keep.tile([P, CV], F32)
+        sum23 = keep.tile([P, CV], F32)
         sum_all = keep.tile([P, CV], F32)
         v_fine = keep.tile([P, CV], F32)
         v_coarse = keep.tile([P, CV], F32)
@@ -295,9 +307,7 @@ def tile_afnb_pa_kernel(
         k_fine = keep.tile([P, KEY_TILES, SLOTS], F32)
         pairs = relu[:].rearrange("c (i two) t s -> c i two t s", two=2)
         add(nc, k_sums[:, 0:4], pairs[:, :, 0], pairs[:, :, 1])
-        add(nc, sum01[:], g_sb[0][:], g_sb[1][:])
         add(nc, k_sums[:, 1], k_sums[:, 0], k_sums[:, 1])
-        add(nc, sum012[:], sum01[:], g_sb[2][:])
         k_three, k_four = pool_along_w(nc, work, "key", KEY_TILES, F32, k_sums[:, 1:3], k_sums[:, 3:5])
         add(nc, k_fine[:], k_three[:, 0], k_three[:, 1])
         nc.scalar.mul(
@@ -306,8 +316,18 @@ def tile_afnb_pa_kernel(
             mul=1.0 / 9.0,
         )
         k_s6 = pool_along_h(nc, work, "key", KEY_TILES, F32, k_four)
-        add(nc, sum_all[:], sum012[:], g_sb[3][:])
-        pool_coarser(nc, work, "key", KEY_TILES, k_s6, key_sb[:, :, :, 0:COARSE])
+        pool_coarser(
+            nc,
+            work,
+            "key",
+            KEY_TILES,
+            k_s6,
+            key_sb[:, :, :, 0:COARSE],
+            lambda out, in_, factor: nc.scalar.mul(out=out, in_=in_, mul=factor),
+        )
+        nc.gpsimd.tensor_tensor(out=sum01[:], in0=g_sb[0][:], in1=g_sb[1][:], op=ALU.add)
+        nc.gpsimd.tensor_tensor(out=sum23[:], in0=g_sb[2][:], in1=g_sb[3][:], op=ALU.add)
+        nc.gpsimd.tensor_tensor(out=sum_all[:], in0=sum01[:], in1=sum23[:], op=ALU.add)
         for t in range(KEY_TILES):
             nc.sync.dma_start(out=out_1[:, P * t : P * (t + 1), :].rearrange("b c l -> c b l"), in_=key_sb[:, t])
 

@@ -34,7 +34,6 @@ WIDE = 4
 COARSE = 46
 FINE = 64
 ROWS = 64
-AHEAD = 2
 
 
 def kind_of(lh, lw):
@@ -78,7 +77,7 @@ def pool_along_h(nc, work, label, tiles, dtype, four):
     return s6
 
 
-def pool_coarser(nc, work, label, tiles, s6, coarse, scale):
+def pool_coarser(nc, work, label, tiles, s6, coarse):
     s3 = work.tile([P, tiles, B, 9], F32, name="%s_s3" % label)
     s1 = work.tile([P, tiles, B, 1], F32, name="%s_s1" % label)
     nc.vector.tensor_reduce(
@@ -93,9 +92,9 @@ def pool_coarser(nc, work, label, tiles, s6, coarse, scale):
         axis=AXIS.X,
         op=ALU.add,
     )
-    scale(coarse[:, :, :, 10:46], s6[:], 1.0 / 16.0)
-    scale(coarse[:, :, :, 1:10], s3[:], 1.0 / 64.0)
-    scale(coarse[:, :, :, 0:1], s1[:], 1.0 / 576.0)
+    nc.scalar.mul(out=coarse[:, :, :, 10:46], in_=s6[:], mul=1.0 / 16.0)
+    nc.scalar.mul(out=coarse[:, :, :, 1:10], in_=s3[:], mul=1.0 / 64.0)
+    nc.scalar.mul(out=coarse[:, :, :, 0:1], in_=s1[:], mul=1.0 / 576.0)
 
 
 def tile_afnb_pa_kernel(
@@ -105,7 +104,7 @@ def tile_afnb_pa_kernel(
     with ExitStack() as ctx:
         keep = ctx.enter_context(tc.tile_pool(name="keep", bufs=1))
         work = ctx.enter_context(tc.tile_pool(name="work", bufs=1))
-        stage = ctx.enter_context(tc.tile_pool(name="stage", bufs=AHEAD + 2))
+        stage = ctx.enter_context(tc.tile_pool(name="stage", bufs=4))
         psum = ctx.enter_context(tc.psum_pool(name="psum", bufs=1))
         ctx.enter_context(tc.manual_schedule())
 
@@ -150,28 +149,6 @@ def tile_afnb_pa_kernel(
                 nc.sync.dma_start(out=tile_[:], in_=vec.rearrange("(t c) -> c t", c=P))
         nc.sync.dma_start(out=bias_rows[0:1, :], in_=bv.unsqueeze(0))
 
-        units = keep.tile([P, 2, 2, KINDS, SLOTS], BF16)
-        pool_mat = keep.tile([P, KINDS, B, ROWS], F32)
-        nc.vector.memset(units[:].bitcast(I32), 0)
-        nc.vector.memset(pool_mat[:], 0.0)
-        nc.vector.tensor_copy(
-            out=units[:].rearrange("c kw kh t s -> c (kw kh t) s")[:, 0 : 4 * KINDS : KINDS + 1, :],
-            in_=ident[:].unsqueeze(1).to_broadcast([P, KINDS, SLOTS]),
-        )
-        mat_three, mat_four = pool_along_w(nc, work, "mat", KINDS, BF16, units[:, 0], units[:, 1])
-        mat_s6 = pool_along_h(nc, work, "mat", KINDS, BF16, mat_four)
-        pool_coarser(
-            nc,
-            work,
-            "mat",
-            KINDS,
-            mat_s6,
-            pool_mat[:, :, :, 0:COARSE],
-            lambda out, in_, factor: nc.gpsimd.tensor_scalar(
-                out=out, in0=in_, scalar1=factor, scalar2=0.0, op0=ALU.mult, op1=ALU.add
-            ),
-        )
-
         bk_c, gk_c, bek_c, mk_c, vk_c = [tile_[:] for tile_ in vecs]
         minus_half = keep.tile([P, KEY_TILES], F32)
         var_eps = keep.tile([P, KEY_TILES], F32)
@@ -187,6 +164,18 @@ def tile_afnb_pa_kernel(
         nc.gpsimd.tensor_tensor(out=centred[:], in0=bk_c, in1=mk_c, op=ALU.subtract)
         nc.gpsimd.tensor_tensor(out=scaled[:], in0=centred[:], in1=bn_scale[:], op=ALU.mult)
         nc.gpsimd.tensor_tensor(out=bn_shift[:], in0=scaled[:], in1=bek_c, op=ALU.add)
+
+        units = keep.tile([P, 2, 2, KINDS, SLOTS], BF16)
+        pool_mat = keep.tile([P, KINDS, B, ROWS], F32)
+        nc.vector.memset(units[:].bitcast(I32), 0)
+        nc.vector.memset(pool_mat[:], 0.0)
+        nc.vector.tensor_copy(
+            out=units[:].rearrange("c kw kh t s -> c (kw kh t) s")[:, 0 : 4 * KINDS : KINDS + 1, :],
+            in_=ident[:].unsqueeze(1).to_broadcast([P, KINDS, SLOTS]),
+        )
+        mat_three, mat_four = pool_along_w(nc, work, "mat", KINDS, BF16, units[:, 0], units[:, 1])
+        mat_s6 = pool_along_h(nc, work, "mat", KINDS, BF16, mat_four)
+        pool_coarser(nc, work, "mat", KINDS, mat_s6, pool_mat[:, :, :, 0:COARSE])
 
         n_layers = len(LAYERS)
         x_codes = keep.tile([P, PASSES, n_layers, SLOTS], U32, align_bytes=64)
@@ -242,11 +231,10 @@ def tile_afnb_pa_kernel(
                     t,
                 )
 
-        for step in steps[:AHEAD]:
-            regroup(*step)
+        regroup(*steps[0])
         for i, (g, pos) in enumerate(steps):
-            if i + AHEAD < len(steps):
-                regroup(*steps[i + AHEAD])
+            if i + 1 < len(steps):
+                regroup(*steps[i + 1])
             nc.vector.quantize_mx(
                 out=x_codes[:, g, pos, :].bitcast(FP8X4),
                 scales=x_planes[:, g, pos, :],
@@ -284,12 +272,13 @@ def tile_afnb_pa_kernel(
                 key_pass(u_last[:, t, :], t, g, x_codes[:, g, n_layers - 1, :], x_planes[:, g, n_layers - 1, :])
             norm_relu(k_sums[:, 4, t, :], u_last[:, t, :], t)
 
-        bv_ps = psum.tile([P, CV], F32, tag="key_c")
-        nc.tensor.matmul(out=bv_ps[:], lhsT=ones[:], rhs=bias_rows[:], start=True, stop=True)
         coarse_ps = psum.tile([P, CV], F32, tag="key_b")
         nc.tensor.matmul(out=coarse_ps[:], lhsT=ones[:], rhs=bias_rows[:], start=True, stop=False)
         for kind in range(KINDS):
-            nc.scalar.copy(out=g_sb[kind][:], in_=v_kind[kind][:])
+            if kind < KINDS // 2:
+                nc.vector.tensor_copy(out=g_sb[kind][:], in_=v_kind[kind][:])
+            else:
+                nc.scalar.copy(out=g_sb[kind][:], in_=v_kind[kind][:])
             nc.tensor.matmul(
                 out=coarse_ps[:],
                 lhsT=pool_mat[:, kind].rearrange("p b l -> p (b l)"),
@@ -297,14 +286,17 @@ def tile_afnb_pa_kernel(
                 start=False,
                 stop=(kind == KINDS - 1),
             )
+        bv_ps = psum.tile([P, CV], F32, tag="key_c")
+        nc.tensor.matmul(out=bv_ps[:], lhsT=ones[:], rhs=bias_rows[:], start=True, stop=True)
 
         sum01 = keep.tile([P, CV], F32)
-        sum23 = keep.tile([P, CV], F32)
+        sum012 = keep.tile([P, CV], F32)
         sum_all = keep.tile([P, CV], F32)
         v_fine = keep.tile([P, CV], F32)
         v_coarse = keep.tile([P, CV], F32)
         key_sb = keep.tile([P, KEY_TILES, B, COARSE + FINE], F32)
         k_fine = keep.tile([P, KEY_TILES, SLOTS], F32)
+        add(nc, sum01[:], g_sb[0][:], g_sb[1][:])
         pairs = relu[:].rearrange("c (i two) t s -> c i two t s", two=2)
         add(nc, k_sums[:, 0:4], pairs[:, :, 0], pairs[:, :, 1])
         add(nc, k_sums[:, 1], k_sums[:, 0], k_sums[:, 1])
@@ -315,28 +307,19 @@ def tile_afnb_pa_kernel(
             in_=k_fine[:].rearrange("c t (b n) -> c t b n", b=B),
             mul=1.0 / 9.0,
         )
+        add(nc, sum012[:], sum01[:], g_sb[2][:])
         k_s6 = pool_along_h(nc, work, "key", KEY_TILES, F32, k_four)
-        pool_coarser(
-            nc,
-            work,
-            "key",
-            KEY_TILES,
-            k_s6,
-            key_sb[:, :, :, 0:COARSE],
-            lambda out, in_, factor: nc.scalar.mul(out=out, in_=in_, mul=factor),
-        )
-        nc.gpsimd.tensor_tensor(out=sum01[:], in0=g_sb[0][:], in1=g_sb[1][:], op=ALU.add)
-        nc.gpsimd.tensor_tensor(out=sum23[:], in0=g_sb[2][:], in1=g_sb[3][:], op=ALU.add)
-        nc.gpsimd.tensor_tensor(out=sum_all[:], in0=sum01[:], in1=sum23[:], op=ALU.add)
+        add(nc, sum_all[:], sum012[:], g_sb[3][:])
+        pool_coarser(nc, work, "key", KEY_TILES, k_s6, key_sb[:, :, :, 0:COARSE])
+        nc.scalar.copy(out=v_coarse[:], in_=coarse_ps[:])
+        for b in range(B):
+            for first, last in ((0, 32), (32, COARSE)):
+                nc.sync.dma_start(out=out_0[b, first:last, :], in_=v_coarse[ROWS * b + first : ROWS * b + last, :])
         for t in range(KEY_TILES):
-            nc.sync.dma_start(out=out_1[:, P * t : P * (t + 1), :].rearrange("b c l -> c b l"), in_=key_sb[:, t])
+            nc.scalar.dma_start(out=out_1[:, P * t : P * (t + 1), :].rearrange("b c l -> c b l"), in_=key_sb[:, t])
 
         nc.vector.scalar_tensor_tensor(
             out=v_fine[:], in0=sum_all[:], scalar=1.0 / 9.0, in1=bv_ps[:], op0=ALU.mult, op1=ALU.add
         )
         for b in range(B):
             nc.sync.dma_start(out=out_0[b, COARSE : COARSE + FINE, :], in_=v_fine[FINE * b : FINE * (b + 1), :])
-        nc.scalar.copy(out=v_coarse[:], in_=coarse_ps[:])
-        for b in range(B):
-            for first, last in ((0, 32), (32, COARSE)):
-                nc.sync.dma_start(out=out_0[b, first:last, :], in_=v_coarse[ROWS * b + first : ROWS * b + last, :])

@@ -24,13 +24,16 @@ KEY_TILES = CK // P
 EPS = 1e-5
 FLOPS = 2 * B * PIX * CL * (CK + CV)
 
-LAYER_BASE = (0, 1, 2)
-LAYER_STEP = (4, 4, 1)
+OFFSETS = ((0, 5), (1, 4), (2, 3))
+EVEN_STEP = 1
 INNER = 2
 LAYERS = sorted([(lh, lw) for lh in range(3) for lw in range(3)], key=lambda hw: (hw[1] == INNER, hw[0] == INNER))
 KINDS = 4
 SLOTS = 128
 WIDE = 4
+GROUPS = (((0, 1), (1, 2), (2, 4), (4, 6), (6, 8), (8, 9)), ((0, 2), (2, 4), (4, 6), (6, 8), (8, 9)))
+WARM_UP = 4
+SCALAR_LAYERS = ((1, 0), (1, 1), (2, 1), (1, 2))
 COARSE = 46
 FINE = 64
 ROWS = 64
@@ -38,6 +41,15 @@ ROWS = 64
 
 def kind_of(lh, lw):
     return 2 * (lw == INNER) + (lh == INNER)
+
+
+def picks(layer, one_by_one):
+    if layer == EVEN_STEP:
+        return [(1, 0, False)]
+    first, second = OFFSETS[layer]
+    if one_by_one:
+        return [(first, 0, False), (second, 1, False)]
+    return [(slice(first, second + 1, second - first), slice(0, 2), True)]
 
 
 def add(nc, out, in0, in1):
@@ -104,7 +116,6 @@ def tile_afnb_pa_kernel(
     with ExitStack() as ctx:
         keep = ctx.enter_context(tc.tile_pool(name="keep", bufs=1))
         work = ctx.enter_context(tc.tile_pool(name="work", bufs=1))
-        stage = ctx.enter_context(tc.tile_pool(name="stage", bufs=4))
         psum = ctx.enter_context(tc.psum_pool(name="psum", bufs=1))
         ctx.enter_context(tc.manual_schedule())
 
@@ -116,9 +127,9 @@ def tile_afnb_pa_kernel(
         ident = keep.tile([P, P], BF16)
         bias_rows = keep.tile([P, CV], BF16)
         ones = keep.tile([P, P], BF16)
-        make_identity(nc, ident[:])
         nc.gpsimd.memset(bias_rows[:], 0.0)
         nc.gpsimd.memset(ones[:], 1.0)
+        make_identity(nc, ident[:])
 
         nc.vector.memset(wv_planes[:].bitcast(I32), 0)
         nc.vector.memset(wk_planes[:].bitcast(I32), 0)
@@ -130,24 +141,24 @@ def tile_afnb_pa_kernel(
                     in_=scales.bitcast(I32)[:, 4 * quad : 4 * quad + 4, :].rearrange("g r n -> r g n"),
                 )
 
-        def load_x(g):
+        def load_x(queue, g):
             for b in range(B):
-                nc.scalar.dma_start(
+                queue.dma_start(
                     out=raw[g][:, :, b, :],
                     in_=low_feats[b, g * K_PASS : (g + 1) * K_PASS].rearrange("(p j) h w -> p j (h w)", j=PACK),
                 )
 
+        load_x(nc.scalar, 0)
+        nc.sync.dma_start(out=bias_rows[0:1, :], in_=bv.unsqueeze(0))
         load_planes(wv_planes, wv_scales)
         nc.sync.dma_start(out=wv_codes[:].bitcast(I32), in_=wv_words.bitcast(I32).rearrange("g p n -> p g n"))
-        load_x(0)
+        load_x(nc.sync, 1)
         load_planes(wk_planes, wk_scales)
         nc.sync.dma_start(out=wk_codes[:].bitcast(I32), in_=wk_words.bitcast(I32).rearrange("g p n -> p g n"))
-        load_x(1)
         vecs = [keep.tile([P, KEY_TILES], BF16, name="vec%d" % i) for i in range(5)]
         with nc.allow_non_contiguous_dma(reason="five vectors of 256 values, one value a partition"):
             for tile_, vec in zip(vecs, (bk, gk, bek, mk, vk)):
                 nc.sync.dma_start(out=tile_[:], in_=vec.rearrange("(t c) -> c t", c=P))
-        nc.sync.dma_start(out=bias_rows[0:1, :], in_=bv.unsqueeze(0))
 
         bk_c, gk_c, bek_c, mk_c, vk_c = [tile_[:] for tile_ in vecs]
         minus_half = keep.tile([P, KEY_TILES], F32)
@@ -177,6 +188,14 @@ def tile_afnb_pa_kernel(
         mat_s6 = pool_along_h(nc, work, "mat", KINDS, BF16, mat_four)
         pool_coarser(nc, work, "mat", KINDS, mat_s6, pool_mat[:, :, :, 0:COARSE])
 
+        bias_ps = psum.tile([P, CV], F32, tag="key_d")
+        bias_sb = keep.tile([P, CV], F32)
+        nc.tensor.matmul(out=bias_ps[:], lhsT=ones[:], rhs=bias_rows[:], start=True, stop=True)
+        nc.scalar.copy(out=bias_sb[:], in_=bias_ps[:])
+        warm_ps = psum.tile([P, CV], F32, tag="key_c")
+        for i in range(WARM_UP):
+            nc.tensor.matmul(out=warm_ps[:], lhsT=ones[:], rhs=raw[0][:, 0, 0, 0:CV], start=True, stop=True)
+
         n_layers = len(LAYERS)
         x_codes = keep.tile([P, PASSES, n_layers, SLOTS], U32, align_bytes=64)
         x_planes = keep.tile([P, PASSES, n_layers, SLOTS], U8, align_bytes=64)
@@ -187,25 +206,38 @@ def tile_afnb_pa_kernel(
         k_sums = keep.tile([P, 5, KEY_TILES, SLOTS], F32)
         g_sb = [keep.tile([P, CV], F32, name="g_sb%d" % kind) for kind in range(KINDS)]
         kinds = [kind_of(lh, lw) for lh, lw in LAYERS]
-        steps = [(g, pos) for g in range(PASSES) for pos in range(n_layers)]
+        rounds = [(g, first, last) for g in range(PASSES) for first, last in GROUPS[g]]
         grouped = {}
 
-        def regroup(g, pos):
+        def regroup(copy, max_dims, g, pos, dst):
             lh, lw = LAYERS[pos]
-            pixels = raw[g][:].rearrange("p j b (eh sh ew sw) -> p j b eh sh ew sw", eh=4, sh=6, ew=4, sw=6)
-            tile_ = stage.tile([P, SLOTS, PACK], BF16, align_bytes=64, name="grouped")
-            grouped[(g, pos)] = tile_
-            halves = tile_[:].rearrange("p (m ph ew pw) j -> p ph m ew pw j", m=8, ph=2, ew=4)
-            cols = slice(LAYER_BASE[lw], LAYER_BASE[lw] + LAYER_STEP[lw] + 1, LAYER_STEP[lw])
-            rows = [
-                pixels[:, :, :, :, LAYER_BASE[lh] + LAYER_STEP[lh] * ph, :, cols].rearrange(
-                    "p j b eh ew pw -> p (b eh) ew pw j"
-                )
-                for ph in range(2)
-            ]
-            nc.vector.tensor_copy(out=halves[:, 0], in_=rows[0])
-            for pw in range(2):
-                nc.scalar.copy(out=halves[:, 1, :, :, pw, :], in_=rows[1][:, :, :, pw, :])
+            span_h = 3 if lh == EVEN_STEP else 6
+            span_w = 3 if lw == EVEN_STEP else 6
+            pixels = raw[g][:].rearrange(
+                "p j b (hb hs wb ws) -> p j b hb hs wb ws", hs=span_h, wb=SIDE // span_w, ws=span_w
+            )
+            slots = dst.rearrange(
+                "p (r ph c pw) j -> p r ph c pw j", ph=span_h // 3, c=SIDE // span_w, pw=span_w // 3
+            )
+            dims = 3 + (lh != EVEN_STEP) + (lw != EVEN_STEP)
+            split_h = lh != EVEN_STEP and dims > max_dims
+            split_w = lw != EVEN_STEP and dims - split_h > max_dims
+            for h_src, h_dst, h_dim in picks(lh, split_h):
+                for w_src, w_dst, w_dim in picks(lw, split_w):
+                    rest = (" ph" if h_dim else "") + " wb" + (" pw" if w_dim else "")
+                    copy(
+                        out=slots[:, :, h_dst, :, w_dst, :],
+                        in_=pixels[:, :, :, :, h_src, :, w_src].rearrange("p j b hb%s -> p (b hb)%s j" % (rest, rest)),
+                    )
+
+        def regroup_round(g, first, last):
+            tile_ = keep.tile([P, last - first, SLOTS, PACK], BF16, align_bytes=64, name="grouped%d%d" % (g, first))
+            grouped[(g, first)] = tile_
+            for pos in range(first, last):
+                if LAYERS[pos] in SCALAR_LAYERS:
+                    regroup(nc.scalar.copy, 3, g, pos, tile_[:, pos - first])
+                else:
+                    regroup(nc.vector.tensor_copy, 4, g, pos, tile_[:, pos - first])
 
         def key_pass(out, t, g, codes, planes):
             nc.tensor.matmul_mx(
@@ -231,27 +263,28 @@ def tile_afnb_pa_kernel(
                     t,
                 )
 
-        regroup(*steps[0])
-        for i, (g, pos) in enumerate(steps):
-            if i + 1 < len(steps):
-                regroup(*steps[i + 1])
+        regroup_round(*rounds[0])
+        for i, (g, first, last) in enumerate(rounds):
+            if i + 1 < len(rounds):
+                regroup_round(*rounds[i + 1])
             nc.vector.quantize_mx(
-                out=x_codes[:, g, pos, :].bitcast(FP8X4),
-                scales=x_planes[:, g, pos, :],
-                in_=grouped[(g, pos)][:].rearrange("p s j -> p (s j)"),
+                out=x_codes[:, g, first:last, :].rearrange("p l s -> p (l s)").bitcast(FP8X4),
+                scales=x_planes[:, g, first:last, :].rearrange("p l s -> p (l s)"),
+                in_=grouped[(g, first)][:].rearrange("p l s j -> p (l s j)"),
             )
-            kind = kinds[pos]
-            nc.tensor.matmul_mx(
-                out=v_kind[kind][:],
-                lhsT=x_codes[:, g, pos, :].bitcast(FP8X4),
-                lhsT_scale=x_planes[:, g, pos, :],
-                rhs=wv_codes[:, g, :].bitcast(FP4X4),
-                rhs_scale=wv_planes[:, g, :],
-                start=(g == 0 and pos == kinds.index(kind)),
-                stop=(g == PASSES - 1 and (pos + 1 == n_layers or kinds[pos + 1] != kind)),
-            )
-            if pos % WIDE == WIDE - 1:
-                q = pos // WIDE
+            for pos in range(first, last):
+                kind = kinds[pos]
+                nc.tensor.matmul_mx(
+                    out=v_kind[kind][:],
+                    lhsT=x_codes[:, g, pos, :].bitcast(FP8X4),
+                    lhsT_scale=x_planes[:, g, pos, :],
+                    rhs=wv_codes[:, g, :].bitcast(FP4X4),
+                    rhs_scale=wv_planes[:, g, :],
+                    start=(g == 0 and pos == kinds.index(kind)),
+                    stop=(g == PASSES - 1 and (pos + 1 == n_layers or kinds[pos + 1] != kind)),
+                )
+            if last % WIDE == 0:
+                q = last // WIDE - 1
                 for t in range(KEY_TILES):
                     if g == 0:
                         u_wide[(t, q)] = psum.tile([P, WIDE * SLOTS], F32, name="u_wide%d%d" % (t, q), tag=key_tags[t][q])
@@ -259,35 +292,33 @@ def tile_afnb_pa_kernel(
                         u_wide[(t, q)][:],
                         t,
                         g,
-                        x_codes[:, g, WIDE * q : WIDE * (q + 1), :].rearrange("p l s -> p (l s)"),
-                        x_planes[:, g, WIDE * q : WIDE * (q + 1), :].rearrange("p l s -> p (l s)"),
+                        x_codes[:, g, WIDE * q : last, :].rearrange("p l s -> p (l s)"),
+                        x_planes[:, g, WIDE * q : last, :].rearrange("p l s -> p (l s)"),
                     )
-            if g == PASSES - 1 and pos == 6:
+            if g == PASSES - 1 and first == 4:
                 relu_wide(0)
+                nc.scalar.copy(out=g_sb[0][:], in_=v_kind[0][:])
+            if g == PASSES - 1 and first == 6:
+                nc.scalar.copy(out=g_sb[1][:], in_=v_kind[1][:])
 
         relu_wide(1)
+        nc.scalar.copy(out=g_sb[2][:], in_=v_kind[2][:])
         u_last = psum.tile([P, KEY_TILES, SLOTS], F32, tag="key_a")
         for t in range(KEY_TILES):
             for g in range(PASSES):
                 key_pass(u_last[:, t, :], t, g, x_codes[:, g, n_layers - 1, :], x_planes[:, g, n_layers - 1, :])
             norm_relu(k_sums[:, 4, t, :], u_last[:, t, :], t)
 
+        nc.scalar.copy(out=g_sb[3][:], in_=v_kind[3][:])
         coarse_ps = psum.tile([P, CV], F32, tag="key_b")
-        nc.tensor.matmul(out=coarse_ps[:], lhsT=ones[:], rhs=bias_rows[:], start=True, stop=False)
         for kind in range(KINDS):
-            if kind < KINDS // 2:
-                nc.vector.tensor_copy(out=g_sb[kind][:], in_=v_kind[kind][:])
-            else:
-                nc.scalar.copy(out=g_sb[kind][:], in_=v_kind[kind][:])
             nc.tensor.matmul(
                 out=coarse_ps[:],
                 lhsT=pool_mat[:, kind].rearrange("p b l -> p (b l)"),
                 rhs=g_sb[kind][:],
-                start=False,
+                start=(kind == 0),
                 stop=(kind == KINDS - 1),
             )
-        bv_ps = psum.tile([P, CV], F32, tag="key_c")
-        nc.tensor.matmul(out=bv_ps[:], lhsT=ones[:], rhs=bias_rows[:], start=True, stop=True)
 
         sum01 = keep.tile([P, CV], F32)
         sum012 = keep.tile([P, CV], F32)
@@ -311,15 +342,15 @@ def tile_afnb_pa_kernel(
         k_s6 = pool_along_h(nc, work, "key", KEY_TILES, F32, k_four)
         add(nc, sum_all[:], sum012[:], g_sb[3][:])
         pool_coarser(nc, work, "key", KEY_TILES, k_s6, key_sb[:, :, :, 0:COARSE])
-        nc.scalar.copy(out=v_coarse[:], in_=coarse_ps[:])
-        for b in range(B):
-            for first, last in ((0, 32), (32, COARSE)):
-                nc.sync.dma_start(out=out_0[b, first:last, :], in_=v_coarse[ROWS * b + first : ROWS * b + last, :])
         for t in range(KEY_TILES):
             nc.scalar.dma_start(out=out_1[:, P * t : P * (t + 1), :].rearrange("b c l -> c b l"), in_=key_sb[:, t])
 
         nc.vector.scalar_tensor_tensor(
-            out=v_fine[:], in0=sum_all[:], scalar=1.0 / 9.0, in1=bv_ps[:], op0=ALU.mult, op1=ALU.add
+            out=v_fine[:], in0=sum_all[:], scalar=1.0 / 9.0, in1=bias_sb[:], op0=ALU.mult, op1=ALU.add
         )
         for b in range(B):
             nc.sync.dma_start(out=out_0[b, COARSE : COARSE + FINE, :], in_=v_fine[FINE * b : FINE * (b + 1), :])
+        add(nc, v_coarse[:], coarse_ps[:], bias_sb[:])
+        for b in range(B):
+            for first, last in ((0, 32), (32, COARSE)):
+                nc.sync.dma_start(out=out_0[b, first:last, :], in_=v_coarse[ROWS * b + first : ROWS * b + last, :])

@@ -89,7 +89,7 @@ def pool_along_h(nc, work, label, tiles, dtype, four):
     return s6
 
 
-def pool_coarser(nc, work, label, tiles, s6, coarse):
+def pool_coarser(nc, work, label, tiles, s6, coarse, unit):
     s3 = work.tile([P, tiles, B, 9], F32, name="%s_s3" % label)
     s1 = work.tile([P, tiles, B, 1], F32, name="%s_s1" % label)
     nc.vector.tensor_reduce(
@@ -104,9 +104,9 @@ def pool_coarser(nc, work, label, tiles, s6, coarse):
         axis=AXIS.X,
         op=ALU.add,
     )
-    nc.scalar.mul(out=coarse[:, :, :, 10:46], in_=s6[:], mul=1.0 / 16.0)
-    nc.scalar.mul(out=coarse[:, :, :, 1:10], in_=s3[:], mul=1.0 / 64.0)
-    nc.scalar.mul(out=coarse[:, :, :, 0:1], in_=s1[:], mul=1.0 / 576.0)
+    nc.scalar.mul(out=coarse[:, :, :, 10:46], in_=s6[:], mul=unit / 16.0)
+    nc.scalar.mul(out=coarse[:, :, :, 1:10], in_=s3[:], mul=unit / 64.0)
+    nc.scalar.mul(out=coarse[:, :, :, 0:1], in_=s1[:], mul=unit / 576.0)
 
 
 def tile_afnb_pa_kernel(
@@ -175,6 +175,10 @@ def tile_afnb_pa_kernel(
         nc.gpsimd.tensor_tensor(out=centred[:], in0=bk_c, in1=mk_c, op=ALU.subtract)
         nc.gpsimd.tensor_tensor(out=scaled[:], in0=centred[:], in1=bn_scale[:], op=ALU.mult)
         nc.gpsimd.tensor_tensor(out=bn_shift[:], in0=scaled[:], in1=bek_c, op=ALU.add)
+        scale_9th = keep.tile([P, KEY_TILES], F32)
+        shift_9th = keep.tile([P, KEY_TILES], F32)
+        nc.gpsimd.tensor_scalar(out=scale_9th[:], in0=bn_scale[:], scalar1=1.0 / 9.0, scalar2=0.0, op0=ALU.mult, op1=ALU.add)
+        nc.gpsimd.tensor_scalar(out=shift_9th[:], in0=bn_shift[:], scalar1=1.0 / 9.0, scalar2=0.0, op0=ALU.mult, op1=ALU.add)
 
         units = keep.tile([P, 2, 2, KINDS, SLOTS], BF16)
         pool_mat = keep.tile([P, KINDS, B, ROWS], F32)
@@ -186,7 +190,7 @@ def tile_afnb_pa_kernel(
         )
         mat_three, mat_four = pool_along_w(nc, work, "mat", KINDS, BF16, units[:, 0], units[:, 1])
         mat_s6 = pool_along_h(nc, work, "mat", KINDS, BF16, mat_four)
-        pool_coarser(nc, work, "mat", KINDS, mat_s6, pool_mat[:, :, :, 0:COARSE])
+        pool_coarser(nc, work, "mat", KINDS, mat_s6, pool_mat[:, :, :, 0:COARSE], 1.0)
 
         bias_ps = psum.tile([P, CV], F32, tag="key_d")
         bias_sb = keep.tile([P, CV], F32)
@@ -252,7 +256,7 @@ def tile_afnb_pa_kernel(
 
         def norm_relu(out, in_, t):
             nc.scalar.activation(
-                out=out, in_=in_, func=ACT.Relu, bias=bn_shift[:, t : t + 1], scale=bn_scale[:, t : t + 1]
+                out=out, in_=in_, func=ACT.Relu, bias=shift_9th[:, t : t + 1], scale=scale_9th[:, t : t + 1]
             )
 
         def relu_wide(q):
@@ -272,17 +276,6 @@ def tile_afnb_pa_kernel(
                 scales=x_planes[:, g, first:last, :].rearrange("p l s -> p (l s)"),
                 in_=grouped[(g, first)][:].rearrange("p l s j -> p (l s j)"),
             )
-            for pos in range(first, last):
-                kind = kinds[pos]
-                nc.tensor.matmul_mx(
-                    out=v_kind[kind][:],
-                    lhsT=x_codes[:, g, pos, :].bitcast(FP8X4),
-                    lhsT_scale=x_planes[:, g, pos, :],
-                    rhs=wv_codes[:, g, :].bitcast(FP4X4),
-                    rhs_scale=wv_planes[:, g, :],
-                    start=(g == 0 and pos == kinds.index(kind)),
-                    stop=(g == PASSES - 1 and (pos + 1 == n_layers or kinds[pos + 1] != kind)),
-                )
             if last % WIDE == 0:
                 q = last // WIDE - 1
                 for t in range(KEY_TILES):
@@ -295,62 +288,83 @@ def tile_afnb_pa_kernel(
                         x_codes[:, g, WIDE * q : last, :].rearrange("p l s -> p (l s)"),
                         x_planes[:, g, WIDE * q : last, :].rearrange("p l s -> p (l s)"),
                     )
+            for pos in range(first, last):
+                kind = kinds[pos]
+                nc.tensor.matmul_mx(
+                    out=v_kind[kind][:],
+                    lhsT=x_codes[:, g, pos, :].bitcast(FP8X4),
+                    lhsT_scale=x_planes[:, g, pos, :],
+                    rhs=wv_codes[:, g, :].bitcast(FP4X4),
+                    rhs_scale=wv_planes[:, g, :],
+                    start=(g == 0 and pos == kinds.index(kind)),
+                    stop=(g == PASSES - 1 and (pos + 1 == n_layers or kinds[pos + 1] != kind)),
+                )
             if g == PASSES - 1 and first == 4:
                 relu_wide(0)
                 nc.scalar.copy(out=g_sb[0][:], in_=v_kind[0][:])
-            if g == PASSES - 1 and first == 6:
-                nc.scalar.copy(out=g_sb[1][:], in_=v_kind[1][:])
 
-        relu_wide(1)
-        nc.scalar.copy(out=g_sb[2][:], in_=v_kind[2][:])
         u_last = psum.tile([P, KEY_TILES, SLOTS], F32, tag="key_a")
         for t in range(KEY_TILES):
             for g in range(PASSES):
                 key_pass(u_last[:, t, :], t, g, x_codes[:, g, n_layers - 1, :], x_planes[:, g, n_layers - 1, :])
-            norm_relu(k_sums[:, 4, t, :], u_last[:, t, :], t)
 
+        relu_wide(1)
+        nc.scalar.copy(out=g_sb[1][:], in_=v_kind[1][:])
+        for t in range(KEY_TILES):
+            norm_relu(k_sums[:, 4, t, :], u_last[:, t, :], t)
+        nc.scalar.copy(out=g_sb[2][:], in_=v_kind[2][:])
         nc.scalar.copy(out=g_sb[3][:], in_=v_kind[3][:])
+
         coarse_ps = psum.tile([P, CV], F32, tag="key_b")
+        nc.tensor.matmul(out=coarse_ps[:], lhsT=ones[:], rhs=bias_rows[:], start=True, stop=False)
         for kind in range(KINDS):
             nc.tensor.matmul(
                 out=coarse_ps[:],
                 lhsT=pool_mat[:, kind].rearrange("p b l -> p (b l)"),
                 rhs=g_sb[kind][:],
-                start=(kind == 0),
+                start=False,
                 stop=(kind == KINDS - 1),
             )
 
-        sum01 = keep.tile([P, CV], F32)
-        sum012 = keep.tile([P, CV], F32)
-        sum_all = keep.tile([P, CV], F32)
-        v_fine = keep.tile([P, CV], F32)
+        partial = [keep.tile([P, CV], F32, name="partial%d" % kind) for kind in range(KINDS)]
         v_coarse = keep.tile([P, CV], F32)
         key_sb = keep.tile([P, KEY_TILES, B, COARSE + FINE], F32)
-        k_fine = keep.tile([P, KEY_TILES, SLOTS], F32)
-        add(nc, sum01[:], g_sb[0][:], g_sb[1][:])
+
+        def add_kind(kind):
+            nc.vector.scalar_tensor_tensor(
+                out=partial[kind][:],
+                in0=v_kind[kind][:],
+                scalar=1.0 / 9.0,
+                in1=(partial[kind - 1][:] if kind else bias_sb[:]),
+                op0=ALU.mult,
+                op1=ALU.add,
+            )
+
+        def key_fine(t):
+            add(
+                nc,
+                key_sb[:, t, :, COARSE : COARSE + FINE],
+                k_three[:, 0, t].rearrange("c (b n) -> c b n", b=B),
+                k_three[:, 1, t].rearrange("c (b n) -> c b n", b=B),
+            )
+
         pairs = relu[:].rearrange("c (i two) t s -> c i two t s", two=2)
-        add(nc, k_sums[:, 0:4], pairs[:, :, 0], pairs[:, :, 1])
+        add_kind(0)
+        add(nc, k_sums[:, 0:2], pairs[:, 0:2, 0], pairs[:, 0:2, 1])
+        add_kind(1)
         add(nc, k_sums[:, 1], k_sums[:, 0], k_sums[:, 1])
+        add(nc, k_sums[:, 2:4], pairs[:, 2:4, 0], pairs[:, 2:4, 1])
+        add_kind(2)
         k_three, k_four = pool_along_w(nc, work, "key", KEY_TILES, F32, k_sums[:, 1:3], k_sums[:, 3:5])
-        add(nc, k_fine[:], k_three[:, 0], k_three[:, 1])
-        nc.scalar.mul(
-            out=key_sb[:, :, :, COARSE : COARSE + FINE],
-            in_=k_fine[:].rearrange("c t (b n) -> c t b n", b=B),
-            mul=1.0 / 9.0,
-        )
-        add(nc, sum012[:], sum01[:], g_sb[2][:])
+        key_fine(0)
         k_s6 = pool_along_h(nc, work, "key", KEY_TILES, F32, k_four)
-        add(nc, sum_all[:], sum012[:], g_sb[3][:])
-        pool_coarser(nc, work, "key", KEY_TILES, k_s6, key_sb[:, :, :, 0:COARSE])
+        key_fine(1)
+        pool_coarser(nc, work, "key", KEY_TILES, k_s6, key_sb[:, :, :, 0:COARSE], 9.0)
         for t in range(KEY_TILES):
             nc.scalar.dma_start(out=out_1[:, P * t : P * (t + 1), :].rearrange("b c l -> c b l"), in_=key_sb[:, t])
-
-        nc.vector.scalar_tensor_tensor(
-            out=v_fine[:], in0=sum_all[:], scalar=1.0 / 9.0, in1=bias_sb[:], op0=ALU.mult, op1=ALU.add
-        )
+        add_kind(3)
         for b in range(B):
-            nc.sync.dma_start(out=out_0[b, COARSE : COARSE + FINE, :], in_=v_fine[FINE * b : FINE * (b + 1), :])
-        add(nc, v_coarse[:], coarse_ps[:], bias_sb[:])
-        for b in range(B):
-            for first, last in ((0, 32), (32, COARSE)):
-                nc.sync.dma_start(out=out_0[b, first:last, :], in_=v_coarse[ROWS * b + first : ROWS * b + last, :])
+            nc.sync.dma_start(out=out_0[b, COARSE : COARSE + FINE, :], in_=partial[3][FINE * b : FINE * (b + 1), :])
+        nc.scalar.copy(out=v_coarse[:], in_=coarse_ps[:])
+        for b, queue in enumerate((nc.sync, nc.scalar)):
+            queue.dma_start(out=out_0[b, 0:COARSE, :], in_=v_coarse[ROWS * b : ROWS * b + COARSE, :])

@@ -367,4 +367,5 @@ def tile_afnb_pa_kernel(
             nc.sync.dma_start(out=out_0[b, COARSE : COARSE + FINE, :], in_=partial[3][FINE * b : FINE * (b + 1), :])
         nc.scalar.copy(out=v_coarse[:], in_=coarse_ps[:])
         for b, queue in enumerate((nc.sync, nc.scalar)):
-            queue.dma_start(out=out_0[b, 0:COARSE, :], in_=v_coarse[ROWS * b : ROWS * b + COARSE, :])
+            for first, last in ((32, COARSE), (0, 32)):
+                queue.dma_start(out=out_0[b, first:last, :], in_=v_coarse[ROWS * b + first : ROWS * b + last, :])

@@ -148,6 +148,10 @@ def tile_afnb_pa_kernel(
                     in_=low_feats[b, g * K_PASS : (g + 1) * K_PASS].rearrange("(p j) h w -> p j (h w)", j=PACK),
                 )
 
+        vecs = [keep.tile([P, KEY_TILES], BF16, name="vec%d" % i) for i in range(5)]
+        with nc.allow_non_contiguous_dma(reason="five vectors of 256 values, one value a partition"):
+            for tile_, vec in zip(vecs, (bk, gk, bek, mk, vk)):
+                nc.sync.dma_start(out=tile_[:], in_=vec.rearrange("(t c) -> c t", c=P))
         load_x(nc.scalar, 0)
         nc.sync.dma_start(out=bias_rows[0:1, :], in_=bv.unsqueeze(0))
         load_planes(wv_planes, wv_scales)
@@ -155,10 +159,6 @@ def tile_afnb_pa_kernel(
         load_x(nc.sync, 1)
         load_planes(wk_planes, wk_scales)
         nc.sync.dma_start(out=wk_codes[:].bitcast(I32), in_=wk_words.bitcast(I32).rearrange("g p n -> p g n"))
-        vecs = [keep.tile([P, KEY_TILES], BF16, name="vec%d" % i) for i in range(5)]
-        with nc.allow_non_contiguous_dma(reason="five vectors of 256 values, one value a partition"):
-            for tile_, vec in zip(vecs, (bk, gk, bek, mk, vk)):
-                nc.sync.dma_start(out=tile_[:], in_=vec.rearrange("(t c) -> c t", c=P))
 
         bk_c, gk_c, bek_c, mk_c, vk_c = [tile_[:] for tile_ in vecs]
         minus_half = keep.tile([P, KEY_TILES], F32)

@@ -89,7 +89,7 @@ def pool_along_h(nc, work, label, tiles, dtype, four):
     return s6
 
 
-def pool_coarser(nc, work, label, tiles, s6, coarse, unit):
+def coarser_sums(nc, work, label, tiles, s6):
     s3 = work.tile([P, tiles, B, 9], F32, name="%s_s3" % label)
     s1 = work.tile([P, tiles, B, 1], F32, name="%s_s1" % label)
     nc.vector.tensor_reduce(
@@ -104,6 +104,10 @@ def pool_coarser(nc, work, label, tiles, s6, coarse, unit):
         axis=AXIS.X,
         op=ALU.add,
     )
+    return s3, s1
+
+
+def coarse_means(nc, s6, s3, s1, coarse, unit):
     nc.scalar.mul(out=coarse[:, :, :, 10:46], in_=s6[:], mul=unit / 16.0)
     nc.scalar.mul(out=coarse[:, :, :, 1:10], in_=s3[:], mul=unit / 64.0)
     nc.scalar.mul(out=coarse[:, :, :, 0:1], in_=s1[:], mul=unit / 576.0)
@@ -123,7 +127,7 @@ def tile_afnb_pa_kernel(
         wv_planes = keep.tile([P, PASSES, CV], U8, align_bytes=64)
         wk_codes = keep.tile([P, PASSES, 2 * CK], U8, align_bytes=64)
         wv_codes = keep.tile([P, PASSES, 2 * CV], U8, align_bytes=64)
-        raw = [keep.tile([P, PACK, B, PIX], BF16, name="raw%d" % g) for g in range(PASSES)]
+        raw = [keep.tile([P, B, PACK, PIX], BF16, name="raw%d" % g) for g in range(PASSES)]
         ident = keep.tile([P, P], BF16)
         bias_rows = keep.tile([P, CV], BF16)
         ones = keep.tile([P, P], BF16)
@@ -144,8 +148,8 @@ def tile_afnb_pa_kernel(
         def load_x(queue, g):
             for b in range(B):
                 queue.dma_start(
-                    out=raw[g][:, :, b, :],
-                    in_=low_feats[b, g * K_PASS : (g + 1) * K_PASS].rearrange("(p j) h w -> p j (h w)", j=PACK),
+                    out=raw[g][:, b].rearrange("p j n -> p (j n)"),
+                    in_=low_feats[b, g * K_PASS : (g + 1) * K_PASS].rearrange("(p j) h w -> p (j h w)", j=PACK),
                 )
 
         vecs = [keep.tile([P, KEY_TILES], BF16, name="vec%d" % i) for i in range(5)]
@@ -180,22 +184,32 @@ def tile_afnb_pa_kernel(
         nc.gpsimd.tensor_scalar(out=scale_9th[:], in0=bn_scale[:], scalar1=1.0 / 9.0, scalar2=0.0, op0=ALU.mult, op1=ALU.add)
         nc.gpsimd.tensor_scalar(out=shift_9th[:], in0=bn_shift[:], scalar1=1.0 / 9.0, scalar2=0.0, op0=ALU.mult, op1=ALU.add)
 
-        units = keep.tile([P, 2, 2, KINDS, SLOTS], BF16)
         pool_mat = keep.tile([P, KINDS, B, ROWS], F32)
-        nc.vector.memset(units[:].bitcast(I32), 0)
+        mat_w = keep.tile([P, 2, 96], BF16)
+        mat_s6 = keep.tile([P, KINDS, B, 36], BF16)
         nc.vector.memset(pool_mat[:], 0.0)
-        nc.vector.tensor_copy(
-            out=units[:].rearrange("c kw kh t s -> c (kw kh t) s")[:, 0 : 4 * KINDS : KINDS + 1, :],
-            in_=ident[:].unsqueeze(1).to_broadcast([P, KINDS, SLOTS]),
-        )
-        mat_three, mat_four = pool_along_w(nc, work, "mat", KINDS, BF16, units[:, 0], units[:, 1])
-        mat_s6 = pool_along_h(nc, work, "mat", KINDS, BF16, mat_four)
-        pool_coarser(nc, work, "mat", KINDS, mat_s6, pool_mat[:, :, :, 0:COARSE], 1.0)
+        nc.vector.memset(mat_w[:], 0.0)
+        nc.vector.memset(mat_s6[:], 0.0)
+
+        def pool_matrix_sums():
+            cells = ident[:].rearrange("c (m a) -> c m a", a=4)
+            by_w = mat_w[:].rearrange("c kw (m k) -> c kw m k", k=3)
+            nc.vector.tensor_copy(out=by_w[:, 0, :, 0:3:2], in_=cells[:, :, 0:4:3])
+            add(nc, by_w[:, 0, :, 1], cells[:, :, 1], cells[:, :, 2])
+            add(nc, by_w[:, 1, :, 0:3:2], cells[:, :, 0:4:2], cells[:, :, 1:4:2])
+            rows = mat_w[:].rearrange("c kw (m a w) -> c kw m a w", a=4, w=6)
+            by_h = mat_s6[:].rearrange("c (kw kh) b (e k w) -> c kw kh (b e) k w", kh=2, k=3, w=6)
+            nc.vector.tensor_copy(out=by_h[:, :, 0, :, 0:3:2, :], in_=rows[:, :, :, 0:4:3, :])
+            add(nc, by_h[:, :, 0, :, 1, :], rows[:, :, :, 1, :], rows[:, :, :, 2, :])
+            for half in range(2):
+                add(nc, by_h[:, :, 1, :, 2 * half, :], rows[:, :, :, 2 * half, :], rows[:, :, :, 2 * half + 1, :])
+            return coarser_sums(nc, work, "mat", KINDS, mat_s6)
+
+        mat_s3, mat_s1 = pool_matrix_sums()
 
         bias_ps = psum.tile([P, CV], F32, tag="key_d")
         bias_sb = keep.tile([P, CV], F32)
         nc.tensor.matmul(out=bias_ps[:], lhsT=ones[:], rhs=bias_rows[:], start=True, stop=True)
-        nc.scalar.copy(out=bias_sb[:], in_=bias_ps[:])
         warm_ps = psum.tile([P, CV], F32, tag="key_c")
         for i in range(WARM_UP):
             nc.tensor.matmul(out=warm_ps[:], lhsT=ones[:], rhs=raw[0][:, 0, 0, 0:CV], start=True, stop=True)
@@ -213,12 +227,20 @@ def tile_afnb_pa_kernel(
         rounds = [(g, first, last) for g in range(PASSES) for first, last in GROUPS[g]]
         grouped = {}
 
-        def regroup(copy, max_dims, g, pos, dst):
+        round_start = [dict((pos, first) for first, last in GROUPS[g] for pos in range(first, last)) for g in range(PASSES)]
+        for g, first, last in rounds:
+            grouped[(g, first)] = keep.tile(
+                [P, last - first, SLOTS, PACK], BF16, align_bytes=64, name="grouped%d%d" % (g, first)
+            )
+
+        def regroup(copy, max_dims, g, b, pos):
             lh, lw = LAYERS[pos]
+            first = round_start[g][pos]
+            dst = grouped[(g, first)][:, pos - first, FINE * b : FINE * (b + 1), :]
             span_h = 3 if lh == EVEN_STEP else 6
             span_w = 3 if lw == EVEN_STEP else 6
-            pixels = raw[g][:].rearrange(
-                "p j b (hb hs wb ws) -> p j b hb hs wb ws", hs=span_h, wb=SIDE // span_w, ws=span_w
+            pixels = raw[g][:, b].rearrange(
+                "p j (hb hs wb ws) -> p j hb hs wb ws", hs=span_h, wb=SIDE // span_w, ws=span_w
             )
             slots = dst.rearrange(
                 "p (r ph c pw) j -> p r ph c pw j", ph=span_h // 3, c=SIDE // span_w, pw=span_w // 3
@@ -231,17 +253,20 @@ def tile_afnb_pa_kernel(
                     rest = (" ph" if h_dim else "") + " wb" + (" pw" if w_dim else "")
                     copy(
                         out=slots[:, :, h_dst, :, w_dst, :],
-                        in_=pixels[:, :, :, :, h_src, :, w_src].rearrange("p j b hb%s -> p (b hb)%s j" % (rest, rest)),
+                        in_=pixels[:, :, :, h_src, :, w_src].rearrange("p j hb%s -> p hb%s j" % (rest, rest)),
                     )
 
-        def regroup_round(g, first, last):
-            tile_ = keep.tile([P, last - first, SLOTS, PACK], BF16, align_bytes=64, name="grouped%d%d" % (g, first))
-            grouped[(g, first)] = tile_
+        def regroup_layers(g, b, first, last):
             for pos in range(first, last):
                 if LAYERS[pos] in SCALAR_LAYERS:
-                    regroup(nc.scalar.copy, 3, g, pos, tile_[:, pos - first])
+                    regroup(nc.scalar.copy, 3, g, b, pos)
                 else:
-                    regroup(nc.vector.tensor_copy, 4, g, pos, tile_[:, pos - first])
+                    regroup(nc.vector.tensor_copy, 4, g, b, pos)
+
+        def regroup_round(g, first, last):
+            if first == 0:
+                regroup_layers(g, 0, 0, n_layers)
+            regroup_layers(g, 1, first, last)
 
         def key_pass(out, t, g, codes, planes):
             nc.tensor.matmul_mx(
@@ -268,6 +293,8 @@ def tile_afnb_pa_kernel(
                 )
 
         regroup_round(*rounds[0])
+        coarse_means(nc, mat_s6, mat_s3, mat_s1, pool_mat[:, :, :, 0:COARSE], 1.0)
+        nc.scalar.copy(out=bias_sb[:], in_=bias_ps[:])
         for i, (g, first, last) in enumerate(rounds):
             if i + 1 < len(rounds):
                 regroup_round(*rounds[i + 1])
@@ -359,7 +386,8 @@ def tile_afnb_pa_kernel(
         key_fine(0)
         k_s6 = pool_along_h(nc, work, "key", KEY_TILES, F32, k_four)
         key_fine(1)
-        pool_coarser(nc, work, "key", KEY_TILES, k_s6, key_sb[:, :, :, 0:COARSE], 9.0)
+        k_s3, k_s1 = coarser_sums(nc, work, "key", KEY_TILES, k_s6)
+        coarse_means(nc, k_s6, k_s3, k_s1, key_sb[:, :, :, 0:COARSE], 9.0)
         for t in range(KEY_TILES):
             nc.scalar.dma_start(out=out_1[:, P * t : P * (t + 1), :].rearrange("b c l -> c b l"), in_=key_sb[:, t])
         add_kind(3)

@@ -166,23 +166,21 @@ def tile_afnb_pa_kernel(
 
         bk_c, gk_c, bek_c, mk_c, vk_c = [tile_[:] for tile_ in vecs]
         minus_half = keep.tile([P, KEY_TILES], F32)
-        var_eps = keep.tile([P, KEY_TILES], F32)
-        rstd = keep.tile([P, KEY_TILES], F32)
-        bn_scale = keep.tile([P, KEY_TILES], F32)
+        var_81 = keep.tile([P, KEY_TILES], F32)
+        rstd_9th = keep.tile([P, KEY_TILES], F32)
         centred = keep.tile([P, KEY_TILES], F32)
+        bek_9th = keep.tile([P, KEY_TILES], F32)
         scaled = keep.tile([P, KEY_TILES], F32)
-        bn_shift = keep.tile([P, KEY_TILES], F32)
-        nc.gpsimd.memset(minus_half[:], -0.5)
-        nc.gpsimd.tensor_scalar(out=var_eps[:], in0=vk_c, scalar1=1.0, scalar2=EPS, op0=ALU.mult, op1=ALU.add)
-        nc.gpsimd.tensor_tensor(out=rstd[:], in0=var_eps[:], in1=minus_half[:], op=ALU.pow)
-        nc.gpsimd.tensor_tensor(out=bn_scale[:], in0=gk_c, in1=rstd[:], op=ALU.mult)
-        nc.gpsimd.tensor_tensor(out=centred[:], in0=bk_c, in1=mk_c, op=ALU.subtract)
-        nc.gpsimd.tensor_tensor(out=scaled[:], in0=centred[:], in1=bn_scale[:], op=ALU.mult)
-        nc.gpsimd.tensor_tensor(out=bn_shift[:], in0=scaled[:], in1=bek_c, op=ALU.add)
         scale_9th = keep.tile([P, KEY_TILES], F32)
         shift_9th = keep.tile([P, KEY_TILES], F32)
-        nc.gpsimd.tensor_scalar(out=scale_9th[:], in0=bn_scale[:], scalar1=1.0 / 9.0, scalar2=0.0, op0=ALU.mult, op1=ALU.add)
-        nc.gpsimd.tensor_scalar(out=shift_9th[:], in0=bn_shift[:], scalar1=1.0 / 9.0, scalar2=0.0, op0=ALU.mult, op1=ALU.add)
+        nc.gpsimd.memset(minus_half[:], -0.5)
+        nc.gpsimd.tensor_scalar(out=var_81[:], in0=vk_c, scalar1=81.0, scalar2=81.0 * EPS, op0=ALU.mult, op1=ALU.add)
+        nc.gpsimd.tensor_tensor(out=rstd_9th[:], in0=var_81[:], in1=minus_half[:], op=ALU.pow)
+        nc.gpsimd.tensor_tensor(out=scale_9th[:], in0=gk_c, in1=rstd_9th[:], op=ALU.mult)
+        nc.gpsimd.tensor_tensor(out=centred[:], in0=bk_c, in1=mk_c, op=ALU.subtract)
+        nc.gpsimd.tensor_tensor(out=scaled[:], in0=centred[:], in1=scale_9th[:], op=ALU.mult)
+        nc.gpsimd.tensor_scalar(out=bek_9th[:], in0=bek_c, scalar1=1.0 / 9.0, scalar2=0.0, op0=ALU.mult, op1=ALU.add)
+        nc.gpsimd.tensor_tensor(out=shift_9th[:], in0=scaled[:], in1=bek_9th[:], op=ALU.add)
 
         pool_mat = keep.tile([P, KINDS, B, ROWS], F32)
         mat_w = keep.tile([P, 2, 96], BF16)
@@ -279,6 +277,30 @@ def tile_afnb_pa_kernel(
                 stop=(g == PASSES - 1),
             )
 
+        def key_passes(g, q):
+            for t in range(KEY_TILES):
+                if g == 0:
+                    u_wide[(t, q)] = psum.tile([P, WIDE * SLOTS], F32, name="u_wide%d%d" % (t, q), tag=key_tags[t][q])
+                key_pass(
+                    u_wide[(t, q)][:],
+                    t,
+                    g,
+                    x_codes[:, g, WIDE * q : WIDE * (q + 1), :].rearrange("p l s -> p (l s)"),
+                    x_planes[:, g, WIDE * q : WIDE * (q + 1), :].rearrange("p l s -> p (l s)"),
+                )
+
+        def value_pass(g, pos):
+            kind = kinds[pos]
+            nc.tensor.matmul_mx(
+                out=v_kind[kind][:],
+                lhsT=x_codes[:, g, pos, :].bitcast(FP8X4),
+                lhsT_scale=x_planes[:, g, pos, :],
+                rhs=wv_codes[:, g, :].bitcast(FP4X4),
+                rhs_scale=wv_planes[:, g, :],
+                start=(g == 0 and pos == kinds.index(kind)),
+                stop=(g == PASSES - 1 and (pos + 1 == n_layers or kinds[pos + 1] != kind)),
+            )
+
         def norm_relu(out, in_, t):
             nc.scalar.activation(
                 out=out, in_=in_, func=ACT.Relu, bias=shift_9th[:, t : t + 1], scale=scale_9th[:, t : t + 1]
@@ -303,29 +325,14 @@ def tile_afnb_pa_kernel(
                 scales=x_planes[:, g, first:last, :].rearrange("p l s -> p (l s)"),
                 in_=grouped[(g, first)][:].rearrange("p l s j -> p (l s j)"),
             )
-            if last % WIDE == 0:
-                q = last // WIDE - 1
-                for t in range(KEY_TILES):
-                    if g == 0:
-                        u_wide[(t, q)] = psum.tile([P, WIDE * SLOTS], F32, name="u_wide%d%d" % (t, q), tag=key_tags[t][q])
-                    key_pass(
-                        u_wide[(t, q)][:],
-                        t,
-                        g,
-                        x_codes[:, g, WIDE * q : last, :].rearrange("p l s -> p (l s)"),
-                        x_planes[:, g, WIDE * q : last, :].rearrange("p l s -> p (l s)"),
-                    )
+            if g == PASSES - 1 and last % WIDE == 0:
+                key_passes(g, last // WIDE - 1)
             for pos in range(first, last):
-                kind = kinds[pos]
-                nc.tensor.matmul_mx(
-                    out=v_kind[kind][:],
-                    lhsT=x_codes[:, g, pos, :].bitcast(FP8X4),
-                    lhsT_scale=x_planes[:, g, pos, :],
-                    rhs=wv_codes[:, g, :].bitcast(FP4X4),
-                    rhs_scale=wv_planes[:, g, :],
-                    start=(g == 0 and pos == kinds.index(kind)),
-                    stop=(g == PASSES - 1 and (pos + 1 == n_layers or kinds[pos + 1] != kind)),
-                )
+                if g == 0 or kinds[pos] == 0:
+                    value_pass(g, pos)
+            if g == 0 and last == n_layers:
+                for q in range(2):
+                    key_passes(g, q)
             if g == PASSES - 1 and first == 4:
                 relu_wide(0)
                 nc.scalar.copy(out=g_sb[0][:], in_=v_kind[0][:])
@@ -336,11 +343,14 @@ def tile_afnb_pa_kernel(
                 key_pass(u_last[:, t, :], t, g, x_codes[:, g, n_layers - 1, :], x_planes[:, g, n_layers - 1, :])
 
         relu_wide(1)
-        nc.scalar.copy(out=g_sb[1][:], in_=v_kind[1][:])
         for t in range(KEY_TILES):
             norm_relu(k_sums[:, 4, t, :], u_last[:, t, :], t)
-        nc.scalar.copy(out=g_sb[2][:], in_=v_kind[2][:])
-        nc.scalar.copy(out=g_sb[3][:], in_=v_kind[3][:])
+
+        for pos in range(n_layers):
+            if kinds[pos] != 0:
+                value_pass(PASSES - 1, pos)
+        for kind in range(1, KINDS):
+            nc.scalar.copy(out=g_sb[kind][:], in_=v_kind[kind][:])
 
         coarse_ps = psum.tile([P, CV], F32, tag="key_b")
         nc.tensor.matmul(out=coarse_ps[:], lhsT=ones[:], rhs=bias_rows[:], start=True, stop=False)
@@ -376,12 +386,10 @@ def tile_afnb_pa_kernel(
             )
 
         pairs = relu[:].rearrange("c (i two) t s -> c i two t s", two=2)
-        add_kind(0)
         add(nc, k_sums[:, 0:2], pairs[:, 0:2, 0], pairs[:, 0:2, 1])
-        add_kind(1)
+        add_kind(0)
         add(nc, k_sums[:, 1], k_sums[:, 0], k_sums[:, 1])
         add(nc, k_sums[:, 2:4], pairs[:, 2:4, 0], pairs[:, 2:4, 1])
-        add_kind(2)
         k_three, k_four = pool_along_w(nc, work, "key", KEY_TILES, F32, k_sums[:, 1:3], k_sums[:, 3:5])
         key_fine(0)
         k_s6 = pool_along_h(nc, work, "key", KEY_TILES, F32, k_four)
@@ -390,7 +398,8 @@ def tile_afnb_pa_kernel(
         coarse_means(nc, k_s6, k_s3, k_s1, key_sb[:, :, :, 0:COARSE], 9.0)
         for t in range(KEY_TILES):
             nc.scalar.dma_start(out=out_1[:, P * t : P * (t + 1), :].rearrange("b c l -> c b l"), in_=key_sb[:, t])
-        add_kind(3)
+        for kind in range(1, KINDS):
+            add_kind(kind)
         for b in range(B):
             nc.sync.dma_start(out=out_0[b, COARSE : COARSE + FINE, :], in_=partial[3][FINE * b : FINE * (b + 1), :])
         nc.scalar.copy(out=v_coarse[:], in_=coarse_ps[:])

@@ -33,7 +33,7 @@ SLOTS = 128
 WIDE = 4
 GROUPS = (((0, 1), (1, 2), (2, 4), (4, 6), (6, 8), (8, 9)), ((0, 2), (2, 4), (4, 6), (6, 8), (8, 9)))
 WARM_UP = 4
-SCALAR_LAYERS = ((1, 0), (1, 1), (2, 1), (1, 2))
+SCALAR_LAYERS = ((0, 1), (1, 0), (1, 1), (2, 1), (1, 2))
 COARSE = 46
 FINE = 64
 ROWS = 64
@@ -138,49 +138,35 @@ def tile_afnb_pa_kernel(
         nc.vector.memset(wv_planes[:].bitcast(I32), 0)
         nc.vector.memset(wk_planes[:].bitcast(I32), 0)
 
-        def load_planes(planes, scales):
+        def load_planes(queue, planes, scales):
             for quad in range(4):
-                nc.sync.dma_start(
+                queue.dma_start(
                     out=planes[32 * quad : 32 * quad + 4].bitcast(I32),
                     in_=scales.bitcast(I32)[:, 4 * quad : 4 * quad + 4, :].rearrange("g r n -> r g n"),
                 )
 
+        def load_x_batch(queue, g, b):
+            queue.dma_start(
+                out=raw[g][:, b].rearrange("p j n -> p (j n)"),
+                in_=low_feats[b, g * K_PASS : (g + 1) * K_PASS].rearrange("(p j) h w -> p (j h w)", j=PACK),
+            )
+
         def load_x(queue, g):
             for b in range(B):
-                queue.dma_start(
-                    out=raw[g][:, b].rearrange("p j n -> p (j n)"),
-                    in_=low_feats[b, g * K_PASS : (g + 1) * K_PASS].rearrange("(p j) h w -> p (j h w)", j=PACK),
-                )
+                load_x_batch(queue, g, b)
 
         vecs = [keep.tile([P, KEY_TILES], BF16, name="vec%d" % i) for i in range(5)]
+        load_x(nc.sync, 0)
+        nc.scalar.dma_start(out=bias_rows[0:1, :], in_=bv.unsqueeze(0))
+        load_planes(nc.scalar, wv_planes, wv_scales)
+        nc.sync.dma_start(out=wv_codes[:].bitcast(I32), in_=wv_words.bitcast(I32).rearrange("g p n -> p g n"))
+        load_x_batch(nc.sync, 1, 0)
         with nc.allow_non_contiguous_dma(reason="five vectors of 256 values, one value a partition"):
             for tile_, vec in zip(vecs, (bk, gk, bek, mk, vk)):
                 nc.sync.dma_start(out=tile_[:], in_=vec.rearrange("(t c) -> c t", c=P))
-        load_x(nc.scalar, 0)
-        nc.sync.dma_start(out=bias_rows[0:1, :], in_=bv.unsqueeze(0))
-        load_planes(wv_planes, wv_scales)
-        nc.sync.dma_start(out=wv_codes[:].bitcast(I32), in_=wv_words.bitcast(I32).rearrange("g p n -> p g n"))
-        load_x(nc.sync, 1)
-        load_planes(wk_planes, wk_scales)
+        load_x_batch(nc.sync, 1, 1)
+        load_planes(nc.sync, wk_planes, wk_scales)
         nc.sync.dma_start(out=wk_codes[:].bitcast(I32), in_=wk_words.bitcast(I32).rearrange("g p n -> p g n"))
-
-        bk_c, gk_c, bek_c, mk_c, vk_c = [tile_[:] for tile_ in vecs]
-        minus_half = keep.tile([P, KEY_TILES], F32)
-        var_81 = keep.tile([P, KEY_TILES], F32)
-        rstd_9th = keep.tile([P, KEY_TILES], F32)
-        centred = keep.tile([P, KEY_TILES], F32)
-        bek_9th = keep.tile([P, KEY_TILES], F32)
-        scaled = keep.tile([P, KEY_TILES], F32)
-        scale_9th = keep.tile([P, KEY_TILES], F32)
-        shift_9th = keep.tile([P, KEY_TILES], F32)
-        nc.gpsimd.memset(minus_half[:], -0.5)
-        nc.gpsimd.tensor_scalar(out=var_81[:], in0=vk_c, scalar1=81.0, scalar2=81.0 * EPS, op0=ALU.mult, op1=ALU.add)
-        nc.gpsimd.tensor_tensor(out=rstd_9th[:], in0=var_81[:], in1=minus_half[:], op=ALU.pow)
-        nc.gpsimd.tensor_tensor(out=scale_9th[:], in0=gk_c, in1=rstd_9th[:], op=ALU.mult)
-        nc.gpsimd.tensor_tensor(out=centred[:], in0=bk_c, in1=mk_c, op=ALU.subtract)
-        nc.gpsimd.tensor_tensor(out=scaled[:], in0=centred[:], in1=scale_9th[:], op=ALU.mult)
-        nc.gpsimd.tensor_scalar(out=bek_9th[:], in0=bek_c, scalar1=1.0 / 9.0, scalar2=0.0, op0=ALU.mult, op1=ALU.add)
-        nc.gpsimd.tensor_tensor(out=shift_9th[:], in0=scaled[:], in1=bek_9th[:], op=ALU.add)
 
         pool_mat = keep.tile([P, KINDS, B, ROWS], F32)
         mat_w = keep.tile([P, 2, 96], BF16)
@@ -204,13 +190,35 @@ def tile_afnb_pa_kernel(
             return coarser_sums(nc, work, "mat", KINDS, mat_s6)
 
         mat_s3, mat_s1 = pool_matrix_sums()
+        for first, last, sums, mean in ((10, 46, mat_s6, 1.0 / 16.0), (1, 10, mat_s3, 1.0 / 64.0), (0, 1, mat_s1, 1.0 / 576.0)):
+            nc.gpsimd.tensor_scalar(
+                out=pool_mat[:, :, :, first:last], in0=sums[:], scalar1=mean, scalar2=0.0, op0=ALU.mult, op1=ALU.add
+            )
+
+        bk_c, gk_c, bek_c, mk_c, vk_c = [tile_[:] for tile_ in vecs]
+        minus_half = keep.tile([P, KEY_TILES], F32)
+        var_81 = keep.tile([P, KEY_TILES], F32)
+        rstd_9th = keep.tile([P, KEY_TILES], F32)
+        centred = keep.tile([P, KEY_TILES], F32)
+        bek_9th = keep.tile([P, KEY_TILES], F32)
+        scaled = keep.tile([P, KEY_TILES], F32)
+        scale_9th = keep.tile([P, KEY_TILES], F32)
+        shift_9th = keep.tile([P, KEY_TILES], F32)
+        nc.gpsimd.memset(minus_half[:], -0.5)
+        nc.gpsimd.tensor_scalar(out=var_81[:], in0=vk_c, scalar1=81.0, scalar2=81.0 * EPS, op0=ALU.mult, op1=ALU.add)
+        nc.gpsimd.tensor_tensor(out=rstd_9th[:], in0=var_81[:], in1=minus_half[:], op=ALU.pow)
+        nc.gpsimd.tensor_tensor(out=scale_9th[:], in0=gk_c, in1=rstd_9th[:], op=ALU.mult)
+        nc.gpsimd.tensor_tensor(out=centred[:], in0=bk_c, in1=mk_c, op=ALU.subtract)
+        nc.gpsimd.tensor_tensor(out=scaled[:], in0=centred[:], in1=scale_9th[:], op=ALU.mult)
+        nc.gpsimd.tensor_scalar(out=bek_9th[:], in0=bek_c, scalar1=1.0 / 9.0, scalar2=0.0, op0=ALU.mult, op1=ALU.add)
+        nc.gpsimd.tensor_tensor(out=shift_9th[:], in0=scaled[:], in1=bek_9th[:], op=ALU.add)
 
         bias_ps = psum.tile([P, CV], F32, tag="key_d")
         bias_sb = keep.tile([P, CV], F32)
-        nc.tensor.matmul(out=bias_ps[:], lhsT=ones[:], rhs=bias_rows[:], start=True, stop=True)
         warm_ps = psum.tile([P, CV], F32, tag="key_c")
         for i in range(WARM_UP):
             nc.tensor.matmul(out=warm_ps[:], lhsT=ones[:], rhs=raw[0][:, 0, 0, 0:CV], start=True, stop=True)
+        nc.tensor.matmul(out=bias_ps[:], lhsT=ones[:], rhs=bias_rows[:], start=True, stop=True)
 
         n_layers = len(LAYERS)
         x_codes = keep.tile([P, PASSES, n_layers, SLOTS], U32, align_bytes=64)
@@ -315,11 +323,11 @@ def tile_afnb_pa_kernel(
                 )
 
         regroup_round(*rounds[0])
-        coarse_means(nc, mat_s6, mat_s3, mat_s1, pool_mat[:, :, :, 0:COARSE], 1.0)
-        nc.scalar.copy(out=bias_sb[:], in_=bias_ps[:])
         for i, (g, first, last) in enumerate(rounds):
             if i + 1 < len(rounds):
                 regroup_round(*rounds[i + 1])
+            if (g, last) == (0, 8):
+                nc.scalar.copy(out=bias_sb[:], in_=bias_ps[:])
             nc.vector.quantize_mx(
                 out=x_codes[:, g, first:last, :].rearrange("p l s -> p (l s)").bitcast(FP8X4),
                 scales=x_planes[:, g, first:last, :].rearrange("p l s -> p (l s)"),

@@ -30,10 +30,11 @@ INNER = 2
 LAYERS = sorted([(lh, lw) for lh in range(3) for lw in range(3)], key=lambda hw: (hw[1] == INNER, hw[0] == INNER))
 KINDS = 4
 SLOTS = 128
+CELL_ROWS = 16
 WIDE = 4
 GROUPS = (((0, 1), (1, 2), (2, 4), (4, 6), (6, 8), (8, 9)), ((0, 2), (2, 4), (4, 6), (6, 8), (8, 9)))
 WARM_UP = 4
-SCALAR_LAYERS = ((0, 1), (1, 0), (1, 1), (2, 1), (1, 2))
+SCALAR_LAYERS = (((1, 0), (1, 1), (2, 1), (1, 2)), ((0, 1), (1, 0), (1, 1), (2, 1), (1, 2)))
 COARSE = 46
 FINE = 64
 ROWS = 64
@@ -56,39 +57,6 @@ def add(nc, out, in0, in1):
     nc.vector.tensor_tensor(out=out, in0=in0, in1=in1, op=ALU.add)
 
 
-def three_to_four(nc, cells, outer, inner, three):
-    add(nc, cells[:, :, :, :, 1], outer[:, :, :, :, 1], outer[:, :, :, :, 2])
-    add(nc, cells[:, :, :, :, 0:3:2], three[:, :, :, :, 0:4:3], inner[:, :, :, :, 1:3])
-
-
-def pool_along_w(nc, work, label, tiles, dtype, outer, inner):
-    three = work.tile([P, 2, tiles, SLOTS], dtype, name="%s_three_w" % label)
-    four = work.tile([P, 2, tiles, 16, 6], dtype, name="%s_four_w" % label)
-    add(nc, three[:], outer, inner)
-    three_to_four(
-        nc,
-        four[:].rearrange("c kh t m (e k) -> c kh (t m) e k", k=3),
-        outer.rearrange("c kh t (m e a) -> c kh (t m) e a", e=2, a=4),
-        inner.rearrange("c kh t (m e a) -> c kh (t m) e a", e=2, a=4),
-        three[:].rearrange("c kh t (m e a) -> c kh (t m) e a", e=2, a=4),
-    )
-    return three, four
-
-
-def pool_along_h(nc, work, label, tiles, dtype, four):
-    three = work.tile([P, tiles, 16, 6], dtype, name="%s_three_h" % label)
-    s6 = work.tile([P, tiles, B, 36], dtype, name="%s_s6" % label)
-    add(nc, three[:], four[:, 0], four[:, 1])
-    three_to_four(
-        nc,
-        s6[:].rearrange("c t b (e k w) -> c t b e k w", e=2, k=3),
-        four[:, 0].rearrange("c t (b e a) w -> c t b e a w", b=B, e=2),
-        four[:, 1].rearrange("c t (b e a) w -> c t b e a w", b=B, e=2),
-        three[:].rearrange("c t (b e a) w -> c t b e a w", b=B, e=2),
-    )
-    return s6
-
-
 def coarser_sums(nc, work, label, tiles, s6):
     s3 = work.tile([P, tiles, B, 9], F32, name="%s_s3" % label)
     s1 = work.tile([P, tiles, B, 1], F32, name="%s_s1" % label)
@@ -105,12 +73,6 @@ def coarser_sums(nc, work, label, tiles, s6):
         op=ALU.add,
     )
     return s3, s1
-
-
-def coarse_means(nc, s6, s3, s1, coarse, unit):
-    nc.scalar.mul(out=coarse[:, :, :, 10:46], in_=s6[:], mul=unit / 16.0)
-    nc.scalar.mul(out=coarse[:, :, :, 1:10], in_=s3[:], mul=unit / 64.0)
-    nc.scalar.mul(out=coarse[:, :, :, 0:1], in_=s1[:], mul=unit / 576.0)
 
 
 def tile_afnb_pa_kernel(
@@ -262,11 +224,12 @@ def tile_afnb_pa_kernel(
                         in_=pixels[:, :, :, h_src, :, w_src].rearrange("p j hb%s -> p hb%s j" % (rest, rest)),
                     )
 
-        def regroup_layers(g, b, first, last):
+        def regroup_layers(g, b, first, last, on_scalar=True, on_vector=True):
             for pos in range(first, last):
-                if LAYERS[pos] in SCALAR_LAYERS:
-                    regroup(nc.scalar.copy, 3, g, b, pos)
-                else:
+                if LAYERS[pos] in SCALAR_LAYERS[g]:
+                    if on_scalar:
+                        regroup(nc.scalar.copy, 3, g, b, pos)
+                elif on_vector:
                     regroup(nc.vector.tensor_copy, 4, g, b, pos)
 
         def regroup_round(g, first, last):
@@ -317,33 +280,47 @@ def tile_afnb_pa_kernel(
         def relu_wide(q):
             for t in range(KEY_TILES):
                 norm_relu(
-                    relu[:, WIDE * q : WIDE * (q + 1), t, :],
-                    u_wide[(t, q)][:].rearrange("c (l s) -> c l s", s=SLOTS),
+                    relu[:, WIDE * q : WIDE * (q + 1), t, :].rearrange("c l (w m) -> c l w m", m=CELL_ROWS),
+                    u_wide[(t, q)][:].rearrange("c (l m w) -> c l w m", l=WIDE, m=CELL_ROWS),
                     t,
                 )
 
-        regroup_round(*rounds[0])
-        for i, (g, first, last) in enumerate(rounds):
-            if i + 1 < len(rounds):
-                regroup_round(*rounds[i + 1])
-            if (g, last) == (0, 8):
-                nc.scalar.copy(out=bias_sb[:], in_=bias_ps[:])
+        def quantise(g, first, last):
             nc.vector.quantize_mx(
                 out=x_codes[:, g, first:last, :].rearrange("p l s -> p (l s)").bitcast(FP8X4),
                 scales=x_planes[:, g, first:last, :].rearrange("p l s -> p (l s)"),
                 in_=grouped[(g, first)][:].rearrange("p l s j -> p (l s j)"),
             )
+
+        regroup_round(*rounds[0])
+        for i, (g, first, last) in enumerate(rounds):
+            closing = last == n_layers
+            if i + 1 < len(rounds):
+                if closing:
+                    regroup_layers(g + 1, 0, 0, 4)
+                else:
+                    regroup_layers(g, 1, *rounds[i + 1][1:], on_vector=g == 0)
+                    if g == 1 and i + 2 < len(rounds):
+                        regroup_layers(g, 1, *rounds[i + 2][1:], on_scalar=False)
+            if (g, last) == (0, 8):
+                nc.scalar.copy(out=bias_sb[:], in_=bias_ps[:])
+            quantise(g, first, last)
+            if closing and g == 0:
+                regroup_layers(1, 0, 4, n_layers)
+                regroup_layers(1, 1, *rounds[i + 1][1:])
+                regroup_layers(1, 1, *rounds[i + 2][1:], on_scalar=False)
             if g == PASSES - 1 and last % WIDE == 0:
                 key_passes(g, last // WIDE - 1)
             for pos in range(first, last):
-                if g == 0 or kinds[pos] == 0:
+                if g == 0 or kinds[pos] < 2:
                     value_pass(g, pos)
-            if g == 0 and last == n_layers:
+            if g == 0 and closing:
                 for q in range(2):
                     key_passes(g, q)
             if g == PASSES - 1 and first == 4:
                 relu_wide(0)
-                nc.scalar.copy(out=g_sb[0][:], in_=v_kind[0][:])
+                for kind in range(2):
+                    nc.scalar.copy(out=g_sb[kind][:], in_=v_kind[kind][:])
 
         u_last = psum.tile([P, KEY_TILES, SLOTS], F32, tag="key_a")
         for t in range(KEY_TILES):
@@ -352,12 +329,16 @@ def tile_afnb_pa_kernel(
 
         relu_wide(1)
         for t in range(KEY_TILES):
-            norm_relu(k_sums[:, 4, t, :], u_last[:, t, :], t)
+            norm_relu(
+                k_sums[:, 4, t, :].rearrange("c (w m) -> c w m", m=CELL_ROWS),
+                u_last[:, t, :].rearrange("c (m w) -> c w m", m=CELL_ROWS),
+                t,
+            )
 
         for pos in range(n_layers):
-            if kinds[pos] != 0:
+            if kinds[pos] >= 2:
                 value_pass(PASSES - 1, pos)
-        for kind in range(1, KINDS):
+        for kind in range(2, KINDS):
             nc.scalar.copy(out=g_sb[kind][:], in_=v_kind[kind][:])
 
         coarse_ps = psum.tile([P, CV], F32, tag="key_b")
@@ -386,31 +367,75 @@ def tile_afnb_pa_kernel(
             )
 
         def key_fine(t):
-            add(
-                nc,
-                key_sb[:, t, :, COARSE : COARSE + FINE],
-                k_three[:, 0, t].rearrange("c (b n) -> c b n", b=B),
-                k_three[:, 1, t].rearrange("c (b n) -> c b n", b=B),
-            )
+            by_cell = [k_three[:, kh, t].rearrange("c (w b r) -> c b r w", b=B, r=8) for kh in range(2)]
+            add(nc, key_sb[:, t, :, COARSE : COARSE + FINE].rearrange("c b (r w) -> c b r w", r=8), *by_cell)
 
         pairs = relu[:].rearrange("c (i two) t s -> c i two t s", two=2)
+        k_three = work.tile([P, 2, KEY_TILES, SLOTS], F32)
+        k_four = work.tile([P, 2, KEY_TILES, 6, CELL_ROWS], F32)
+        k_three_h = work.tile([P, KEY_TILES, 6, CELL_ROWS], F32)
+        k_s6 = work.tile([P, 3, KEY_TILES, B, 2, 6], F32)
+        k_pairs = work.tile([P, 3, KEY_TILES, B, 2, 3], F32)
+
         add(nc, k_sums[:, 0:2], pairs[:, 0:2, 0], pairs[:, 0:2, 1])
         add_kind(0)
         add(nc, k_sums[:, 1], k_sums[:, 0], k_sums[:, 1])
+        add_kind(1)
         add(nc, k_sums[:, 2:4], pairs[:, 2:4, 0], pairs[:, 2:4, 1])
-        k_three, k_four = pool_along_w(nc, work, "key", KEY_TILES, F32, k_sums[:, 1:3], k_sums[:, 3:5])
+        add_kind(2)
+        outer_w = k_sums[:, 1:3].rearrange("c kh t (e a m) -> c (kh t e) a m", e=2, a=4)
+        inner_w = k_sums[:, 3:5].rearrange("c kh t (e a m) -> c (kh t e) a m", e=2, a=4)
+        three_w = k_three[:].rearrange("c kh t (e a m) -> c (kh t e) a m", e=2, a=4)
+        four_w = k_four[:].rearrange("c kh t (e k) m -> c (kh t e) k m", e=2)
+        add(nc, k_three[:], k_sums[:, 1:3], k_sums[:, 3:5])
+        add(nc, four_w[:, :, 1], outer_w[:, :, 1], outer_w[:, :, 2])
+        add(nc, four_w[:, :, 0:3:2], three_w[:, :, 0:4:3], inner_w[:, :, 1:3])
         key_fine(0)
-        k_s6 = pool_along_h(nc, work, "key", KEY_TILES, F32, k_four)
+        add(nc, k_three_h[:], k_four[:, 0], k_four[:, 1])
+        outer_h = k_four[:, 0].rearrange("c t w (be a) -> c t be w a", a=4)
+        inner_h = k_four[:, 1].rearrange("c t w (be a) -> c t be w a", a=4)
+        three_h = k_three_h[:].rearrange("c t w (be a) -> c t be w a", a=4)
+        s6 = k_s6[:].rearrange("c k t b e w -> c k t (b e) w")
+        add(nc, s6[:, 1], outer_h[:, :, :, :, 1], outer_h[:, :, :, :, 2])
         key_fine(1)
-        k_s3, k_s1 = coarser_sums(nc, work, "key", KEY_TILES, k_s6)
-        coarse_means(nc, k_s6, k_s3, k_s1, key_sb[:, :, :, 0:COARSE], 9.0)
-        for t in range(KEY_TILES):
-            nc.scalar.dma_start(out=out_1[:, P * t : P * (t + 1), :].rearrange("b c l -> c b l"), in_=key_sb[:, t])
-        for kind in range(1, KINDS):
-            add_kind(kind)
+        for half in range(2):
+            add(nc, s6[:, 2 * half], three_h[:, :, :, :, 3 * half], inner_h[:, :, :, :, 1 + half])
+        add_kind(3)
+        by_pair = k_s6[:].rearrange("c k t b e (w j) -> c (k t b e w) j", j=2)
+        add(nc, k_pairs[:].rearrange("c k t b e w -> c (k t b e w)"), by_pair[:, :, 0], by_pair[:, :, 1])
+        for k in range(3):
+            nc.scalar.mul(
+                out=key_sb[:, :, :, 10:46].rearrange("c t b (e k w) -> c (t b) e k w", e=2, k=3)[:, :, :, k],
+                in_=k_s6[:, k].rearrange("c t b e w -> c (t b) e w"),
+                mul=9.0 / 16.0,
+            )
+        k_s3 = work.tile([P, 3, KEY_TILES * B, 3], F32)
+        k_s1 = work.tile([P, KEY_TILES * B, 1], F32)
+        for row, ((k0, e0), (k1, e1)) in enumerate((((0, 0), (1, 0)), ((2, 0), (0, 1)), ((1, 1), (2, 1)))):
+            halves = [
+                k_pairs[:, k].rearrange("c t b e w -> c (t b) e w")[:, :, e] for k, e in ((k0, e0), (k1, e1))
+            ]
+            add(nc, k_s3[:, row], *halves)
+        nc.vector.tensor_reduce(
+            out=k_s1[:, :, 0],
+            in_=k_pairs[:].rearrange("c k t b e w -> c (t b) k (e w)"),
+            axis=AXIS.XY,
+            op=ALU.add,
+        )
         for b in range(B):
             nc.sync.dma_start(out=out_0[b, COARSE : COARSE + FINE, :], in_=partial[3][FINE * b : FINE * (b + 1), :])
+
         nc.scalar.copy(out=v_coarse[:], in_=coarse_ps[:])
-        for b, queue in enumerate((nc.sync, nc.scalar)):
-            for first, last in ((32, COARSE), (0, 32)):
-                queue.dma_start(out=out_0[b, first:last, :], in_=v_coarse[ROWS * b + first : ROWS * b + last, :])
+        nc.scalar.mul(
+            out=key_sb[:, :, :, 1:10].rearrange("c t b (r w) -> c (t b) r w", r=3),
+            in_=k_s3[:].rearrange("c r m w -> c m r w"),
+            mul=9.0 / 64.0,
+        )
+        nc.scalar.mul(out=key_sb[:, :, :, 0:1].rearrange("c t b o -> c (t b) o"), in_=k_s1[:], mul=9.0 / 576.0)
+        parts = ((0, 32), (32, COARSE))
+        for first, last in parts:
+            nc.sync.dma_start(out=out_0[0, first:last, :], in_=v_coarse[first:last, :])
+        for t in range(KEY_TILES):
+            nc.scalar.dma_start(out=out_1[:, P * t : P * (t + 1), :].rearrange("b c l -> c b l"), in_=key_sb[:, t])
+        for first, last in parts:
+            nc.scalar.dma_start(out=out_0[1, first:last, :], in_=v_coarse[ROWS + first : ROWS + last, :])

@@ -33,7 +33,7 @@ SLOTS = 128
 CELL_ROWS = 16
 WIDE = 4
 GROUPS = (((0, 1), (1, 2), (2, 4), (4, 6), (6, 8), (8, 9)), ((0, 2), (2, 4), (4, 6), (6, 8), (8, 9)))
-WARM_UP = 4
+WARM_UP = 2
 SCALAR_LAYERS = (((1, 0), (1, 1), (2, 1), (1, 2)), ((0, 1), (1, 0), (1, 1), (2, 1), (1, 2)))
 COARSE = 46
 FINE = 64
@@ -97,6 +97,8 @@ def tile_afnb_pa_kernel(
         nc.gpsimd.memset(ones[:], 1.0)
         make_identity(nc, ident[:])
 
+        idle = keep.tile([P, CV], F32)
+        nc.vector.memset(idle[:], 0.0)
         nc.vector.memset(wv_planes[:].bitcast(I32), 0)
         nc.vector.memset(wk_planes[:].bitcast(I32), 0)
 
@@ -123,12 +125,12 @@ def tile_afnb_pa_kernel(
         load_planes(nc.scalar, wv_planes, wv_scales)
         nc.sync.dma_start(out=wv_codes[:].bitcast(I32), in_=wv_words.bitcast(I32).rearrange("g p n -> p g n"))
         load_x_batch(nc.sync, 1, 0)
-        with nc.allow_non_contiguous_dma(reason="five vectors of 256 values, one value a partition"):
-            for tile_, vec in zip(vecs, (bk, gk, bek, mk, vk)):
-                nc.sync.dma_start(out=tile_[:], in_=vec.rearrange("(t c) -> c t", c=P))
-        load_x_batch(nc.sync, 1, 1)
-        load_planes(nc.sync, wk_planes, wk_scales)
         nc.sync.dma_start(out=wk_codes[:].bitcast(I32), in_=wk_words.bitcast(I32).rearrange("g p n -> p g n"))
+        load_planes(nc.sync, wk_planes, wk_scales)
+        load_x_batch(nc.sync, 1, 1)
+        with nc.allow_non_contiguous_dma(reason="five vectors of 256 values, one value a partition"):
+            for i in (4, 1, 0, 3, 2):
+                nc.sync.dma_start(out=vecs[i][:], in_=(bk, gk, bek, mk, vk)[i].rearrange("(t c) -> c t", c=P))
 
         pool_mat = keep.tile([P, KINDS, B, ROWS], F32)
         mat_w = keep.tile([P, 2, 96], BF16)
@@ -170,16 +172,12 @@ def tile_afnb_pa_kernel(
         nc.gpsimd.tensor_scalar(out=var_81[:], in0=vk_c, scalar1=81.0, scalar2=81.0 * EPS, op0=ALU.mult, op1=ALU.add)
         nc.gpsimd.tensor_tensor(out=rstd_9th[:], in0=var_81[:], in1=minus_half[:], op=ALU.pow)
         nc.gpsimd.tensor_tensor(out=scale_9th[:], in0=gk_c, in1=rstd_9th[:], op=ALU.mult)
-        nc.gpsimd.tensor_tensor(out=centred[:], in0=bk_c, in1=mk_c, op=ALU.subtract)
-        nc.gpsimd.tensor_tensor(out=scaled[:], in0=centred[:], in1=scale_9th[:], op=ALU.mult)
-        nc.gpsimd.tensor_scalar(out=bek_9th[:], in0=bek_c, scalar1=1.0 / 9.0, scalar2=0.0, op0=ALU.mult, op1=ALU.add)
-        nc.gpsimd.tensor_tensor(out=shift_9th[:], in0=scaled[:], in1=bek_9th[:], op=ALU.add)
 
         bias_ps = psum.tile([P, CV], F32, tag="key_d")
         bias_sb = keep.tile([P, CV], F32)
         warm_ps = psum.tile([P, CV], F32, tag="key_c")
         for i in range(WARM_UP):
-            nc.tensor.matmul(out=warm_ps[:], lhsT=ones[:], rhs=raw[0][:, 0, 0, 0:CV], start=True, stop=True)
+            nc.tensor.matmul(out=warm_ps[:], lhsT=idle[:, 0:P], rhs=idle[:], start=True, stop=True)
         nc.tensor.matmul(out=bias_ps[:], lhsT=ones[:], rhs=bias_rows[:], start=True, stop=True)
 
         n_layers = len(LAYERS)
@@ -309,6 +307,11 @@ def tile_afnb_pa_kernel(
                 regroup_layers(1, 0, 4, n_layers)
                 regroup_layers(1, 1, *rounds[i + 1][1:])
                 regroup_layers(1, 1, *rounds[i + 2][1:], on_scalar=False)
+            if (g, first) == (1, 0):
+                nc.vector.tensor_tensor(out=centred[:], in0=bk_c, in1=mk_c, op=ALU.subtract)
+                nc.vector.tensor_scalar(out=bek_9th[:], in0=bek_c, scalar1=1.0 / 9.0, scalar2=0.0, op0=ALU.mult, op1=ALU.add)
+                nc.gpsimd.tensor_tensor(out=scaled[:], in0=centred[:], in1=scale_9th[:], op=ALU.mult)
+                nc.gpsimd.tensor_tensor(out=shift_9th[:], in0=scaled[:], in1=bek_9th[:], op=ALU.add)
             if g == PASSES - 1 and last % WIDE == 0:
                 key_passes(g, last // WIDE - 1)
             for pos in range(first, last):

@@ -98,8 +98,8 @@ def tile_afnb_pa_kernel(
         make_identity(nc, ident[:])
 
         idle = keep.tile([P, CV], F32)
-        nc.vector.memset(idle[:], 0.0)
         nc.vector.memset(wv_planes[:].bitcast(I32), 0)
+        nc.vector.memset(idle[:], 0.0)
         nc.vector.memset(wk_planes[:].bitcast(I32), 0)
 
         def load_planes(queue, planes, scales):
@@ -121,16 +121,15 @@ def tile_afnb_pa_kernel(
 
         vecs = [keep.tile([P, KEY_TILES], BF16, name="vec%d" % i) for i in range(5)]
         load_x(nc.sync, 0)
-        nc.scalar.dma_start(out=bias_rows[0:1, :], in_=bv.unsqueeze(0))
-        load_planes(nc.scalar, wv_planes, wv_scales)
+        load_planes(nc.sync, wv_planes, wv_scales)
         nc.sync.dma_start(out=wv_codes[:].bitcast(I32), in_=wv_words.bitcast(I32).rearrange("g p n -> p g n"))
-        load_x_batch(nc.sync, 1, 0)
+        load_x(nc.sync, 1)
         nc.sync.dma_start(out=wk_codes[:].bitcast(I32), in_=wk_words.bitcast(I32).rearrange("g p n -> p g n"))
         load_planes(nc.sync, wk_planes, wk_scales)
-        load_x_batch(nc.sync, 1, 1)
         with nc.allow_non_contiguous_dma(reason="five vectors of 256 values, one value a partition"):
             for i in (4, 1, 0, 3, 2):
                 nc.sync.dma_start(out=vecs[i][:], in_=(bk, gk, bek, mk, vk)[i].rearrange("(t c) -> c t", c=P))
+        nc.gpsimd.dma_start(out=bias_rows[0:1, :], in_=bv.unsqueeze(0))
 
         pool_mat = keep.tile([P, KINDS, B, ROWS], F32)
         mat_w = keep.tile([P, 2, 96], BF16)
@@ -172,18 +171,21 @@ def tile_afnb_pa_kernel(
         nc.gpsimd.tensor_scalar(out=var_81[:], in0=vk_c, scalar1=81.0, scalar2=81.0 * EPS, op0=ALU.mult, op1=ALU.add)
         nc.gpsimd.tensor_tensor(out=rstd_9th[:], in0=var_81[:], in1=minus_half[:], op=ALU.pow)
         nc.gpsimd.tensor_tensor(out=scale_9th[:], in0=gk_c, in1=rstd_9th[:], op=ALU.mult)
+        nc.gpsimd.tensor_tensor(out=centred[:], in0=bk_c, in1=mk_c, op=ALU.subtract)
+        nc.gpsimd.tensor_tensor(out=scaled[:], in0=centred[:], in1=scale_9th[:], op=ALU.mult)
+        nc.gpsimd.tensor_scalar(out=bek_9th[:], in0=bek_c, scalar1=1.0 / 9.0, scalar2=0.0, op0=ALU.mult, op1=ALU.add)
+        nc.gpsimd.tensor_tensor(out=shift_9th[:], in0=scaled[:], in1=bek_9th[:], op=ALU.add)
 
         bias_ps = psum.tile([P, CV], F32, tag="key_d")
         bias_sb = keep.tile([P, CV], F32)
         warm_ps = psum.tile([P, CV], F32, tag="key_c")
         for i in range(WARM_UP):
             nc.tensor.matmul(out=warm_ps[:], lhsT=idle[:, 0:P], rhs=idle[:], start=True, stop=True)
-        nc.tensor.matmul(out=bias_ps[:], lhsT=ones[:], rhs=bias_rows[:], start=True, stop=True)
 
         n_layers = len(LAYERS)
         x_codes = keep.tile([P, PASSES, n_layers, SLOTS], U32, align_bytes=64)
         x_planes = keep.tile([P, PASSES, n_layers, SLOTS], U8, align_bytes=64)
-        v_kind = [psum.tile([P, CV], F32, name="v_kind%d" % kind) for kind in range(KINDS)]
+        v_kind = [psum.tile([P, CV], F32, name="v_kind%d" % kind, tag="v_kind%d" % kind) for kind in range(KINDS)]
         key_tags = (("key_a", "key_c"), ("key_b", "key_d"))
         u_wide = {}
         relu = keep.tile([P, 2 * WIDE, KEY_TILES, SLOTS], F32)
@@ -291,27 +293,27 @@ def tile_afnb_pa_kernel(
             )
 
         regroup_round(*rounds[0])
+        def regroup_second(i, on_scalar, on_vector):
+            if i < len(rounds):
+                for b in range(B):
+                    regroup_layers(1, b, *rounds[i][1:], on_scalar=on_scalar, on_vector=on_vector)
+
         for i, (g, first, last) in enumerate(rounds):
             closing = last == n_layers
-            if i + 1 < len(rounds):
-                if closing:
-                    regroup_layers(g + 1, 0, 0, 4)
-                else:
-                    regroup_layers(g, 1, *rounds[i + 1][1:], on_vector=g == 0)
-                    if g == 1 and i + 2 < len(rounds):
-                        regroup_layers(g, 1, *rounds[i + 2][1:], on_scalar=False)
-            if (g, last) == (0, 8):
+            if g == 0 and not closing:
+                regroup_layers(0, 1, *rounds[i + 1][1:])
+            else:
+                if g == 0:
+                    regroup_second(i + 1, False, True)
+                regroup_second(i + 1, True, False)
+                regroup_second(i + 2 if g == 0 else i + 3, False, True)
+            if (g, last) == (0, 6):
+                nc.tensor.matmul(out=bias_ps[:], lhsT=ones[:], rhs=bias_rows[:], start=True, stop=True)
+            if g == 0 and closing:
                 nc.scalar.copy(out=bias_sb[:], in_=bias_ps[:])
             quantise(g, first, last)
-            if closing and g == 0:
-                regroup_layers(1, 0, 4, n_layers)
-                regroup_layers(1, 1, *rounds[i + 1][1:])
-                regroup_layers(1, 1, *rounds[i + 2][1:], on_scalar=False)
-            if (g, first) == (1, 0):
-                nc.vector.tensor_tensor(out=centred[:], in0=bk_c, in1=mk_c, op=ALU.subtract)
-                nc.vector.tensor_scalar(out=bek_9th[:], in0=bek_c, scalar1=1.0 / 9.0, scalar2=0.0, op0=ALU.mult, op1=ALU.add)
-                nc.gpsimd.tensor_tensor(out=scaled[:], in0=centred[:], in1=scale_9th[:], op=ALU.mult)
-                nc.gpsimd.tensor_tensor(out=shift_9th[:], in0=scaled[:], in1=bek_9th[:], op=ALU.add)
+            if g == 0 and closing:
+                regroup_second(i + 3, False, True)
             if g == PASSES - 1 and last % WIDE == 0:
                 key_passes(g, last // WIDE - 1)
             for pos in range(first, last):
@@ -322,38 +324,24 @@ def tile_afnb_pa_kernel(
                     key_passes(g, q)
             if g == PASSES - 1 and first == 4:
                 relu_wide(0)
-                for kind in range(2):
-                    nc.scalar.copy(out=g_sb[kind][:], in_=v_kind[kind][:])
 
         u_last = psum.tile([P, KEY_TILES, SLOTS], F32, tag="key_a")
         for t in range(KEY_TILES):
             for g in range(PASSES):
                 key_pass(u_last[:, t, :], t, g, x_codes[:, g, n_layers - 1, :], x_planes[:, g, n_layers - 1, :])
 
-        relu_wide(1)
-        for t in range(KEY_TILES):
-            norm_relu(
-                k_sums[:, 4, t, :].rearrange("c (w m) -> c w m", m=CELL_ROWS),
-                u_last[:, t, :].rearrange("c (m w) -> c w m", m=CELL_ROWS),
-                t,
-            )
+        def relu_last():
+            relu_wide(1)
+            for t in range(KEY_TILES):
+                norm_relu(
+                    k_sums[:, 4, t, :].rearrange("c (w m) -> c w m", m=CELL_ROWS),
+                    u_last[:, t, :].rearrange("c (m w) -> c w m", m=CELL_ROWS),
+                    t,
+                )
 
         for pos in range(n_layers):
             if kinds[pos] >= 2:
                 value_pass(PASSES - 1, pos)
-        for kind in range(2, KINDS):
-            nc.scalar.copy(out=g_sb[kind][:], in_=v_kind[kind][:])
-
-        coarse_ps = psum.tile([P, CV], F32, tag="key_b")
-        nc.tensor.matmul(out=coarse_ps[:], lhsT=ones[:], rhs=bias_rows[:], start=True, stop=False)
-        for kind in range(KINDS):
-            nc.tensor.matmul(
-                out=coarse_ps[:],
-                lhsT=pool_mat[:, kind].rearrange("p b l -> p (b l)"),
-                rhs=g_sb[kind][:],
-                start=False,
-                stop=(kind == KINDS - 1),
-            )
 
         partial = [keep.tile([P, CV], F32, name="partial%d" % kind) for kind in range(KINDS)]
         v_coarse = keep.tile([P, CV], F32)
@@ -380,12 +368,32 @@ def tile_afnb_pa_kernel(
         k_s6 = work.tile([P, 3, KEY_TILES, B, 2, 6], F32)
         k_pairs = work.tile([P, 3, KEY_TILES, B, 2, 3], F32)
 
-        add(nc, k_sums[:, 0:2], pairs[:, 0:2, 0], pairs[:, 0:2, 1])
         add_kind(0)
-        add(nc, k_sums[:, 1], k_sums[:, 0], k_sums[:, 1])
+        nc.scalar.copy(out=g_sb[0][:], in_=v_kind[0][:])
+        relu_last()
+        add(nc, k_sums[:, 0:2], pairs[:, 0:2, 0], pairs[:, 0:2, 1])
         add_kind(1)
-        add(nc, k_sums[:, 2:4], pairs[:, 2:4, 0], pairs[:, 2:4, 1])
+        add(nc, k_sums[:, 1], k_sums[:, 0], k_sums[:, 1])
         add_kind(2)
+        add(nc, k_sums[:, 2:4], pairs[:, 2:4, 0], pairs[:, 2:4, 1])
+        add_kind(3)
+        for kind in range(1, KINDS):
+            nc.scalar.copy(out=g_sb[kind][:], in_=v_kind[kind][:])
+
+        coarse_ps = [psum.tile([P, CV // 2], F32, name="coarse_ps%d" % h, tag=("key_b", "v_kind0")[h]) for h in range(2)]
+        column_halves = [slice(CV // 2 * h, CV // 2 * (h + 1)) for h in range(2)]
+        for out, half in zip(coarse_ps, column_halves):
+            nc.tensor.matmul(out=out[:], lhsT=ones[:], rhs=bias_rows[:, half], start=True, stop=False)
+        for kind in range(KINDS):
+            for out, half in zip(coarse_ps, column_halves):
+                nc.tensor.matmul(
+                    out=out[:],
+                    lhsT=pool_mat[:, kind].rearrange("p b l -> p (b l)"),
+                    rhs=g_sb[kind][:, half],
+                    start=False,
+                    stop=(kind == KINDS - 1),
+                )
+
         outer_w = k_sums[:, 1:3].rearrange("c kh t (e a m) -> c (kh t e) a m", e=2, a=4)
         inner_w = k_sums[:, 3:5].rearrange("c kh t (e a m) -> c (kh t e) a m", e=2, a=4)
         three_w = k_three[:].rearrange("c kh t (e a m) -> c (kh t e) a m", e=2, a=4)
@@ -403,7 +411,6 @@ def tile_afnb_pa_kernel(
         key_fine(1)
         for half in range(2):
             add(nc, s6[:, 2 * half], three_h[:, :, :, :, 3 * half], inner_h[:, :, :, :, 1 + half])
-        add_kind(3)
         by_pair = k_s6[:].rearrange("c k t b e (w j) -> c (k t b e w) j", j=2)
         add(nc, k_pairs[:].rearrange("c k t b e w -> c (k t b e w)"), by_pair[:, :, 0], by_pair[:, :, 1])
         for k in range(3):
@@ -428,7 +435,8 @@ def tile_afnb_pa_kernel(
         for b in range(B):
             nc.sync.dma_start(out=out_0[b, COARSE : COARSE + FINE, :], in_=partial[3][FINE * b : FINE * (b + 1), :])
 
-        nc.scalar.copy(out=v_coarse[:], in_=coarse_ps[:])
+        nc.scalar.copy(out=v_coarse[:, column_halves[0]], in_=coarse_ps[0][:])
+        nc.vector.tensor_copy(out=v_coarse[:, column_halves[1]], in_=coarse_ps[1][:])
         nc.scalar.mul(
             out=key_sb[:, :, :, 1:10].rearrange("c t b (r w) -> c (t b) r w", r=3),
             in_=k_s3[:].rearrange("c r m w -> c m r w"),

from contextlib import ExitStack

import concourse.mybir as mybir
from concourse.masks import make_identity

F32 = mybir.dt.float32
BF16 = mybir.dt.bfloat16
I32 = mybir.dt.int32
U32 = mybir.dt.uint32
U8 = mybir.dt.uint8
FP8X4 = mybir.dt.float8_e4m3fn_x4
FP4X4 = mybir.dt.float4_e2m1fn_x4
ALU = mybir.AluOpType
ACT = mybir.ActivationFunctionType
AXIS = mybir.AxisListType

P = 128
PACK = 4
K_PASS = P * PACK
B, CL, CK, CV, SIDE = 2, 1024, 256, 512, 24
PIX = SIDE * SIDE
PASSES = CL // K_PASS
KEY_TILES = CK // P
EPS = 1e-5
FLOPS = 2 * B * PIX * CL * (CK + CV)

OFFSETS = ((0, 5), (1, 4), (2, 3))
EVEN_STEP = 1
INNER = 2
LAYERS = sorted([(lh, lw) for lh in range(3) for lw in range(3)], key=lambda hw: (hw[1] == INNER, hw[0] == INNER))
KINDS = 4
SLOTS = 128
CELL_ROWS = 16
WIDE = 4
GROUPS = (((0, 1), (1, 2), (2, 4), (4, 6), (6, 8), (8, 9)), ((0, 2), (2, 4), (4, 6), (6, 8), (8, 9)))
WARM_UP = 2
SCALAR_LAYERS = (((1, 0), (1, 1), (2, 1), (1, 2)), ((0, 1), (1, 0), (1, 1), (2, 1), (1, 2)))
COARSE = 46
FINE = 64
ROWS = 64


def kind_of(lh, lw):
    return 2 * (lw == INNER) + (lh == INNER)


def picks(layer, one_by_one):
    if layer == EVEN_STEP:
        return [(1, 0, False)]
    first, second = OFFSETS[layer]
    if one_by_one:
        return [(first, 0, False), (second, 1, False)]
    return [(slice(first, second + 1, second - first), slice(0, 2), True)]


def add(nc, out, in0, in1):
    nc.vector.tensor_tensor(out=out, in0=in0, in1=in1, op=ALU.add)


def coarser_sums(nc, work, label, tiles, s6):
    s3 = work.tile([P, tiles, B, 9], F32, name="%s_s3" % label)
    s1 = work.tile([P, tiles, B, 1], F32, name="%s_s1" % label)
    nc.vector.tensor_reduce(
        out=s3[:].rearrange("c t b (h w) -> c (t b h) w", h=3),
        in_=s6[:].rearrange("c t b (h i w j) -> c (t b h) w i j", h=3, i=2, w=3, j=2),
        axis=AXIS.XY,
        op=ALU.add,
    )
    nc.vector.tensor_reduce(
        out=s1[:].rearrange("c t b o -> c (t b o)"),
        in_=s6[:].rearrange("c t b n -> c (t b) n"),
        axis=AXIS.X,
        op=ALU.add,
    )
    return s3, s1


def tile_afnb_pa_kernel(
    tc, low_feats, wk_words, wk_scales, bk, gk, bek, mk, vk, wv_words, wv_scales, bv, out_0, out_1
):
    nc = tc.nc
    with ExitStack() as ctx:
        keep = ctx.enter_context(tc.tile_pool(name="keep", bufs=1))
        work = ctx.enter_context(tc.tile_pool(name="work", bufs=1))
        psum = ctx.enter_context(tc.psum_pool(name="psum", bufs=1))
        ctx.enter_context(tc.manual_schedule())

        wk_planes = keep.tile([P, PASSES, CK], U8, align_bytes=64)
        wv_planes = keep.tile([P, PASSES, CV], U8, align_bytes=64)
        wk_codes = keep.tile([P, PASSES, 2 * CK], U8, align_bytes=64)
        wv_codes = keep.tile([P, PASSES, 2 * CV], U8, align_bytes=64)
        raw = [keep.tile([P, B, PACK, PIX], BF16, name="raw%d" % g) for g in range(PASSES)]
        ident = keep.tile([P, P], BF16)
        bias_rows = keep.tile([P, CV], BF16)
        ones = keep.tile([P, P], BF16)
        nc.gpsimd.memset(bias_rows[:], 0.0)
        nc.gpsimd.memset(ones[:], 1.0)
        make_identity(nc, ident[:])

        idle = keep.tile([P, CV], F32)
        nc.vector.memset(wv_planes[:].bitcast(I32), 0)
        nc.vector.memset(idle[:], 0.0)
        nc.vector.memset(wk_planes[:].bitcast(I32), 0)

        def load_planes(queue, planes, scales):
            for quad in range(4):
                queue.dma_start(
                    out=planes[32 * quad : 32 * quad + 4].bitcast(I32),
                    in_=scales.bitcast(I32)[:, 4 * quad : 4 * quad + 4, :].rearrange("g r n -> r g n"),
                )

        def load_x_batch(queue, g, b):
            queue.dma_start(
                out=raw[g][:, b].rearrange("p j n -> p (j n)"),
                in_=low_feats[b, g * K_PASS : (g + 1) * K_PASS].rearrange("(p j) h w -> p (j h w)", j=PACK),
            )

        def load_x(queue, g):
            for b in range(B):
                load_x_batch(queue, g, b)

        vecs = [keep.tile([P, KEY_TILES], BF16, name="vec%d" % i) for i in range(5)]
        load_x(nc.sync, 0)
        load_planes(nc.sync, wv_planes, wv_scales)
        nc.sync.dma_start(out=wv_codes[:].bitcast(I32), in_=wv_words.bitcast(I32).rearrange("g p n -> p g n"))
        load_x(nc.sync, 1)
        nc.sync.dma_start(out=wk_codes[:].bitcast(I32), in_=wk_words.bitcast(I32).rearrange("g p n -> p g n"))
        load_planes(nc.sync, wk_planes, wk_scales)
        with nc.allow_non_contiguous_dma(reason="five vectors of 256 values, one value a partition"):
            for i in (4, 1, 0, 3, 2):
                nc.sync.dma_start(out=vecs[i][:], in_=(bk, gk, bek, mk, vk)[i].rearrange("(t c) -> c t", c=P))
        nc.gpsimd.dma_start(out=bias_rows[0:1, :], in_=bv.unsqueeze(0))

        pool_mat = keep.tile([P, KINDS, B, ROWS], F32)
        mat_w = keep.tile([P, 2, 96], BF16)
        mat_s6 = keep.tile([P, KINDS, B, 36], BF16)
        nc.vector.memset(pool_mat[:], 0.0)
        nc.vector.memset(mat_w[:], 0.0)
        nc.vector.memset(mat_s6[:], 0.0)

        def pool_matrix_sums():
            cells = ident[:].rearrange("c (m a) -> c m a", a=4)
            by_w = mat_w[:].rearrange("c kw (m k) -> c kw m k", k=3)
            nc.vector.tensor_copy(out=by_w[:, 0, :, 0:3:2], in_=cells[:, :, 0:4:3])
            add(nc, by_w[:, 0, :, 1], cells[:, :, 1], cells[:, :, 2])
            add(nc, by_w[:, 1, :, 0:3:2], cells[:, :, 0:4:2], cells[:, :, 1:4:2])
            rows = mat_w[:].rearrange("c kw (m a w) -> c kw m a w", a=4, w=6)
            by_h = mat_s6[:].rearrange("c (kw kh) b (e k w) -> c kw kh (b e) k w", kh=2, k=3, w=6)
            nc.vector.tensor_copy(out=by_h[:, :, 0, :, 0:3:2, :], in_=rows[:, :, :, 0:4:3, :])
            add(nc, by_h[:, :, 0, :, 1, :], rows[:, :, :, 1, :], rows[:, :, :, 2, :])
            for half in range(2):
                add(nc, by_h[:, :, 1, :, 2 * half, :], rows[:, :, :, 2 * half, :], rows[:, :, :, 2 * half + 1, :])
            return coarser_sums(nc, work, "mat", KINDS, mat_s6)

        mat_s3, mat_s1 = pool_matrix_sums()
        for first, last, sums, mean in ((10, 46, mat_s6, 1.0 / 16.0), (1, 10, mat_s3, 1.0 / 64.0), (0, 1, mat_s1, 1.0 / 576.0)):
            nc.gpsimd.tensor_scalar(
                out=pool_mat[:, :, :, first:last], in0=sums[:], scalar1=mean, scalar2=0.0, op0=ALU.mult, op1=ALU.add
            )

        bk_c, gk_c, bek_c, mk_c, vk_c = [tile_[:] for tile_ in vecs]
        minus_half = keep.tile([P, KEY_TILES], F32)
        var_81 = keep.tile([P, KEY_TILES], F32)
        rstd_9th = keep.tile([P, KEY_TILES], F32)
        centred = keep.tile([P, KEY_TILES], F32)
        bek_9th = keep.tile([P, KEY_TILES], F32)
        scaled = keep.tile([P, KEY_TILES], F32)
        scale_9th = keep.tile([P, KEY_TILES], F32)
        shift_9th = keep.tile([P, KEY_TILES], F32)
        nc.gpsimd.memset(minus_half[:], -0.5)
        nc.gpsimd.tensor_scalar(out=var_81[:], in0=vk_c, scalar1=81.0, scalar2=81.0 * EPS, op0=ALU.mult, op1=ALU.add)
        nc.gpsimd.tensor_tensor(out=rstd_9th[:], in0=var_81[:], in1=minus_half[:], op=ALU.pow)
        nc.gpsimd.tensor_tensor(out=scale_9th[:], in0=gk_c, in1=rstd_9th[:], op=ALU.mult)
        nc.gpsimd.tensor_tensor(out=centred[:], in0=bk_c, in1=mk_c, op=ALU.subtract)
        nc.gpsimd.tensor_tensor(out=scaled[:], in0=centred[:], in1=scale_9th[:], op=ALU.mult)
        nc.gpsimd.tensor_scalar(out=bek_9th[:], in0=bek_c, scalar1=1.0 / 9.0, scalar2=0.0, op0=ALU.mult, op1=ALU.add)
        nc.gpsimd.tensor_tensor(out=shift_9th[:], in0=scaled[:], in1=bek_9th[:], op=ALU.add)

        bias_ps = psum.tile([P, CV], F32, tag="key_d")
        bias_sb = keep.tile([P, CV], F32)
        warm_ps = psum.tile([P, CV], F32, tag="key_c")
        for i in range(WARM_UP):
            nc.tensor.matmul(out=warm_ps[:], lhsT=idle[:, 0:P], rhs=idle[:], start=True, stop=True)

        n_layers = len(LAYERS)
        x_codes = keep.tile([P, PASSES, n_layers, SLOTS], U32, align_bytes=64)
        x_planes = keep.tile([P, PASSES, n_layers, SLOTS], U8, align_bytes=64)
        v_kind = [psum.tile([P, CV], F32, name="v_kind%d" % kind, tag="v_kind%d" % kind) for kind in range(KINDS)]
        key_tags = (("key_a", "key_c"), ("key_b", "key_d"))
        u_wide = {}
        relu = keep.tile([P, 2 * WIDE, KEY_TILES, SLOTS], F32)
        k_sums = keep.tile([P, 5, KEY_TILES, SLOTS], F32)
        g_sb = [keep.tile([P, CV], F32, name="g_sb%d" % kind) for kind in range(KINDS)]
        kinds = [kind_of(lh, lw) for lh, lw in LAYERS]
        rounds = [(g, first, last) for g in range(PASSES) for first, last in GROUPS[g]]
        grouped = {}

        round_start = [dict((pos, first) for first, last in GROUPS[g] for pos in range(first, last)) for g in range(PASSES)]
        for g, first, last in rounds:
            grouped[(g, first)] = keep.tile(
                [P, last - first, SLOTS, PACK], BF16, align_bytes=64, name="grouped%d%d" % (g, first)
            )

        def regroup(copy, max_dims, g, b, pos):
            lh, lw = LAYERS[pos]
            first = round_start[g][pos]
            dst = grouped[(g, first)][:, pos - first, FINE * b : FINE * (b + 1), :]
            span_h = 3 if lh == EVEN_STEP else 6
            span_w = 3 if lw == EVEN_STEP else 6
            pixels = raw[g][:, b].rearrange(
                "p j (hb hs wb ws) -> p j hb hs wb ws", hs=span_h, wb=SIDE // span_w, ws=span_w
            )
            slots = dst.rearrange(
                "p (r ph c pw) j -> p r ph c pw j", ph=span_h // 3, c=SIDE // span_w, pw=span_w // 3
            )
            dims = 3 + (lh != EVEN_STEP) + (lw != EVEN_STEP)
            split_h = lh != EVEN_STEP and dims > max_dims
            split_w = lw != EVEN_STEP and dims - split_h > max_dims
            for h_src, h_dst, h_dim in picks(lh, split_h):
                for w_src, w_dst, w_dim in picks(lw, split_w):
                    rest = (" ph" if h_dim else "") + " wb" + (" pw" if w_dim else "")
                    copy(
                        out=slots[:, :, h_dst, :, w_dst, :],
                        in_=pixels[:, :, :, h_src, :, w_src].rearrange("p j hb%s -> p hb%s j" % (rest, rest)),
                    )

        def regroup_layers(g, b, first, last, on_scalar=True, on_vector=True):
            for pos in range(first, last):
                if LAYERS[pos] in SCALAR_LAYERS[g]:
                    if on_scalar:
                        regroup(nc.scalar.copy, 3, g, b, pos)
                elif on_vector:
                    regroup(nc.vector.tensor_copy, 4, g, b, pos)

        def regroup_round(g, first, last):
            if first == 0:
                regroup_layers(g, 0, 0, n_layers)
            regroup_layers(g, 1, first, last)

        def key_pass(out, t, g, codes, planes):
            nc.tensor.matmul_mx(
                out=out,
                lhsT=wk_codes[:, g, 2 * P * t : 2 * P * (t + 1)].bitcast(FP4X4),
                lhsT_scale=wk_planes[:, g, P * t : P * (t + 1)],
                rhs=codes.bitcast(FP8X4),
                rhs_scale=planes,
                start=(g == 0),
                stop=(g == PASSES - 1),
            )

        def key_passes(g, q):
            for t in range(KEY_TILES):
                if g == 0:
                    u_wide[(t, q)] = psum.tile([P, WIDE * SLOTS], F32, name="u_wide%d%d" % (t, q), tag=key_tags[t][q])
                key_pass(
                    u_wide[(t, q)][:],
                    t,
                    g,
                    x_codes[:, g, WIDE * q : WIDE * (q + 1), :].rearrange("p l s -> p (l s)"),
                    x_planes[:, g, WIDE * q : WIDE * (q + 1), :].rearrange("p l s -> p (l s)"),
                )

        def value_pass(g, pos):
            kind = kinds[pos]
            nc.tensor.matmul_mx(
                out=v_kind[kind][:],
                lhsT=x_codes[:, g, pos, :].bitcast(FP8X4),
                lhsT_scale=x_planes[:, g, pos, :],
                rhs=wv_codes[:, g, :].bitcast(FP4X4),
                rhs_scale=wv_planes[:, g, :],
                start=(g == 0 and pos == kinds.index(kind)),
                stop=(g == PASSES - 1 and (pos + 1 == n_layers or kinds[pos + 1] != kind)),
            )

        def norm_relu(out, in_, t):
            nc.scalar.activation(
                out=out, in_=in_, func=ACT.Relu, bias=shift_9th[:, t : t + 1], scale=scale_9th[:, t : t + 1]
            )

        def relu_wide(q):
            for t in range(KEY_TILES):
                norm_relu(
                    relu[:, WIDE * q : WIDE * (q + 1), t, :].rearrange("c l (w m) -> c l w m", m=CELL_ROWS),
                    u_wide[(t, q)][:].rearrange("c (l m w) -> c l w m", l=WIDE, m=CELL_ROWS),
                    t,
                )

        def quantise(g, first, last):
            nc.vector.quantize_mx(
                out=x_codes[:, g, first:last, :].rearrange("p l s -> p (l s)").bitcast(FP8X4),
                scales=x_planes[:, g, first:last, :].rearrange("p l s -> p (l s)"),
                in_=grouped[(g, first)][:].rearrange("p l s j -> p (l s j)"),
            )

        regroup_round(*rounds[0])
        def regroup_second(i, on_scalar, on_vector):
            if i < len(rounds):
                for b in range(B):
                    regroup_layers(1, b, *rounds[i][1:], on_scalar=on_scalar, on_vector=on_vector)

        for i, (g, first, last) in enumerate(rounds):
            closing = last == n_layers
            if g == 0 and not closing:
                regroup_layers(0, 1, *rounds[i + 1][1:])
            else:
                if g == 0:
                    regroup_second(i + 1, False, True)
                regroup_second(i + 1, True, False)
                regroup_second(i + 2 if g == 0 else i + 3, False, True)
            if (g, last) == (0, 6):
                nc.tensor.matmul(out=bias_ps[:], lhsT=ones[:], rhs=bias_rows[:], start=True, stop=True)
            if g == 0 and closing:
                nc.scalar.copy(out=bias_sb[:], in_=bias_ps[:])
            quantise(g, first, last)
            if g == 0 and closing:
                regroup_second(i + 3, False, True)
            if g == PASSES - 1 and last % WIDE == 0:
                key_passes(g, last // WIDE - 1)
            for pos in range(first, last):
                if g == 0 or kinds[pos] < 2:
                    value_pass(g, pos)
            if g == 0 and closing:
                for q in range(2):
                    key_passes(g, q)
            if g == PASSES - 1 and first == 4:
                relu_wide(0)

        u_last = psum.tile([P, KEY_TILES, SLOTS], F32, tag="key_a")
        for t in range(KEY_TILES):
            for g in range(PASSES):
                key_pass(u_last[:, t, :], t, g, x_codes[:, g, n_layers - 1, :], x_planes[:, g, n_layers - 1, :])

        def relu_last():
            relu_wide(1)
            for t in range(KEY_TILES):
                norm_relu(
                    k_sums[:, 4, t, :].rearrange("c (w m) -> c w m", m=CELL_ROWS),
                    u_last[:, t, :].rearrange("c (m w) -> c w m", m=CELL_ROWS),
                    t,
                )

        for pos in range(n_layers):
            if kinds[pos] >= 2:
                value_pass(PASSES - 1, pos)

        partial = [keep.tile([P, CV], F32, name="partial%d" % kind) for kind in range(KINDS)]
        v_coarse = keep.tile([P, CV], F32)
        key_sb = keep.tile([P, KEY_TILES, B, COARSE + FINE], F32)

        def add_kind(kind):
            nc.vector.scalar_tensor_tensor(
                out=partial[kind][:],
                in0=v_kind[kind][:],
                scalar=1.0 / 9.0,
                in1=(partial[kind - 1][:] if kind else bias_sb[:]),
                op0=ALU.mult,
                op1=ALU.add,
            )

        def key_fine(t):
            by_cell = [k_three[:, kh, t].rearrange("c (w b r) -> c b r w", b=B, r=8) for kh in range(2)]
            add(nc, key_sb[:, t, :, COARSE : COARSE + FINE].rearrange("c b (r w) -> c b r w", r=8), *by_cell)

        pairs = relu[:].rearrange("c (i two) t s -> c i two t s", two=2)
        k_three = work.tile([P, 2, KEY_TILES, SLOTS], F32)
        k_four = work.tile([P, 2, KEY_TILES, 6, CELL_ROWS], F32)
        k_three_h = work.tile([P, KEY_TILES, 6, CELL_ROWS], F32)
        k_s6 = work.tile([P, 3, KEY_TILES, B, 2, 6], F32)
        k_pairs = work.tile([P, 3, KEY_TILES, B, 2, 3], F32)

        add_kind(0)
        nc.scalar.copy(out=g_sb[0][:], in_=v_kind[0][:])
        relu_last()
        add(nc, k_sums[:, 0:2], pairs[:, 0:2, 0], pairs[:, 0:2, 1])
        add_kind(1)
        add(nc, k_sums[:, 1], k_sums[:, 0], k_sums[:, 1])
        add_kind(2)
        add(nc, k_sums[:, 2:4], pairs[:, 2:4, 0], pairs[:, 2:4, 1])
        add_kind(3)
        for kind in range(1, KINDS):
            nc.scalar.copy(out=g_sb[kind][:], in_=v_kind[kind][:])

        coarse_ps = [psum.tile([P, CV // 2], F32, name="coarse_ps%d" % h, tag=("key_b", "v_kind0")[h]) for h in range(2)]
        column_halves = [slice(CV // 2 * h, CV // 2 * (h + 1)) for h in range(2)]
        for out, half in zip(coarse_ps, column_halves):
            nc.tensor.matmul(out=out[:], lhsT=ones[:], rhs=bias_rows[:, half], start=True, stop=False)
        for kind in range(KINDS):
            for out, half in zip(coarse_ps, column_halves):
                nc.tensor.matmul(
                    out=out[:],
                    lhsT=pool_mat[:, kind].rearrange("p b l -> p (b l)"),
                    rhs=g_sb[kind][:, half],
                    start=False,
                    stop=(kind == KINDS - 1),
                )

        outer_w = k_sums[:, 1:3].rearrange("c kh t (e a m) -> c (kh t e) a m", e=2, a=4)
        inner_w = k_sums[:, 3:5].rearrange("c kh t (e a m) -> c (kh t e) a m", e=2, a=4)
        three_w = k_three[:].rearrange("c kh t (e a m) -> c (kh t e) a m", e=2, a=4)
        four_w = k_four[:].rearrange("c kh t (e k) m -> c (kh t e) k m", e=2)
        add(nc, k_three[:], k_sums[:, 1:3], k_sums[:, 3:5])
        add(nc, four_w[:, :, 1], outer_w[:, :, 1], outer_w[:, :, 2])
        add(nc, four_w[:, :, 0:3:2], three_w[:, :, 0:4:3], inner_w[:, :, 1:3])
        key_fine(0)
        add(nc, k_three_h[:], k_four[:, 0], k_four[:, 1])
        outer_h = k_four[:, 0].rearrange("c t w (be a) -> c t be w a", a=4)
        inner_h = k_four[:, 1].rearrange("c t w (be a) -> c t be w a", a=4)
        three_h = k_three_h[:].rearrange("c t w (be a) -> c t be w a", a=4)
        s6 = k_s6[:].rearrange("c k t b e w -> c k t (b e) w")
        add(nc, s6[:, 1], outer_h[:, :, :, :, 1], outer_h[:, :, :, :, 2])
        key_fine(1)
        for half in range(2):
            add(nc, s6[:, 2 * half], three_h[:, :, :, :, 3 * half], inner_h[:, :, :, :, 1 + half])
        by_pair = k_s6[:].rearrange("c k t b e (w j) -> c (k t b e w) j", j=2)
        add(nc, k_pairs[:].rearrange("c k t b e w -> c (k t b e w)"), by_pair[:, :, 0], by_pair[:, :, 1])
        for k in range(3):
            nc.scalar.mul(
                out=key_sb[:, :, :, 10:46].rearrange("c t b (e k w) -> c (t b) e k w", e=2, k=3)[:, :, :, k],
                in_=k_s6[:, k].rearrange("c t b e w -> c (t b) e w"),
                mul=9.0 / 16.0,
            )
        k_s3 = work.tile([P, 3, KEY_TILES * B, 3], F32)
        k_s1 = work.tile([P, KEY_TILES * B, 1], F32)
        for row, ((k0, e0), (k1, e1)) in enumerate((((0, 0), (1, 0)), ((2, 0), (0, 1)), ((1, 1), (2, 1)))):
            halves = [
                k_pairs[:, k].rearrange("c t b e w -> c (t b) e w")[:, :, e] for k, e in ((k0, e0), (k1, e1))
            ]
            add(nc, k_s3[:, row], *halves)
        nc.vector.tensor_reduce(
            out=k_s1[:, :, 0],
            in_=k_pairs[:].rearrange("c k t b e w -> c (t b) k (e w)"),
            axis=AXIS.XY,
            op=ALU.add,
        )
        for b in range(B):
            nc.sync.dma_start(out=out_0[b, COARSE : COARSE + FINE, :], in_=partial[3][FINE * b : FINE * (b + 1), :])

        nc.scalar.copy(out=v_coarse[:, column_halves[0]], in_=coarse_ps[0][:])
        nc.vector.tensor_copy(out=v_coarse[:, column_halves[1]], in_=coarse_ps[1][:])
        nc.scalar.mul(
            out=key_sb[:, :, :, 1:10].rearrange("c t b (r w) -> c (t b) r w", r=3),
            in_=k_s3[:].rearrange("c r m w -> c m r w"),
            mul=9.0 / 64.0,
        )
        nc.scalar.mul(out=key_sb[:, :, :, 0:1].rearrange("c t b o -> c (t b) o"), in_=k_s1[:], mul=9.0 / 576.0)
        parts = ((0, 32), (32, COARSE))
        for first, last in parts:
            nc.sync.dma_start(out=out_0[0, first:last, :], in_=v_coarse[first:last, :])
        for t in range(KEY_TILES):
            nc.scalar.dma_start(out=out_1[:, P * t : P * (t + 1), :].rearrange("b c l -> c b l"), in_=key_sb[:, t])
        for first, last in parts:
            nc.scalar.dma_start(out=out_0[1, first:last, :], in_=v_coarse[ROWS + first : ROWS + last, :])
